import numpy as np
import ml_dtypes


def mxq(x, axis, fmt="e4m3"):
    dtype, down = {"e4m3": (ml_dtypes.float8_e4m3fn, 7), "e5m2": (ml_dtypes.float8_e5m2, 14)}[fmt]
    v = np.moveaxis(np.asarray(x, np.float32).astype(ml_dtypes.bfloat16).astype(np.float64), axis, -1)
    blocks = v.reshape(v.shape[:-1] + (-1, 32))
    amax = np.abs(blocks).max(-1, keepdims=True)
    byte = np.maximum(np.where(amax > 0, np.frexp(amax)[1] - 1 + 127, 0) - down, 1)
    scale = np.exp2(byte - 127.0)
    codes = (blocks / scale).astype(np.float32).astype(dtype).astype(np.float64)
    return np.moveaxis((codes * scale).reshape(v.shape), -1, axis)


WIDE = False


def mx_kscale(k):
    if not WIDE:
        return np.ones(k)
    levels = np.array([10, -10, 5, -5, 0])
    a = np.random.permutation(np.resize(levels, k // 512 * 4)).reshape(k // 512, 4)
    idx = np.arange(k)
    return np.exp2(a[idx // 512, idx % 128 // 32])


BF16 = ml_dtypes.bfloat16


def bf(x):
    return np.asarray(x, np.float32).astype(BF16)


def f64(x):
    return np.asarray(x).astype(np.float64)


B, T, STOCH, ACT, HID, DETER, G = 4, 64, 1024, 512, 512, 4096, 8
N = B * T
BH = DETER // G
BLK_IN = BH + 3 * HID
EPS = 1e-3


def silu(v):
    return v / (1.0 + np.exp(-v))


def ln(v, g, b):
    mu = v.mean(-1, keepdims=True)
    var = v.var(-1, keepdims=True)
    return (v - mu) / np.sqrt(var + EPS) * g + b


def setup_inputs():
    ss, sa, sd = mx_kscale(STOCH), mx_kscale(ACT), mx_kscale(DETER)
    w_hid = np.random.standard_normal((G, BLK_IN, BH)) * 0.2 / np.sqrt(BLK_IN)
    w_hid[:, :BH] = w_hid[:, :BH] / sd.reshape(G, BH)[:, :, None]
    return {
        "s": bf(np.random.standard_normal((B, T, STOCH)) * ss),
        "a": bf(np.random.standard_normal((B, T, ACT)) * sa),
        "d": bf(np.random.standard_normal((B, T, DETER)) * sd),
        "W_s": bf(np.random.standard_normal((STOCH, HID)) * 0.15 / np.sqrt(STOCH) / ss[:, None]),
        "W_a": bf(np.random.standard_normal((ACT, HID)) * 0.15 / np.sqrt(ACT) / sa[:, None]),
        "W_d": bf(np.random.standard_normal((DETER, HID)) * 0.15 / np.sqrt(DETER) / sd[:, None]),
        "ln_s_g": bf(1.0 + 0.1 * np.random.standard_normal(HID)),
        "ln_s_b": bf(0.2 * np.random.standard_normal(HID)),
        "ln_a_g": bf(1.0 + 0.1 * np.random.standard_normal(HID)),
        "ln_a_b": bf(0.2 * np.random.standard_normal(HID)),
        "ln_d_g": bf(1.0 + 0.1 * np.random.standard_normal(HID)),
        "ln_d_b": bf(0.2 * np.random.standard_normal(HID)),
        "W_hid": bf(w_hid),
        "ln_h_g": bf(1.0 + 0.1 * np.random.standard_normal(DETER)),
        "ln_h_b": bf(0.2 * np.random.standard_normal(DETER)),
    }


def reference(s, a, d, W_s, W_a, W_d, ln_s_g, ln_s_b, ln_a_g, ln_a_b, ln_d_g, ln_d_b, W_hid, ln_h_g, ln_h_b):
    sq = mxq(f64(s).reshape(N, STOCH), 1, "e4m3")
    aq = mxq(f64(a).reshape(N, ACT), 1, "e4m3")
    dq = mxq(f64(d).reshape(N, DETER), 1, "e4m3")
    s_h = silu(ln(sq @ mxq(f64(W_s), 0, "e4m3"), f64(ln_s_g), f64(ln_s_b)))
    a_h = silu(ln(aq @ mxq(f64(W_a), 0, "e4m3"), f64(ln_a_g), f64(ln_a_b)))
    d_h = silu(ln(dq @ mxq(f64(W_d), 0, "e4m3"), f64(ln_d_g), f64(ln_d_b)))
    xq = mxq(np.concatenate([s_h, a_h, d_h], axis=-1), 1, "e4m3")
    wq = mxq(f64(W_hid), 1, "e4m3")
    p = (dq.reshape(N, G, BH).transpose(1, 0, 2) @ wq[:, :BH]) + (xq @ wq[:, BH:])
    p = p.transpose(1, 0, 2).reshape(N, DETER)
    return silu(ln(p, f64(ln_h_g), f64(ln_h_b)))

@@ -1,0 +1,243 @@
+from contextlib import ExitStack
+
+import concourse.mybir as mybir
+from concourse.masks import make_identity
+
+F32 = mybir.dt.float32
+BF16 = mybir.dt.bfloat16
+U32 = mybir.dt.uint32
+U8 = mybir.dt.uint8
+FP8X4 = mybir.dt.float8_e4m3fn_x4
+ALU = mybir.AluOpType
+ACT = mybir.ActivationFunctionType
+
+P = 128
+PACK = 4
+K_PASS = P * PACK
+ROWS = 256
+RT = ROWS // P
+STOCH, ACTION, HID, DETER, G = 1024, 512, 512, 4096, 8
+BH = DETER // G
+BLK_PASSES = (BH + 3 * HID) // K_PASS
+EPS = 1e-3
+BN_DIM = 6
+
+RUN = 4
+V_RUNS = 64
+TAIL_COLS = 1024
+
+FLOPS = 2 * ROWS * ((STOCH + ACTION + DETER) * HID + G * (BH + 3 * HID) * BH)
+
+
+def tile_blockrecurrentmodel_pa_kernel(
+    tc, s, a, d, W_s, W_a, W_d, ln_s_g, ln_s_b, ln_a_g, ln_a_b, ln_d_g, ln_d_b, W_hid, ln_h_g, ln_h_b, out
+):
+    nc = tc.nc
+    with ExitStack() as ctx:
+        const = ctx.enter_context(tc.tile_pool(name="const", bufs=1))
+        keep = ctx.enter_context(tc.tile_pool(name="keep", bufs=1))
+        rows_pool = ctx.enter_context(tc.tile_pool(name="rows", bufs=1))
+        rows_grouped_pool = ctx.enter_context(tc.tile_pool(name="rows_grouped", bufs=3))
+        raw_pool = ctx.enter_context(tc.tile_pool(name="raw", bufs=4))
+        grouped_pool = ctx.enter_context(tc.tile_pool(name="grouped", bufs=6))
+        quantised_pool = ctx.enter_context(tc.tile_pool(name="quantised", bufs=8))
+        norm_pool = ctx.enter_context(tc.tile_pool(name="norm", bufs=4))
+        small = ctx.enter_context(tc.tile_pool(name="small", bufs=4))
+        psum_t = ctx.enter_context(tc.psum_pool(name="psum_t", bufs=2))
+        psum_acc = ctx.enter_context(tc.psum_pool(name="psum_acc", bufs=6))
+
+        ident = const.tile([P, P], F32)
+        make_identity(nc, ident[:])
+        minus_half = const.tile([P, RT, 1], F32)
+        nc.vector.memset(minus_half[:], -0.5)
+
+        cols_bf = const.tile([P, 6, 16], BF16)
+        for i, vec in enumerate((ln_s_g, ln_s_b, ln_a_g, ln_a_b, ln_d_g, ln_d_b)):
+            nc.scalar.dma_start(out=cols_bf[:, i, 0:PACK], in_=vec.rearrange("(q t) -> q t", t=PACK))
+        cols = const.tile([P, 6, PACK], F32)
+        nc.vector.tensor_copy(out=cols[:], in_=cols_bf[:, :, 0:PACK])
+
+        def load_rows(x, width, tag):
+            rows = rows_pool.tile([P, RT, width], BF16, name=tag, tag=tag)
+            nc.sync.dma_start(out=rows[:], in_=x.flatten_outer_dims().rearrange("(rt p) k -> p rt k", p=P))
+            return rows
+
+        def quantise_rows(rows, passes, codes, scales):
+            for c in range(passes):
+                planes = psum_t.tile([P, 2, ROWS], F32, name="planes", tag="bank")
+                for rt in range(RT):
+                    words = rows[:, rt, c * K_PASS : (c + 1) * K_PASS].bitcast(F32)
+                    words = words.rearrange("p (q u) -> p u q", u=2)
+                    for u in range(2):
+                        nc.tensor.transpose(planes[:, u, rt * P : (rt + 1) * P], words[:, u, :], ident[:])
+                rows_grouped = rows_grouped_pool.tile([P, ROWS * PACK], BF16, align_bytes=64)
+                nc.scalar.copy(
+                    out=rows_grouped[:].bitcast(F32).rearrange("p (r u) -> p r u", u=2),
+                    in_=planes[:].rearrange("p u r -> p r u"),
+                )
+                nc.vector.quantize_mx(
+                    out=codes[:, c, :].bitcast(FP8X4), scales=scales[:, c, :], in_=rows_grouped[:]
+                )
+
+        def load_weight(w_rows, passes):
+            raw = raw_pool.tile([P, passes, PACK, HID], BF16, name="raw", tag="raw")
+            nc.sync.dma_start(out=raw[:], in_=w_rows.rearrange("(c p j) n -> p c j n", p=P, j=PACK))
+            return raw
+
+        def regroup(dst_tile, src_rows, v_runs, runs):
+            dst = dst_tile.rearrange("p (c i) t -> p c t i", i=RUN)
+            src = src_rows.rearrange("p t (c i) -> p c t i", i=RUN)
+            nc.vector.tensor_copy(out=dst[:, :v_runs], in_=src[:, :v_runs])
+            if v_runs < runs:
+                nc.scalar.copy(out=dst[:, v_runs:], in_=src[:, v_runs:])
+
+        def quantise_weight(raw_pass):
+            grouped = grouped_pool.tile([P, HID, PACK], BF16, align_bytes=64)
+            regroup(grouped[:], raw_pass, V_RUNS, HID // RUN)
+            w_codes = quantised_pool.tile([P, HID], U32, align_bytes=64)
+            w_scales = quantised_pool.tile([P, HID], U8, align_bytes=64)
+            nc.vector.quantize_mx(
+                out=w_codes[:].bitcast(FP8X4), scales=w_scales[:], in_=grouped[:].rearrange("p w t -> p (w t)")
+            )
+            return w_codes, w_scales
+
+        def new_sums():
+            return [psum_acc.tile([P, HID], F32, name="sums%d" % rt, tag="sums") for rt in range(RT)]
+
+        def multiply(sums, x_codes, x_scales, c, w_codes, w_scales, start, stop):
+            for rt in range(RT):
+                r = slice(rt * P, (rt + 1) * P)
+                nc.tensor.matmul_mx(
+                    out=sums[rt][:],
+                    lhsT=x_codes[:, c, r].bitcast(FP8X4),
+                    lhsT_scale=x_scales[:, c, r],
+                    rhs=w_codes[:].bitcast(FP8X4),
+                    rhs_scale=w_scales[:],
+                    start=start,
+                    stop=stop,
+                )
+
+        def inverse_std(mean_var):
+            var_eps = small.tile([P, RT, 1], F32)
+            nc.vector.tensor_scalar(out=var_eps[:], in0=mean_var[:, :, 1:2], scalar1=EPS, scalar2=None, op0=ALU.add)
+            rstd = small.tile([P, RT, 1], F32)
+            nc.gpsimd.tensor_tensor(out=rstd[:], in0=var_eps[:], in1=minus_half[:], op=ALU.pow)
+            return rstd
+
+        def codes_and_scales(passes, name):
+            codes = keep.tile([P, passes, ROWS], U32, align_bytes=64, name=name + "_codes")
+            scales = keep.tile([P, passes, ROWS], U8, align_bytes=64, name=name + "_scales")
+            return codes, scales
+
+        x_codes, x_scales = codes_and_scales(3, "x")
+
+        def embed(rows, in_codes, in_scales, weight, passes, vec, place):
+            quantise_rows(rows, passes, in_codes, in_scales)
+            sums = new_sums()
+            chunk = min(passes, BLK_PASSES)
+            for c0 in range(0, passes, chunk):
+                raw = load_weight(weight[c0 * K_PASS : (c0 + chunk) * K_PASS, :], chunk)
+                for c in range(c0, c0 + chunk):
+                    w_codes, w_scales = quantise_weight(raw[:, c - c0])
+                    multiply(sums, in_codes, in_scales, c, w_codes, w_scales, c == 0, c == passes - 1)
+
+            stats = small.tile([P, RT, BN_DIM], F32)
+            mean_var = small.tile([P, RT, 2], F32)
+            for rt in range(RT):
+                nc.vector.bn_stats(out=stats[:, rt, :], in_=sums[rt][:])
+                nc.vector.bn_aggr(out=mean_var[:, rt, :], in_=stats[:, rt, :])
+            rstd = inverse_std(mean_var)
+            shift = small.tile([P, RT, 1], F32)
+            nc.vector.scalar_tensor_tensor(
+                out=shift[:], in0=mean_var[:, :, 0:1], scalar=-1.0, in1=rstd[:], op0=ALU.mult, op1=ALU.mult
+            )
+            z = []
+            for rt in range(RT):
+                z_rt = norm_pool.tile([P, PACK, P], F32, name="z%d" % rt, tag="z")
+                nc.scalar.activation(
+                    out=z_rt[:],
+                    in_=sums[rt][:].rearrange("r (q t) -> r t q", t=PACK),
+                    func=ACT.Identity,
+                    bias=shift[:, rt, :],
+                    scale=rstd[:, rt, :],
+                )
+                z.append(z_rt)
+
+            x_planes = norm_pool.tile([P, PACK, ROWS], BF16)
+            for half in range(2):
+                z_t = psum_t.tile([P, 2, ROWS], F32, name="z_t", tag="bank")
+                for i in range(2):
+                    for rt in range(RT):
+                        nc.tensor.transpose(z_t[:, i, rt * P : (rt + 1) * P], z[rt][:, 2 * half + i, :], ident[:])
+                for i in range(2):
+                    t = 2 * half + i
+                    nc.scalar.activation(
+                        out=x_planes[:, t, :],
+                        in_=z_t[:, i, :],
+                        func=ACT.Silu,
+                        bias=cols[:, 2 * vec + 1, t : t + 1],
+                        scale=cols[:, 2 * vec, t : t + 1],
+                    )
+            x_grouped = norm_pool.tile([P, ROWS, PACK], BF16, align_bytes=64)
+            regroup(x_grouped[:], x_planes[:], ROWS // RUN, ROWS // RUN)
+            nc.vector.quantize_mx(
+                out=x_codes[:, place, :].bitcast(FP8X4),
+                scales=x_scales[:, place, :],
+                in_=x_grouped[:].rearrange("p r t -> p (r t)"),
+            )
+
+        a_codes, a_scales = codes_and_scales(ACTION // K_PASS, "a")
+        s_codes, s_scales = codes_and_scales(STOCH // K_PASS, "s")
+        d_codes, d_scales = codes_and_scales(DETER // K_PASS, "d")
+        a_rows = load_rows(a, ACTION, "a_rows")
+        embed(a_rows, a_codes, a_scales, W_a, ACTION // K_PASS, 1, 1)
+        s_rows = load_rows(s, STOCH, "s_rows")
+        embed(s_rows, s_codes, s_scales, W_s, STOCH // K_PASS, 0, 0)
+        d_rows = load_rows(d, DETER, "d_rows")
+        embed(d_rows, d_codes, d_scales, W_d, DETER // K_PASS, 2, 2)
+
+        gain_bias = rows_pool.tile([P, 2, DETER], BF16, name="gain_bias", tag="d_rows")
+        nc.sync.dma_start(out=gain_bias[:, 0, :], in_=ln_h_g.partition_broadcast(P))
+        nc.sync.dma_start(out=gain_bias[:, 1, :], in_=ln_h_b.partition_broadcast(P))
+
+        pre = keep.tile([P, RT, DETER], F32)
+        stats = keep.tile([P, RT, G, BN_DIM], F32)
+        for g in range(G):
+            raw = load_weight(W_hid[g], BLK_PASSES)
+            sums = new_sums()
+            for c in range(BLK_PASSES):
+                w_codes, w_scales = quantise_weight(raw[:, c])
+                if c == 0:
+                    multiply(sums, d_codes, d_scales, g, w_codes, w_scales, True, False)
+                else:
+                    multiply(sums, x_codes, x_scales, c - 1, w_codes, w_scales, False, c == BLK_PASSES - 1)
+            for rt in range(RT):
+                block = pre[:, rt, g * BH : (g + 1) * BH]
+                nc.scalar.copy(out=block, in_=sums[rt][:])
+                nc.vector.bn_stats(out=stats[:, rt, g, :], in_=block)
+
+        mean_var = small.tile([P, RT, 2], F32)
+        for rt in range(RT):
+            nc.vector.bn_aggr(out=mean_var[:, rt, :], in_=stats[:, rt].rearrange("p g v -> p (g v)"))
+        rstd = inverse_std(mean_var)
+        for rt in range(RT):
+            for c0 in range(0, DETER, TAIL_COLS):
+                piece = pre[:, rt, c0 : c0 + TAIL_COLS]
+                nc.vector.scalar_tensor_tensor(
+                    out=piece,
+                    in0=piece,
+                    scalar=mean_var[:, rt, 0:1],
+                    in1=gain_bias[:, 0, c0 : c0 + TAIL_COLS],
+                    op0=ALU.subtract,
+                    op1=ALU.mult,
+                )
+                nc.vector.scalar_tensor_tensor(
+                    out=piece,
+                    in0=piece,
+                    scalar=rstd[:, rt, :],
+                    in1=gain_bias[:, 1, c0 : c0 + TAIL_COLS],
+                    op0=ALU.mult,
+                    op1=ALU.add,
+                )
+                nc.scalar.activation(out=piece, in_=piece, func=ACT.Silu)
+                nc.sync.dma_start(out=out[rt * P : (rt + 1) * P, c0 : c0 + TAIL_COLS], in_=piece)

@@ -24,6 +24,7 @@ BN_DIM = 6
 
 RUN = 4
 V_RUNS = 64
+AHEAD = 8
 TAIL_COLS = 1024
 
 FLOPS = 2 * ROWS * ((STOCH + ACTION + DETER) * HID + G * (BH + 3 * HID) * BH)
@@ -34,55 +35,69 @@ def tile_blockrecurrentmodel_pa_kernel(
 ):
     nc = tc.nc
     with ExitStack() as ctx:
+        ctx.enter_context(tc.manual_schedule())
         const = ctx.enter_context(tc.tile_pool(name="const", bufs=1))
         keep = ctx.enter_context(tc.tile_pool(name="keep", bufs=1))
-        rows_pool = ctx.enter_context(tc.tile_pool(name="rows", bufs=1))
-        rows_grouped_pool = ctx.enter_context(tc.tile_pool(name="rows_grouped", bufs=3))
-        raw_pool = ctx.enter_context(tc.tile_pool(name="raw", bufs=4))
-        grouped_pool = ctx.enter_context(tc.tile_pool(name="grouped", bufs=6))
+        raw_pool = ctx.enter_context(tc.tile_pool(name="raw", bufs=AHEAD + 1))
+        grouped_pool = ctx.enter_context(tc.tile_pool(name="grouped", bufs=3))
         quantised_pool = ctx.enter_context(tc.tile_pool(name="quantised", bufs=8))
         norm_pool = ctx.enter_context(tc.tile_pool(name="norm", bufs=4))
         small = ctx.enter_context(tc.tile_pool(name="small", bufs=4))
-        psum_t = ctx.enter_context(tc.psum_pool(name="psum_t", bufs=2))
-        psum_acc = ctx.enter_context(tc.psum_pool(name="psum_acc", bufs=6))
+        psum_t = ctx.enter_context(tc.psum_pool(name="psum_t", bufs=4))
+        psum_acc = ctx.enter_context(tc.psum_pool(name="psum_acc", bufs=4))
 
         ident = const.tile([P, P], F32)
         make_identity(nc, ident[:])
         minus_half = const.tile([P, RT, 1], F32)
         nc.vector.memset(minus_half[:], -0.5)
 
+        weight_rows = []
+        row_slices = []
+        for x, w, width in ((a, W_a, ACTION), (s, W_s, STOCH), (d, W_d, DETER)):
+            x_rows = x.flatten_outer_dims().rearrange("(rt p) k -> p rt k", p=P)
+            for c in range(width // K_PASS):
+                weight_rows.append(w[c * K_PASS : (c + 1) * K_PASS, :])
+                row_slices.append(x_rows[:, :, c * K_PASS : (c + 1) * K_PASS])
+        for g in range(G):
+            for c in range(BLK_PASSES):
+                weight_rows.append(W_hid[g, c * K_PASS : (c + 1) * K_PASS, :])
+        n_passes = len(weight_rows)
+
+        gain_bias = keep.tile([P, 2, DETER], BF16)
+        raws = {}
+        slices = {}
+
+        def load_pass(i):
+            if i < len(row_slices):
+                slices[i] = raw_pool.tile([P, RT, K_PASS], BF16, name="rows", tag="rows")
+                nc.sync.dma_start(out=slices[i][:], in_=row_slices[i])
+            if i < n_passes:
+                raws[i] = raw_pool.tile([P, PACK, HID], BF16, name="raw", tag="raw")
+                nc.sync.dma_start(out=raws[i][:], in_=weight_rows[i].rearrange("(p j) n -> p j n", j=PACK))
+            if i == n_passes:
+                nc.sync.dma_start(out=gain_bias[:, 0, :], in_=ln_h_g.partition_broadcast(P))
+                nc.sync.dma_start(out=gain_bias[:, 1, :], in_=ln_h_b.partition_broadcast(P))
+
         cols_bf = const.tile([P, 6, 16], BF16)
+        load_pass(0)
         for i, vec in enumerate((ln_s_g, ln_s_b, ln_a_g, ln_a_b, ln_d_g, ln_d_b)):
-            nc.scalar.dma_start(out=cols_bf[:, i, 0:PACK], in_=vec.rearrange("(q t) -> q t", t=PACK))
-        cols = const.tile([P, 6, PACK], F32)
-        nc.vector.tensor_copy(out=cols[:], in_=cols_bf[:, :, 0:PACK])
+            nc.sync.dma_start(out=cols_bf[:, i, 0:PACK], in_=vec.rearrange("(q t) -> q t", t=PACK))
+        for i in range(1, AHEAD):
+            load_pass(i)
 
-        def load_rows(x, width, tag):
-            rows = rows_pool.tile([P, RT, width], BF16, name=tag, tag=tag)
-            nc.sync.dma_start(out=rows[:], in_=x.flatten_outer_dims().rearrange("(rt p) k -> p rt k", p=P))
-            return rows
+        chains = []
 
-        def quantise_rows(rows, passes, codes, scales):
-            for c in range(passes):
-                planes = psum_t.tile([P, 2, ROWS], F32, name="planes", tag="bank")
-                for rt in range(RT):
-                    words = rows[:, rt, c * K_PASS : (c + 1) * K_PASS].bitcast(F32)
-                    words = words.rearrange("p (q u) -> p u q", u=2)
-                    for u in range(2):
-                        nc.tensor.transpose(planes[:, u, rt * P : (rt + 1) * P], words[:, u, :], ident[:])
-                rows_grouped = rows_grouped_pool.tile([P, ROWS * PACK], BF16, align_bytes=64)
-                nc.scalar.copy(
-                    out=rows_grouped[:].bitcast(F32).rearrange("p (r u) -> p r u", u=2),
-                    in_=planes[:].rearrange("p u r -> p r u"),
-                )
-                nc.vector.quantize_mx(
-                    out=codes[:, c, :].bitcast(FP8X4), scales=scales[:, c, :], in_=rows_grouped[:]
-                )
+        def wait_one_pass():
+            return None
 
-        def load_weight(w_rows, passes):
-            raw = raw_pool.tile([P, passes, PACK, HID], BF16, name="raw", tag="raw")
-            nc.sync.dma_start(out=raw[:], in_=w_rows.rearrange("(c p j) n -> p c j n", p=P, j=PACK))
-            return raw
+        def open_chain(steps):
+            chains.append({"steps": steps, "next": 0})
+
+        def advance_chains():
+            for chain in chains:
+                if chain["next"] < len(chain["steps"]):
+                    chain["steps"][chain["next"]]()
+                    chain["next"] = chain["next"] + 1
 
         def regroup(dst_tile, src_rows, v_runs, runs):
             dst = dst_tile.rearrange("p (c i) t -> p c t i", i=RUN)
@@ -91,31 +106,77 @@ def tile_blockrecurrentmodel_pa_kernel(
             if v_runs < runs:
                 nc.scalar.copy(out=dst[:, v_runs:], in_=src[:, v_runs:])
 
-        def quantise_weight(raw_pass):
-            grouped = grouped_pool.tile([P, HID, PACK], BF16, align_bytes=64)
-            regroup(grouped[:], raw_pass, V_RUNS, HID // RUN)
+        def transpose_rows(rows):
+            planes = psum_t.tile([P, 2, ROWS], F32, name="planes", tag="bank")
+            for rt in range(RT):
+                words = rows[:, rt, :].bitcast(F32).rearrange("p (q u) -> p u q", u=2)
+                for u in range(2):
+                    nc.tensor.transpose(planes[:, u, rt * P : (rt + 1) * P], words[:, u, :], ident[:])
+            return planes
+
+        state = {"pass": 0, "waiting": None}
+
+        def finish_waiting():
+            job = state["waiting"]
+            if job is None:
+                return
             w_codes = quantised_pool.tile([P, HID], U32, align_bytes=64)
             w_scales = quantised_pool.tile([P, HID], U8, align_bytes=64)
             nc.vector.quantize_mx(
-                out=w_codes[:].bitcast(FP8X4), scales=w_scales[:], in_=grouped[:].rearrange("p w t -> p (w t)")
+                out=w_codes[:].bitcast(FP8X4),
+                scales=w_scales[:],
+                in_=job["grouped"][:].rearrange("p w t -> p (w t)"),
             )
-            return w_codes, w_scales
-
-        def new_sums():
-            return [psum_acc.tile([P, HID], F32, name="sums%d" % rt, tag="sums") for rt in range(RT)]
-
-        def multiply(sums, x_codes, x_scales, c, w_codes, w_scales, start, stop):
+            c = job["c"]
+            if job["rows_grouped"] is not None:
+                nc.vector.quantize_mx(
+                    out=job["codes"][:, c, :].bitcast(FP8X4),
+                    scales=job["scales"][:, c, :],
+                    in_=job["rows_grouped"][:],
+                )
+            if job["start"]:
+                for rt in range(RT):
+                    job["sums"].append(psum_acc.tile([P, HID], F32, name="sums%d" % rt, tag="sums"))
             for rt in range(RT):
                 r = slice(rt * P, (rt + 1) * P)
                 nc.tensor.matmul_mx(
-                    out=sums[rt][:],
-                    lhsT=x_codes[:, c, r].bitcast(FP8X4),
-                    lhsT_scale=x_scales[:, c, r],
+                    out=job["sums"][rt][:],
+                    lhsT=job["codes"][:, c, r].bitcast(FP8X4),
+                    lhsT_scale=job["scales"][:, c, r],
                     rhs=w_codes[:].bitcast(FP8X4),
                     rhs_scale=w_scales[:],
-                    start=start,
-                    stop=stop,
+                    start=job["start"],
+                    stop=job["stop"],
                 )
+            state["waiting"] = None
+
+        def weight_pass(sums, codes, scales, c, start, stop, from_rows):
+            i = state["pass"]
+            state["pass"] = i + 1
+            load_pass(i + AHEAD)
+            grouped = grouped_pool.tile([P, HID, PACK], BF16, align_bytes=64)
+            rows_grouped = None
+            if from_rows:
+                planes = transpose_rows(slices[i])
+            regroup(grouped[:], raws[i][:], V_RUNS, HID // RUN)
+            if from_rows:
+                rows_grouped = grouped_pool.tile([P, ROWS * PACK], BF16, align_bytes=64)
+                nc.scalar.copy(
+                    out=rows_grouped[:].bitcast(F32).rearrange("p (r u) -> p r u", u=2),
+                    in_=planes[:].rearrange("p u r -> p r u"),
+                )
+            advance_chains()
+            finish_waiting()
+            state["waiting"] = {
+                "grouped": grouped,
+                "rows_grouped": rows_grouped,
+                "sums": sums,
+                "codes": codes,
+                "scales": scales,
+                "c": c,
+                "start": start,
+                "stop": stop,
+            }
 
         def inverse_std(mean_var):
             var_eps = small.tile([P, RT, 1], F32)
@@ -131,113 +192,122 @@ def tile_blockrecurrentmodel_pa_kernel(
 
         x_codes, x_scales = codes_and_scales(3, "x")
 
-        def embed(rows, in_codes, in_scales, weight, passes, vec, place):
-            quantise_rows(rows, passes, in_codes, in_scales)
-            sums = new_sums()
-            chunk = min(passes, BLK_PASSES)
-            for c0 in range(0, passes, chunk):
-                raw = load_weight(weight[c0 * K_PASS : (c0 + chunk) * K_PASS, :], chunk)
-                for c in range(c0, c0 + chunk):
-                    w_codes, w_scales = quantise_weight(raw[:, c - c0])
-                    multiply(sums, in_codes, in_scales, c, w_codes, w_scales, c == 0, c == passes - 1)
+        def embedding_norm(sums, vec, place):
+            tiles = {}
 
-            stats = small.tile([P, RT, BN_DIM], F32)
-            mean_var = small.tile([P, RT, 2], F32)
-            for rt in range(RT):
-                nc.vector.bn_stats(out=stats[:, rt, :], in_=sums[rt][:])
-                nc.vector.bn_aggr(out=mean_var[:, rt, :], in_=stats[:, rt, :])
-            rstd = inverse_std(mean_var)
-            shift = small.tile([P, RT, 1], F32)
-            nc.vector.scalar_tensor_tensor(
-                out=shift[:], in0=mean_var[:, :, 0:1], scalar=-1.0, in1=rstd[:], op0=ALU.mult, op1=ALU.mult
-            )
-            z = []
-            for rt in range(RT):
-                z_rt = norm_pool.tile([P, PACK, P], F32, name="z%d" % rt, tag="z")
-                nc.scalar.activation(
-                    out=z_rt[:],
-                    in_=sums[rt][:].rearrange("r (q t) -> r t q", t=PACK),
-                    func=ACT.Identity,
-                    bias=shift[:, rt, :],
-                    scale=rstd[:, rt, :],
+            def statistics():
+                stats = small.tile([P, RT, BN_DIM], F32)
+                tiles["mean_var"] = small.tile([P, RT, 2], F32, name="mean_var")
+                for rt in range(RT):
+                    nc.vector.bn_stats(out=stats[:, rt, :], in_=sums[rt][:])
+                    nc.vector.bn_aggr(out=tiles["mean_var"][:, rt, :], in_=stats[:, rt, :])
+                tiles["rstd"] = inverse_std(tiles["mean_var"])
+
+            def normalise():
+                shift = small.tile([P, RT, 1], F32)
+                nc.vector.scalar_tensor_tensor(
+                    out=shift[:], in0=tiles["mean_var"][:, :, 0:1], scalar=-1.0, in1=tiles["rstd"][:],
+                    op0=ALU.mult, op1=ALU.mult,
                 )
-                z.append(z_rt)
-
-            x_planes = norm_pool.tile([P, PACK, ROWS], BF16)
-            for half in range(2):
-                z_t = psum_t.tile([P, 2, ROWS], F32, name="z_t", tag="bank")
-                for i in range(2):
-                    for rt in range(RT):
-                        nc.tensor.transpose(z_t[:, i, rt * P : (rt + 1) * P], z[rt][:, 2 * half + i, :], ident[:])
-                for i in range(2):
-                    t = 2 * half + i
+                tiles["cols"] = small.tile([P, 2, PACK], F32, name="cols")
+                nc.vector.tensor_copy(out=tiles["cols"][:], in_=cols_bf[:, 2 * vec : 2 * vec + 2, 0:PACK])
+                z = []
+                for rt in range(RT):
+                    z.append(norm_pool.tile([P, PACK, P], F32, name="z%d" % rt, tag="z"))
                     nc.scalar.activation(
-                        out=x_planes[:, t, :],
-                        in_=z_t[:, i, :],
-                        func=ACT.Silu,
-                        bias=cols[:, 2 * vec + 1, t : t + 1],
-                        scale=cols[:, 2 * vec, t : t + 1],
+                        out=z[rt][:],
+                        in_=sums[rt][:].rearrange("r (q t) -> r t q", t=PACK),
+                        func=ACT.Identity,
+                        bias=shift[:, rt, :],
+                        scale=tiles["rstd"][:, rt, :],
                     )
-            x_grouped = norm_pool.tile([P, ROWS, PACK], BF16, align_bytes=64)
-            regroup(x_grouped[:], x_planes[:], ROWS // RUN, ROWS // RUN)
-            nc.vector.quantize_mx(
-                out=x_codes[:, place, :].bitcast(FP8X4),
-                scales=x_scales[:, place, :],
-                in_=x_grouped[:].rearrange("p r t -> p (r t)"),
-            )
+                tiles["z_t"] = []
+                for half in range(2):
+                    tiles["z_t"].append(psum_t.tile([P, 2, ROWS], F32, name="z_t%d" % half, tag="bank"))
+                    for i in range(2):
+                        for rt in range(RT):
+                            nc.tensor.transpose(
+                                tiles["z_t"][half][:, i, rt * P : (rt + 1) * P], z[rt][:, 2 * half + i, :], ident[:]
+                            )
 
-        a_codes, a_scales = codes_and_scales(ACTION // K_PASS, "a")
-        s_codes, s_scales = codes_and_scales(STOCH // K_PASS, "s")
+            def gate():
+                tiles["x_planes"] = norm_pool.tile([P, PACK, ROWS], BF16, name="x_planes")
+                for t in range(PACK):
+                    nc.scalar.activation(
+                        out=tiles["x_planes"][:, t, :],
+                        in_=tiles["z_t"][t // 2][:, t % 2, :],
+                        func=ACT.Silu,
+                        bias=tiles["cols"][:, 1, t : t + 1],
+                        scale=tiles["cols"][:, 0, t : t + 1],
+                    )
+
+            def quantise_x():
+                x_grouped = norm_pool.tile([P, ROWS, PACK], BF16, align_bytes=64)
+                regroup(x_grouped[:], tiles["x_planes"][:], ROWS // RUN, ROWS // RUN)
+                nc.vector.quantize_mx(
+                    out=x_codes[:, place, :].bitcast(FP8X4),
+                    scales=x_scales[:, place, :],
+                    in_=x_grouped[:].rearrange("p r t -> p (r t)"),
+                )
+
+            open_chain([wait_one_pass, statistics, normalise, gate, quantise_x])
+
         d_codes, d_scales = codes_and_scales(DETER // K_PASS, "d")
-        a_rows = load_rows(a, ACTION, "a_rows")
-        embed(a_rows, a_codes, a_scales, W_a, ACTION // K_PASS, 1, 1)
-        s_rows = load_rows(s, STOCH, "s_rows")
-        embed(s_rows, s_codes, s_scales, W_s, STOCH // K_PASS, 0, 0)
-        d_rows = load_rows(d, DETER, "d_rows")
-        embed(d_rows, d_codes, d_scales, W_d, DETER // K_PASS, 2, 2)
-
-        gain_bias = rows_pool.tile([P, 2, DETER], BF16, name="gain_bias", tag="d_rows")
-        nc.sync.dma_start(out=gain_bias[:, 0, :], in_=ln_h_g.partition_broadcast(P))
-        nc.sync.dma_start(out=gain_bias[:, 1, :], in_=ln_h_b.partition_broadcast(P))
+        for name, width, vec, place in (("a", ACTION, 1, 1), ("s", STOCH, 0, 0), ("d", DETER, 2, 2)):
+            passes = width // K_PASS
+            codes, scales = (d_codes, d_scales) if name == "d" else codes_and_scales(passes, name)
+            sums = []
+            for c in range(passes):
+                weight_pass(sums, codes, scales, c, c == 0, c == passes - 1, True)
+            embedding_norm(sums, vec, place)
 
         pre = keep.tile([P, RT, DETER], F32)
         stats = keep.tile([P, RT, G, BN_DIM], F32)
+
+        def close_block(sums, g):
+            def evacuate():
+                for rt in range(RT):
+                    nc.scalar.copy(out=pre[:, rt, g * BH : (g + 1) * BH], in_=sums[rt][:])
+
+            def statistics():
+                for rt in range(RT):
+                    nc.vector.bn_stats(out=stats[:, rt, g, :], in_=pre[:, rt, g * BH : (g + 1) * BH])
+
+            open_chain([wait_one_pass, evacuate, statistics])
+
         for g in range(G):
-            raw = load_weight(W_hid[g], BLK_PASSES)
-            sums = new_sums()
-            for c in range(BLK_PASSES):
-                w_codes, w_scales = quantise_weight(raw[:, c])
-                if c == 0:
-                    multiply(sums, d_codes, d_scales, g, w_codes, w_scales, True, False)
-                else:
-                    multiply(sums, x_codes, x_scales, c - 1, w_codes, w_scales, False, c == BLK_PASSES - 1)
-            for rt in range(RT):
-                block = pre[:, rt, g * BH : (g + 1) * BH]
-                nc.scalar.copy(out=block, in_=sums[rt][:])
-                nc.vector.bn_stats(out=stats[:, rt, g, :], in_=block)
+            sums = []
+            weight_pass(sums, d_codes, d_scales, g, True, False, False)
+            for c in range(1, BLK_PASSES):
+                weight_pass(sums, x_codes, x_scales, c - 1, False, c == BLK_PASSES - 1, False)
+            close_block(sums, g)
+        advance_chains()
+        finish_waiting()
+        advance_chains()
+        advance_chains()
 
         mean_var = small.tile([P, RT, 2], F32)
         for rt in range(RT):
             nc.vector.bn_aggr(out=mean_var[:, rt, :], in_=stats[:, rt].rearrange("p g v -> p (g v)"))
         rstd = inverse_std(mean_var)
-        for rt in range(RT):
-            for c0 in range(0, DETER, TAIL_COLS):
-                piece = pre[:, rt, c0 : c0 + TAIL_COLS]
+        pieces = [(rt, c0) for rt in range(RT) for c0 in range(0, DETER, TAIL_COLS)]
+        for k in range(len(pieces) + 1):
+            if k < len(pieces):
+                rt, c0 = pieces[k]
                 nc.vector.scalar_tensor_tensor(
-                    out=piece,
-                    in0=piece,
+                    out=pre[:, rt, c0 : c0 + TAIL_COLS],
+                    in0=pre[:, rt, c0 : c0 + TAIL_COLS],
                     scalar=mean_var[:, rt, 0:1],
                     in1=gain_bias[:, 0, c0 : c0 + TAIL_COLS],
                     op0=ALU.subtract,
                     op1=ALU.mult,
                 )
+            if k > 0:
+                rt, c0 = pieces[k - 1]
+                piece = pre[:, rt, c0 : c0 + TAIL_COLS]
                 nc.vector.scalar_tensor_tensor(
-                    out=piece,
-                    in0=piece,
-                    scalar=rstd[:, rt, :],
-                    in1=gain_bias[:, 1, c0 : c0 + TAIL_COLS],
-                    op0=ALU.mult,
-                    op1=ALU.add,
+                    out=piece, in0=piece, scalar=rstd[:, rt, :], in1=gain_bias[:, 1, c0 : c0 + TAIL_COLS],
+                    op0=ALU.mult, op1=ALU.add,
                 )
                 nc.scalar.activation(out=piece, in_=piece, func=ACT.Silu)
                 nc.sync.dma_start(out=out[rt * P : (rt + 1) * P, c0 : c0 + TAIL_COLS], in_=piece)

@@ -23,8 +23,7 @@ EPS = 1e-3
 BN_DIM = 6
 
 RUN = 4
-V_RUNS = 64
-AHEAD = 8
+UNIT = 2
 TAIL_COLS = 1024
 
 FLOPS = 2 * ROWS * ((STOCH + ACTION + DETER) * HID + G * (BH + 3 * HID) * BH)
@@ -35,12 +34,11 @@ def tile_blockrecurrentmodel_pa_kernel(
 ):
     nc = tc.nc
     with ExitStack() as ctx:
-        ctx.enter_context(tc.manual_schedule())
         const = ctx.enter_context(tc.tile_pool(name="const", bufs=1))
         keep = ctx.enter_context(tc.tile_pool(name="keep", bufs=1))
-        raw_pool = ctx.enter_context(tc.tile_pool(name="raw", bufs=AHEAD + 1))
+        raw_pool = ctx.enter_context(tc.tile_pool(name="raw", bufs=5))
         grouped_pool = ctx.enter_context(tc.tile_pool(name="grouped", bufs=3))
-        quantised_pool = ctx.enter_context(tc.tile_pool(name="quantised", bufs=8))
+        quantised_pool = ctx.enter_context(tc.tile_pool(name="quantised", bufs=5))
         norm_pool = ctx.enter_context(tc.tile_pool(name="norm", bufs=4))
         small = ctx.enter_context(tc.tile_pool(name="small", bufs=4))
         psum_t = ctx.enter_context(tc.psum_pool(name="psum_t", bufs=4))
@@ -51,132 +49,73 @@ def tile_blockrecurrentmodel_pa_kernel(
         minus_half = const.tile([P, RT, 1], F32)
         nc.vector.memset(minus_half[:], -0.5)
 
-        weight_rows = []
-        row_slices = []
-        for x, w, width in ((a, W_a, ACTION), (s, W_s, STOCH), (d, W_d, DETER)):
-            x_rows = x.flatten_outer_dims().rearrange("(rt p) k -> p rt k", p=P)
-            for c in range(width // K_PASS):
-                weight_rows.append(w[c * K_PASS : (c + 1) * K_PASS, :])
-                row_slices.append(x_rows[:, :, c * K_PASS : (c + 1) * K_PASS])
-        for g in range(G):
-            for c in range(BLK_PASSES):
-                weight_rows.append(W_hid[g, c * K_PASS : (c + 1) * K_PASS, :])
-        n_passes = len(weight_rows)
-
-        gain_bias = keep.tile([P, 2, DETER], BF16)
-        raws = {}
-        slices = {}
-
-        def load_pass(i):
-            if i < len(row_slices):
-                slices[i] = raw_pool.tile([P, RT, K_PASS], BF16, name="rows", tag="rows")
-                nc.sync.dma_start(out=slices[i][:], in_=row_slices[i])
-            if i < n_passes:
-                raws[i] = raw_pool.tile([P, PACK, HID], BF16, name="raw", tag="raw")
-                nc.sync.dma_start(out=raws[i][:], in_=weight_rows[i].rearrange("(p j) n -> p j n", j=PACK))
-            if i == n_passes:
-                nc.sync.dma_start(out=gain_bias[:, 0, :], in_=ln_h_g.partition_broadcast(P))
-                nc.sync.dma_start(out=gain_bias[:, 1, :], in_=ln_h_b.partition_broadcast(P))
-
         cols_bf = const.tile([P, 6, 16], BF16)
-        load_pass(0)
         for i, vec in enumerate((ln_s_g, ln_s_b, ln_a_g, ln_a_b, ln_d_g, ln_d_b)):
-            nc.sync.dma_start(out=cols_bf[:, i, 0:PACK], in_=vec.rearrange("(q t) -> q t", t=PACK))
-        for i in range(1, AHEAD):
-            load_pass(i)
+            nc.scalar.dma_start(out=cols_bf[:, i, 0:PACK], in_=vec.rearrange("(q t) -> q t", t=PACK))
+        cols = const.tile([P, 6, PACK], F32)
+        nc.vector.tensor_copy(out=cols[:], in_=cols_bf[:, :, 0:PACK])
 
-        chains = []
+        def regrouped(dst, src):
+            return dst.rearrange("p (c i) t -> p c t i", i=RUN), src.rearrange("p t (c i) -> p c t i", i=RUN)
 
-        def wait_one_pass():
-            return None
-
-        def open_chain(steps):
-            chains.append({"steps": steps, "next": 0})
-
-        def advance_chains():
-            for chain in chains:
-                if chain["next"] < len(chain["steps"]):
-                    chain["steps"][chain["next"]]()
-                    chain["next"] = chain["next"] + 1
-
-        def regroup(dst_tile, src_rows, v_runs, runs):
-            dst = dst_tile.rearrange("p (c i) t -> p c t i", i=RUN)
-            src = src_rows.rearrange("p t (c i) -> p c t i", i=RUN)
-            nc.vector.tensor_copy(out=dst[:, :v_runs], in_=src[:, :v_runs])
-            if v_runs < runs:
-                nc.scalar.copy(out=dst[:, v_runs:], in_=src[:, v_runs:])
-
-        def transpose_rows(rows):
-            planes = psum_t.tile([P, 2, ROWS], F32, name="planes", tag="bank")
-            for rt in range(RT):
-                words = rows[:, rt, :].bitcast(F32).rearrange("p (q u) -> p u q", u=2)
-                for u in range(2):
-                    nc.tensor.transpose(planes[:, u, rt * P : (rt + 1) * P], words[:, u, :], ident[:])
-            return planes
-
-        state = {"pass": 0, "waiting": None}
-
-        def finish_waiting():
-            job = state["waiting"]
-            if job is None:
-                return
-            w_codes = quantised_pool.tile([P, HID], U32, align_bytes=64)
-            w_scales = quantised_pool.tile([P, HID], U8, align_bytes=64)
+        def quantise_weight(w_rows):
+            passes = w_rows.shape[0] // K_PASS
+            raw = raw_pool.tile([P, passes, PACK, HID], BF16, name="raw", tag="raw")
+            nc.sync.dma_start(out=raw[:], in_=w_rows.rearrange("(c p j) n -> p c j n", p=P, j=PACK))
+            grouped = grouped_pool.tile([P, passes * HID, PACK], BF16, align_bytes=64)
+            if passes == UNIT:
+                first, second = (grouped[:, :HID], raw[:, 0]), (grouped[:, HID:], raw[:, 1])
+            else:
+                half = HID // 2
+                first, second = (grouped[:, :half], raw[:, 0, :, :half]), (grouped[:, half:], raw[:, 0, :, half:])
+            dst, src = regrouped(first[0], first[1])
+            nc.vector.tensor_copy(out=dst, in_=src)
+            dst, src = regrouped(second[0], second[1])
+            nc.scalar.copy(out=dst, in_=src)
+            w_codes = quantised_pool.tile([P, passes, HID], U32, align_bytes=64)
+            w_scales = quantised_pool.tile([P, passes, HID], U8, align_bytes=64)
             nc.vector.quantize_mx(
-                out=w_codes[:].bitcast(FP8X4),
-                scales=w_scales[:],
-                in_=job["grouped"][:].rearrange("p w t -> p (w t)"),
+                out=w_codes[:].rearrange("p c w -> p (c w)").bitcast(FP8X4),
+                scales=w_scales[:].rearrange("p c w -> p (c w)"),
+                in_=grouped[:].rearrange("p w t -> p (w t)"),
             )
-            c = job["c"]
-            if job["rows_grouped"] is not None:
-                nc.vector.quantize_mx(
-                    out=job["codes"][:, c, :].bitcast(FP8X4),
-                    scales=job["scales"][:, c, :],
-                    in_=job["rows_grouped"][:],
-                )
-            if job["start"]:
+            return w_codes, w_scales
+
+        def quantise_rows(x_rows, codes, scales):
+            passes = x_rows.shape[2] // K_PASS
+            rows = raw_pool.tile([P, RT, passes * K_PASS], BF16, name="rows", tag="rows")
+            nc.sync.dma_start(out=rows[:], in_=x_rows)
+            rows_grouped = grouped_pool.tile([P, passes * ROWS * PACK], BF16, align_bytes=64)
+            pairs = rows_grouped[:].bitcast(F32).rearrange("p (c r u) -> p c r u", c=passes, u=2)
+            for c in range(passes):
+                planes = psum_t.tile([P, 2, ROWS], F32, name="planes", tag="bank")
                 for rt in range(RT):
-                    job["sums"].append(psum_acc.tile([P, HID], F32, name="sums%d" % rt, tag="sums"))
+                    words = rows[:, rt, c * K_PASS : (c + 1) * K_PASS].bitcast(F32)
+                    words = words.rearrange("p (q u) -> p u q", u=2)
+                    for u in range(2):
+                        nc.tensor.transpose(planes[:, u, rt * P : (rt + 1) * P], words[:, u, :], ident[:])
+                nc.scalar.copy(out=pairs[:, c], in_=planes[:].rearrange("p u r -> p r u"))
+            nc.vector.quantize_mx(
+                out=codes.rearrange("p c r -> p (c r)").bitcast(FP8X4),
+                scales=scales.rearrange("p c r -> p (c r)"),
+                in_=rows_grouped[:],
+            )
+
+        def new_sums():
+            return [psum_acc.tile([P, HID], F32, name="sums%d" % rt, tag="sums") for rt in range(RT)]
+
+        def multiply(sums, x_codes, x_scales, c, w_codes, w_scales, n, start, stop):
             for rt in range(RT):
                 r = slice(rt * P, (rt + 1) * P)
                 nc.tensor.matmul_mx(
-                    out=job["sums"][rt][:],
-                    lhsT=job["codes"][:, c, r].bitcast(FP8X4),
-                    lhsT_scale=job["scales"][:, c, r],
-                    rhs=w_codes[:].bitcast(FP8X4),
-                    rhs_scale=w_scales[:],
-                    start=job["start"],
-                    stop=job["stop"],
+                    out=sums[rt][:],
+                    lhsT=x_codes[:, c, r].bitcast(FP8X4),
+                    lhsT_scale=x_scales[:, c, r],
+                    rhs=w_codes[:, n, :].bitcast(FP8X4),
+                    rhs_scale=w_scales[:, n, :],
+                    start=start,
+                    stop=stop,
                 )
-            state["waiting"] = None
-
-        def weight_pass(sums, codes, scales, c, start, stop, from_rows):
-            i = state["pass"]
-            state["pass"] = i + 1
-            load_pass(i + AHEAD)
-            grouped = grouped_pool.tile([P, HID, PACK], BF16, align_bytes=64)
-            rows_grouped = None
-            if from_rows:
-                planes = transpose_rows(slices[i])
-            regroup(grouped[:], raws[i][:], V_RUNS, HID // RUN)
-            if from_rows:
-                rows_grouped = grouped_pool.tile([P, ROWS * PACK], BF16, align_bytes=64)
-                nc.scalar.copy(
-                    out=rows_grouped[:].bitcast(F32).rearrange("p (r u) -> p r u", u=2),
-                    in_=planes[:].rearrange("p u r -> p r u"),
-                )
-            advance_chains()
-            finish_waiting()
-            state["waiting"] = {
-                "grouped": grouped,
-                "rows_grouped": rows_grouped,
-                "sums": sums,
-                "codes": codes,
-                "scales": scales,
-                "c": c,
-                "start": start,
-                "stop": stop,
-            }
 
         def inverse_std(mean_var):
             var_eps = small.tile([P, RT, 1], F32)
@@ -192,119 +131,103 @@ def tile_blockrecurrentmodel_pa_kernel(
 
         x_codes, x_scales = codes_and_scales(3, "x")
 
-        def embedding_norm(sums, vec, place):
-            tiles = {}
+        def embed(x, weight, in_codes, in_scales, vec, place):
+            x_rows = x.flatten_outer_dims().rearrange("(rt p) k -> p rt k", p=P)
+            passes = weight.shape[0] // K_PASS
+            unit = min(passes, UNIT)
+            sums = new_sums()
+            for c0 in range(0, passes, unit):
+                k = slice(c0 * K_PASS, (c0 + unit) * K_PASS)
+                w_codes, w_scales = quantise_weight(weight[k, :])
+                quantise_rows(x_rows[:, :, k], in_codes[:, c0 : c0 + unit, :], in_scales[:, c0 : c0 + unit, :])
+                for n in range(unit):
+                    c = c0 + n
+                    multiply(sums, in_codes, in_scales, c, w_codes, w_scales, n, c == 0, c == passes - 1)
 
-            def statistics():
-                stats = small.tile([P, RT, BN_DIM], F32)
-                tiles["mean_var"] = small.tile([P, RT, 2], F32, name="mean_var")
-                for rt in range(RT):
-                    nc.vector.bn_stats(out=stats[:, rt, :], in_=sums[rt][:])
-                    nc.vector.bn_aggr(out=tiles["mean_var"][:, rt, :], in_=stats[:, rt, :])
-                tiles["rstd"] = inverse_std(tiles["mean_var"])
-
-            def normalise():
-                shift = small.tile([P, RT, 1], F32)
-                nc.vector.scalar_tensor_tensor(
-                    out=shift[:], in0=tiles["mean_var"][:, :, 0:1], scalar=-1.0, in1=tiles["rstd"][:],
-                    op0=ALU.mult, op1=ALU.mult,
+            stats = small.tile([P, RT, BN_DIM], F32)
+            mean_var = small.tile([P, RT, 2], F32)
+            for rt in range(RT):
+                nc.vector.bn_stats(out=stats[:, rt, :], in_=sums[rt][:])
+                nc.vector.bn_aggr(out=mean_var[:, rt, :], in_=stats[:, rt, :])
+            rstd = inverse_std(mean_var)
+            shift = small.tile([P, RT, 1], F32)
+            nc.vector.scalar_tensor_tensor(
+                out=shift[:], in0=mean_var[:, :, 0:1], scalar=-1.0, in1=rstd[:], op0=ALU.mult, op1=ALU.mult
+            )
+            z = []
+            for rt in range(RT):
+                z.append(norm_pool.tile([P, PACK, P], F32, name="z%d" % rt, tag="z"))
+                nc.scalar.activation(
+                    out=z[rt][:],
+                    in_=sums[rt][:].rearrange("r (q t) -> r t q", t=PACK),
+                    func=ACT.Identity,
+                    bias=shift[:, rt, :],
+                    scale=rstd[:, rt, :],
                 )
-                tiles["cols"] = small.tile([P, 2, PACK], F32, name="cols")
-                nc.vector.tensor_copy(out=tiles["cols"][:], in_=cols_bf[:, 2 * vec : 2 * vec + 2, 0:PACK])
-                z = []
-                for rt in range(RT):
-                    z.append(norm_pool.tile([P, PACK, P], F32, name="z%d" % rt, tag="z"))
-                    nc.scalar.activation(
-                        out=z[rt][:],
-                        in_=sums[rt][:].rearrange("r (q t) -> r t q", t=PACK),
-                        func=ACT.Identity,
-                        bias=shift[:, rt, :],
-                        scale=tiles["rstd"][:, rt, :],
-                    )
-                tiles["z_t"] = []
-                for half in range(2):
-                    tiles["z_t"].append(psum_t.tile([P, 2, ROWS], F32, name="z_t%d" % half, tag="bank"))
-                    for i in range(2):
-                        for rt in range(RT):
-                            nc.tensor.transpose(
-                                tiles["z_t"][half][:, i, rt * P : (rt + 1) * P], z[rt][:, 2 * half + i, :], ident[:]
-                            )
 
-            def gate():
-                tiles["x_planes"] = norm_pool.tile([P, PACK, ROWS], BF16, name="x_planes")
-                for t in range(PACK):
+            x_planes = norm_pool.tile([P, PACK, ROWS], BF16)
+            for half in range(2):
+                z_t = psum_t.tile([P, 2, ROWS], F32, name="z_t", tag="bank")
+                for i in range(2):
+                    for rt in range(RT):
+                        nc.tensor.transpose(z_t[:, i, rt * P : (rt + 1) * P], z[rt][:, 2 * half + i, :], ident[:])
+                for i in range(2):
+                    t = 2 * half + i
                     nc.scalar.activation(
-                        out=tiles["x_planes"][:, t, :],
-                        in_=tiles["z_t"][t // 2][:, t % 2, :],
+                        out=x_planes[:, t, :],
+                        in_=z_t[:, i, :],
                         func=ACT.Silu,
-                        bias=tiles["cols"][:, 1, t : t + 1],
-                        scale=tiles["cols"][:, 0, t : t + 1],
+                        bias=cols[:, 2 * vec + 1, t : t + 1],
+                        scale=cols[:, 2 * vec, t : t + 1],
                     )
+            x_grouped = norm_pool.tile([P, ROWS, PACK], BF16, align_bytes=64)
+            dst, src = regrouped(x_grouped[:], x_planes[:])
+            nc.vector.tensor_copy(out=dst, in_=src)
+            nc.vector.quantize_mx(
+                out=x_codes[:, place, :].bitcast(FP8X4),
+                scales=x_scales[:, place, :],
+                in_=x_grouped[:].rearrange("p r t -> p (r t)"),
+            )
 
-            def quantise_x():
-                x_grouped = norm_pool.tile([P, ROWS, PACK], BF16, align_bytes=64)
-                regroup(x_grouped[:], tiles["x_planes"][:], ROWS // RUN, ROWS // RUN)
-                nc.vector.quantize_mx(
-                    out=x_codes[:, place, :].bitcast(FP8X4),
-                    scales=x_scales[:, place, :],
-                    in_=x_grouped[:].rearrange("p r t -> p (r t)"),
-                )
-
-            open_chain([wait_one_pass, statistics, normalise, gate, quantise_x])
-
+        a_codes, a_scales = codes_and_scales(ACTION // K_PASS, "a")
+        s_codes, s_scales = codes_and_scales(STOCH // K_PASS, "s")
         d_codes, d_scales = codes_and_scales(DETER // K_PASS, "d")
-        for name, width, vec, place in (("a", ACTION, 1, 1), ("s", STOCH, 0, 0), ("d", DETER, 2, 2)):
-            passes = width // K_PASS
-            codes, scales = (d_codes, d_scales) if name == "d" else codes_and_scales(passes, name)
-            sums = []
-            for c in range(passes):
-                weight_pass(sums, codes, scales, c, c == 0, c == passes - 1, True)
-            embedding_norm(sums, vec, place)
+        embed(a, W_a, a_codes, a_scales, 1, 1)
+        embed(s, W_s, s_codes, s_scales, 0, 0)
+        embed(d, W_d, d_codes, d_scales, 2, 2)
 
         pre = keep.tile([P, RT, DETER], F32)
         stats = keep.tile([P, RT, G, BN_DIM], F32)
-
-        def close_block(sums, g):
-            def evacuate():
-                for rt in range(RT):
-                    nc.scalar.copy(out=pre[:, rt, g * BH : (g + 1) * BH], in_=sums[rt][:])
-
-            def statistics():
-                for rt in range(RT):
-                    nc.vector.bn_stats(out=stats[:, rt, g, :], in_=pre[:, rt, g * BH : (g + 1) * BH])
-
-            open_chain([wait_one_pass, evacuate, statistics])
-
         for g in range(G):
-            sums = []
-            weight_pass(sums, d_codes, d_scales, g, True, False, False)
-            for c in range(1, BLK_PASSES):
-                weight_pass(sums, x_codes, x_scales, c - 1, False, c == BLK_PASSES - 1, False)
-            close_block(sums, g)
-        advance_chains()
-        finish_waiting()
-        advance_chains()
-        advance_chains()
+            sums = new_sums()
+            for c0 in range(0, BLK_PASSES, UNIT):
+                w_codes, w_scales = quantise_weight(W_hid[g, c0 * K_PASS : (c0 + UNIT) * K_PASS, :])
+                for n in range(UNIT):
+                    c = c0 + n
+                    if c == 0:
+                        multiply(sums, d_codes, d_scales, g, w_codes, w_scales, n, True, False)
+                    else:
+                        multiply(sums, x_codes, x_scales, c - 1, w_codes, w_scales, n, False, c == BLK_PASSES - 1)
+            for rt in range(RT):
+                block = pre[:, rt, g * BH : (g + 1) * BH]
+                nc.scalar.copy(out=block, in_=sums[rt][:])
+                nc.vector.bn_stats(out=stats[:, rt, g, :], in_=block)
+
+        gain_bias = keep.tile([P, 2, DETER], BF16)
+        nc.sync.dma_start(out=gain_bias[:, 0, :], in_=ln_h_g.partition_broadcast(P))
+        nc.sync.dma_start(out=gain_bias[:, 1, :], in_=ln_h_b.partition_broadcast(P))
 
         mean_var = small.tile([P, RT, 2], F32)
         for rt in range(RT):
             nc.vector.bn_aggr(out=mean_var[:, rt, :], in_=stats[:, rt].rearrange("p g v -> p (g v)"))
         rstd = inverse_std(mean_var)
-        pieces = [(rt, c0) for rt in range(RT) for c0 in range(0, DETER, TAIL_COLS)]
-        for k in range(len(pieces) + 1):
-            if k < len(pieces):
-                rt, c0 = pieces[k]
-                nc.vector.scalar_tensor_tensor(
-                    out=pre[:, rt, c0 : c0 + TAIL_COLS],
-                    in0=pre[:, rt, c0 : c0 + TAIL_COLS],
-                    scalar=mean_var[:, rt, 0:1],
-                    in1=gain_bias[:, 0, c0 : c0 + TAIL_COLS],
-                    op0=ALU.subtract,
-                    op1=ALU.mult,
-                )
-            if k > 0:
-                rt, c0 = pieces[k - 1]
+        for rt in range(RT):
+            for c0 in range(0, DETER, TAIL_COLS):
                 piece = pre[:, rt, c0 : c0 + TAIL_COLS]
+                nc.vector.scalar_tensor_tensor(
+                    out=piece, in0=piece, scalar=mean_var[:, rt, 0:1], in1=gain_bias[:, 0, c0 : c0 + TAIL_COLS],
+                    op0=ALU.subtract, op1=ALU.mult,
+                )
                 nc.vector.scalar_tensor_tensor(
                     out=piece, in0=piece, scalar=rstd[:, rt, :], in1=gain_bias[:, 1, c0 : c0 + TAIL_COLS],
                     op0=ALU.mult, op1=ALU.add,

@@ -24,7 +24,8 @@ BN_DIM = 6
 
 RUN = 4
 UNIT = 2
-TAIL_COLS = 1024
+KEPT = 3
+AHEAD = 4
 
 FLOPS = 2 * ROWS * ((STOCH + ACTION + DETER) * HID + G * (BH + 3 * HID) * BH)
 
@@ -36,86 +37,147 @@ def tile_blockrecurrentmodel_pa_kernel(
     with ExitStack() as ctx:
         const = ctx.enter_context(tc.tile_pool(name="const", bufs=1))
         keep = ctx.enter_context(tc.tile_pool(name="keep", bufs=1))
-        raw_pool = ctx.enter_context(tc.tile_pool(name="raw", bufs=5))
+        raw_pool = ctx.enter_context(tc.tile_pool(name="raw", bufs=AHEAD + 1))
         grouped_pool = ctx.enter_context(tc.tile_pool(name="grouped", bufs=3))
         quantised_pool = ctx.enter_context(tc.tile_pool(name="quantised", bufs=5))
         norm_pool = ctx.enter_context(tc.tile_pool(name="norm", bufs=4))
         small = ctx.enter_context(tc.tile_pool(name="small", bufs=4))
-        psum_t = ctx.enter_context(tc.psum_pool(name="psum_t", bufs=4))
-        psum_acc = ctx.enter_context(tc.psum_pool(name="psum_acc", bufs=4))
+        psum = ctx.enter_context(tc.psum_pool(name="psum", bufs=8))
 
         ident = const.tile([P, P], F32)
         make_identity(nc, ident[:])
         minus_half = const.tile([P, RT, 1], F32)
         nc.vector.memset(minus_half[:], -0.5)
 
+        weight_rows = []
+        row_slices = []
+        for x, w, width in ((a, W_a, ACTION), (s, W_s, STOCH), (d, W_d, DETER)):
+            x_rows = x.flatten_outer_dims().rearrange("(rt p) k -> p rt k", p=P)
+            step = min(width, UNIT * K_PASS)
+            for k0 in range(0, width, step):
+                weight_rows.append(w[k0 : k0 + step, :])
+                row_slices.append(x_rows[:, :, k0 : k0 + step])
+        for g in range(G):
+            for k0 in range(0, BLK_PASSES * K_PASS, UNIT * K_PASS):
+                weight_rows.append(W_hid[g, k0 : k0 + UNIT * K_PASS, :])
+        n_units = len(weight_rows)
+
+        gain_bias = keep.tile([P, 2, DETER], BF16)
+        raws = {}
+        slices = {}
+
+        def load_unit(i):
+            if i < len(row_slices):
+                slices[i] = raw_pool.tile([P, RT, row_slices[i].shape[2]], BF16, name="rows", tag="rows")
+                nc.sync.dma_start(out=slices[i][:], in_=row_slices[i])
+            if i < n_units:
+                raws[i] = raw_pool.tile([P, weight_rows[i].shape[0] // K_PASS, PACK, HID], BF16, name="raw", tag="raw")
+                nc.sync.dma_start(out=raws[i][:], in_=weight_rows[i].rearrange("(c p j) n -> p c j n", p=P, j=PACK))
+            if i == n_units:
+                nc.sync.dma_start(out=gain_bias[:, 0, :], in_=ln_h_g.partition_broadcast(P))
+                nc.sync.dma_start(out=gain_bias[:, 1, :], in_=ln_h_b.partition_broadcast(P))
+
         cols_bf = const.tile([P, 6, 16], BF16)
+        load_unit(0)
         for i, vec in enumerate((ln_s_g, ln_s_b, ln_a_g, ln_a_b, ln_d_g, ln_d_b)):
-            nc.scalar.dma_start(out=cols_bf[:, i, 0:PACK], in_=vec.rearrange("(q t) -> q t", t=PACK))
-        cols = const.tile([P, 6, PACK], F32)
-        nc.vector.tensor_copy(out=cols[:], in_=cols_bf[:, :, 0:PACK])
+            nc.sync.dma_start(out=cols_bf[:, i, 0:PACK], in_=vec.rearrange("(q t) -> q t", t=PACK))
+        for i in range(1, AHEAD):
+            load_unit(i)
+
+        chains = []
+
+        def wait_a_step():
+            return None
+
+        def open_chain(steps):
+            chains.append({"steps": steps, "next": 0})
+
+        def advance_chains():
+            for chain in chains:
+                if chain["next"] < len(chain["steps"]):
+                    chain["steps"][chain["next"]]()
+                    chain["next"] = chain["next"] + 1
 
         def regrouped(dst, src):
             return dst.rearrange("p (c i) t -> p c t i", i=RUN), src.rearrange("p t (c i) -> p c t i", i=RUN)
 
-        def quantise_weight(w_rows):
-            passes = w_rows.shape[0] // K_PASS
-            raw = raw_pool.tile([P, passes, PACK, HID], BF16, name="raw", tag="raw")
-            nc.sync.dma_start(out=raw[:], in_=w_rows.rearrange("(c p j) n -> p c j n", p=P, j=PACK))
-            grouped = grouped_pool.tile([P, passes * HID, PACK], BF16, align_bytes=64)
-            if passes == UNIT:
-                first, second = (grouped[:, :HID], raw[:, 0]), (grouped[:, HID:], raw[:, 1])
-            else:
-                half = HID // 2
-                first, second = (grouped[:, :half], raw[:, 0, :, :half]), (grouped[:, half:], raw[:, 0, :, half:])
-            dst, src = regrouped(first[0], first[1])
-            nc.vector.tensor_copy(out=dst, in_=src)
-            dst, src = regrouped(second[0], second[1])
-            nc.scalar.copy(out=dst, in_=src)
-            w_codes = quantised_pool.tile([P, passes, HID], U32, align_bytes=64)
-            w_scales = quantised_pool.tile([P, passes, HID], U8, align_bytes=64)
-            nc.vector.quantize_mx(
-                out=w_codes[:].rearrange("p c w -> p (c w)").bitcast(FP8X4),
-                scales=w_scales[:].rearrange("p c w -> p (c w)"),
-                in_=grouped[:].rearrange("p w t -> p (w t)"),
-            )
-            return w_codes, w_scales
-
-        def quantise_rows(x_rows, codes, scales):
-            passes = x_rows.shape[2] // K_PASS
-            rows = raw_pool.tile([P, RT, passes * K_PASS], BF16, name="rows", tag="rows")
-            nc.sync.dma_start(out=rows[:], in_=x_rows)
-            rows_grouped = grouped_pool.tile([P, passes * ROWS * PACK], BF16, align_bytes=64)
-            pairs = rows_grouped[:].bitcast(F32).rearrange("p (c r u) -> p c r u", c=passes, u=2)
-            for c in range(passes):
-                planes = psum_t.tile([P, 2, ROWS], F32, name="planes", tag="bank")
+        def transpose_rows(rows):
+            banks = []
+            for c in range(rows.shape[2] // K_PASS):
+                planes = psum.tile([P, 2, ROWS], F32, name="planes", tag="bank")
                 for rt in range(RT):
                     words = rows[:, rt, c * K_PASS : (c + 1) * K_PASS].bitcast(F32)
                     words = words.rearrange("p (q u) -> p u q", u=2)
                     for u in range(2):
                         nc.tensor.transpose(planes[:, u, rt * P : (rt + 1) * P], words[:, u, :], ident[:])
-                nc.scalar.copy(out=pairs[:, c], in_=planes[:].rearrange("p u r -> p r u"))
+                banks.append(planes)
+            return banks
+
+        state = {"unit": 0, "waiting": None}
+
+        def finish_waiting():
+            job = state["waiting"]
+            if job is None:
+                return
+            uses = job["uses"]
+            w_codes = quantised_pool.tile([P, len(uses), HID], U32, align_bytes=64)
+            w_scales = quantised_pool.tile([P, len(uses), HID], U8, align_bytes=64)
             nc.vector.quantize_mx(
-                out=codes.rearrange("p c r -> p (c r)").bitcast(FP8X4),
-                scales=scales.rearrange("p c r -> p (c r)"),
-                in_=rows_grouped[:],
+                out=w_codes[:].rearrange("p c w -> p (c w)").bitcast(FP8X4),
+                scales=w_scales[:].rearrange("p c w -> p (c w)"),
+                in_=job["grouped"][:].rearrange("p w t -> p (w t)"),
             )
-
-        def new_sums():
-            return [psum_acc.tile([P, HID], F32, name="sums%d" % rt, tag="sums") for rt in range(RT)]
-
-        def multiply(sums, x_codes, x_scales, c, w_codes, w_scales, n, start, stop):
-            for rt in range(RT):
-                r = slice(rt * P, (rt + 1) * P)
-                nc.tensor.matmul_mx(
-                    out=sums[rt][:],
-                    lhsT=x_codes[:, c, r].bitcast(FP8X4),
-                    lhsT_scale=x_scales[:, c, r],
-                    rhs=w_codes[:, n, :].bitcast(FP8X4),
-                    rhs_scale=w_scales[:, n, :],
-                    start=start,
-                    stop=stop,
+            if job["rows_grouped"] is not None:
+                codes, scales, c0 = uses[0][0], uses[0][1], uses[0][2]
+                nc.vector.quantize_mx(
+                    out=codes[:, c0 : c0 + len(uses), :].rearrange("p c r -> p (c r)").bitcast(FP8X4),
+                    scales=scales[:, c0 : c0 + len(uses), :].rearrange("p c r -> p (c r)"),
+                    in_=job["rows_grouped"][:],
                 )
+            for n, (codes, scales, c, start, stop) in enumerate(uses):
+                if start:
+                    for rt in range(RT):
+                        job["sums"].append(psum.tile([P, HID], F32, name="sums%d" % rt, tag="bank"))
+                for rt in range(RT):
+                    r = slice(rt * P, (rt + 1) * P)
+                    nc.tensor.matmul_mx(
+                        out=job["sums"][rt][:],
+                        lhsT=codes[:, c, r].bitcast(FP8X4),
+                        lhsT_scale=scales[:, c, r],
+                        rhs=w_codes[:, n, :].bitcast(FP8X4),
+                        rhs_scale=w_scales[:, n, :],
+                        start=start,
+                        stop=stop,
+                    )
+            state["waiting"] = None
+
+        def weight_unit(sums, uses, from_rows):
+            i = state["unit"]
+            state["unit"] = i + 1
+            load_unit(i + AHEAD)
+            if from_rows:
+                banks = transpose_rows(slices[i])
+            advance_chains()
+            grouped = grouped_pool.tile([P, len(uses) * HID, PACK], BF16, align_bytes=64)
+            if len(uses) == UNIT:
+                first, second = (grouped[:, :HID], raws[i][:, 0]), (grouped[:, HID:], raws[i][:, 1])
+            else:
+                half = HID // 2
+                first = (grouped[:, :half], raws[i][:, 0, :, :half])
+                second = (grouped[:, half:], raws[i][:, 0, :, half:])
+            dst, src = regrouped(first[0], first[1])
+            nc.vector.tensor_copy(out=dst, in_=src)
+            dst, src = regrouped(second[0], second[1])
+            nc.scalar.copy(out=dst, in_=src)
+            rows_grouped = None
+            if from_rows:
+                rows_grouped = grouped_pool.tile([P, len(uses) * ROWS * PACK], BF16, align_bytes=64)
+                pairs = rows_grouped[:].bitcast(F32).rearrange("p (c r u) -> p c r u", c=len(uses), u=2)
+                for c in range(len(uses)):
+                    nc.scalar.copy(out=pairs[:, c], in_=banks[c][:].rearrange("p u r -> p r u"))
+            advance_chains()
+            finish_waiting()
+            state["waiting"] = {"grouped": grouped, "rows_grouped": rows_grouped, "sums": sums, "uses": uses}
 
         def inverse_std(mean_var):
             var_eps = small.tile([P, RT, 1], F32)
@@ -131,106 +193,135 @@ def tile_blockrecurrentmodel_pa_kernel(
 
         x_codes, x_scales = codes_and_scales(3, "x")
 
-        def embed(x, weight, in_codes, in_scales, vec, place):
-            x_rows = x.flatten_outer_dims().rearrange("(rt p) k -> p rt k", p=P)
-            passes = weight.shape[0] // K_PASS
-            unit = min(passes, UNIT)
-            sums = new_sums()
-            for c0 in range(0, passes, unit):
-                k = slice(c0 * K_PASS, (c0 + unit) * K_PASS)
-                w_codes, w_scales = quantise_weight(weight[k, :])
-                quantise_rows(x_rows[:, :, k], in_codes[:, c0 : c0 + unit, :], in_scales[:, c0 : c0 + unit, :])
-                for n in range(unit):
-                    c = c0 + n
-                    multiply(sums, in_codes, in_scales, c, w_codes, w_scales, n, c == 0, c == passes - 1)
+        def embedding_norm(sums, vec, place):
+            tiles = {}
 
-            stats = small.tile([P, RT, BN_DIM], F32)
-            mean_var = small.tile([P, RT, 2], F32)
-            for rt in range(RT):
-                nc.vector.bn_stats(out=stats[:, rt, :], in_=sums[rt][:])
-                nc.vector.bn_aggr(out=mean_var[:, rt, :], in_=stats[:, rt, :])
-            rstd = inverse_std(mean_var)
-            shift = small.tile([P, RT, 1], F32)
-            nc.vector.scalar_tensor_tensor(
-                out=shift[:], in0=mean_var[:, :, 0:1], scalar=-1.0, in1=rstd[:], op0=ALU.mult, op1=ALU.mult
-            )
-            z = []
-            for rt in range(RT):
-                z.append(norm_pool.tile([P, PACK, P], F32, name="z%d" % rt, tag="z"))
-                nc.scalar.activation(
-                    out=z[rt][:],
-                    in_=sums[rt][:].rearrange("r (q t) -> r t q", t=PACK),
-                    func=ACT.Identity,
-                    bias=shift[:, rt, :],
-                    scale=rstd[:, rt, :],
+            def statistics():
+                stats = small.tile([P, RT, BN_DIM], F32)
+                tiles["mean_var"] = small.tile([P, RT, 2], F32, name="mean_var")
+                for rt in range(RT):
+                    nc.vector.bn_stats(out=stats[:, rt, :], in_=sums[rt][:])
+                    nc.vector.bn_aggr(out=tiles["mean_var"][:, rt, :], in_=stats[:, rt, :])
+                tiles["rstd"] = inverse_std(tiles["mean_var"])
+
+            def normalise():
+                shift = small.tile([P, RT, 1], F32)
+                nc.vector.scalar_tensor_tensor(
+                    out=shift[:], in0=tiles["mean_var"][:, :, 0:1], scalar=-1.0, in1=tiles["rstd"][:],
+                    op0=ALU.mult, op1=ALU.mult,
+                )
+                tiles["cols"] = small.tile([P, 2, PACK], F32, name="cols")
+                nc.vector.tensor_copy(out=tiles["cols"][:], in_=cols_bf[:, 2 * vec : 2 * vec + 2, 0:PACK])
+                z = []
+                for rt in range(RT):
+                    z.append(norm_pool.tile([P, PACK, P], F32, name="z%d" % rt, tag="z"))
+                    nc.scalar.activation(
+                        out=z[rt][:],
+                        in_=sums[rt][:].rearrange("r (q t) -> r t q", t=PACK),
+                        func=ACT.Identity,
+                        bias=shift[:, rt, :],
+                        scale=tiles["rstd"][:, rt, :],
+                    )
+                tiles["z_t"] = []
+                for half in range(2):
+                    tiles["z_t"].append(psum.tile([P, 2, ROWS], F32, name="z_t%d" % half, tag="bank"))
+                    for i in range(2):
+                        for rt in range(RT):
+                            nc.tensor.transpose(
+                                tiles["z_t"][half][:, i, rt * P : (rt + 1) * P], z[rt][:, 2 * half + i, :], ident[:]
+                            )
+
+            def gate():
+                tiles["x_planes"] = norm_pool.tile([P, PACK, ROWS], BF16, name="x_planes")
+                for t in range(PACK):
+                    nc.scalar.activation(
+                        out=tiles["x_planes"][:, t, :],
+                        in_=tiles["z_t"][t // 2][:, t % 2, :],
+                        func=ACT.Silu,
+                        bias=tiles["cols"][:, 1, t : t + 1],
+                        scale=tiles["cols"][:, 0, t : t + 1],
+                    )
+
+            def quantise_x():
+                x_grouped = norm_pool.tile([P, ROWS, PACK], BF16, align_bytes=64)
+                dst, src = regrouped(x_grouped[:], tiles["x_planes"][:])
+                nc.vector.tensor_copy(out=dst, in_=src)
+                nc.vector.quantize_mx(
+                    out=x_codes[:, place, :].bitcast(FP8X4),
+                    scales=x_scales[:, place, :],
+                    in_=x_grouped[:].rearrange("p r t -> p (r t)"),
                 )
 
-            x_planes = norm_pool.tile([P, PACK, ROWS], BF16)
-            for half in range(2):
-                z_t = psum_t.tile([P, 2, ROWS], F32, name="z_t", tag="bank")
-                for i in range(2):
-                    for rt in range(RT):
-                        nc.tensor.transpose(z_t[:, i, rt * P : (rt + 1) * P], z[rt][:, 2 * half + i, :], ident[:])
-                for i in range(2):
-                    t = 2 * half + i
-                    nc.scalar.activation(
-                        out=x_planes[:, t, :],
-                        in_=z_t[:, i, :],
-                        func=ACT.Silu,
-                        bias=cols[:, 2 * vec + 1, t : t + 1],
-                        scale=cols[:, 2 * vec, t : t + 1],
-                    )
-            x_grouped = norm_pool.tile([P, ROWS, PACK], BF16, align_bytes=64)
-            dst, src = regrouped(x_grouped[:], x_planes[:])
-            nc.vector.tensor_copy(out=dst, in_=src)
-            nc.vector.quantize_mx(
-                out=x_codes[:, place, :].bitcast(FP8X4),
-                scales=x_scales[:, place, :],
-                in_=x_grouped[:].rearrange("p r t -> p (r t)"),
-            )
+            open_chain([wait_a_step, wait_a_step, statistics, normalise, gate, quantise_x])
 
-        a_codes, a_scales = codes_and_scales(ACTION // K_PASS, "a")
-        s_codes, s_scales = codes_and_scales(STOCH // K_PASS, "s")
         d_codes, d_scales = codes_and_scales(DETER // K_PASS, "d")
-        embed(a, W_a, a_codes, a_scales, 1, 1)
-        embed(s, W_s, s_codes, s_scales, 0, 0)
-        embed(d, W_d, d_codes, d_scales, 2, 2)
+        for name, width, vec, place in (("a", ACTION, 1, 1), ("s", STOCH, 0, 0), ("d", DETER, 2, 2)):
+            passes = width // K_PASS
+            codes, scales = (d_codes, d_scales) if name == "d" else codes_and_scales(passes, name)
+            sums = []
+            for c0 in range(0, passes, UNIT):
+                cs = range(c0, min(c0 + UNIT, passes))
+                weight_unit(sums, [(codes, scales, c, c == 0, c == passes - 1) for c in cs], True)
+            embedding_norm(sums, vec, place)
 
         pre = keep.tile([P, RT, DETER], F32)
         stats = keep.tile([P, RT, G, BN_DIM], F32)
-        for g in range(G):
-            sums = new_sums()
-            for c0 in range(0, BLK_PASSES, UNIT):
-                w_codes, w_scales = quantise_weight(W_hid[g, c0 * K_PASS : (c0 + UNIT) * K_PASS, :])
-                for n in range(UNIT):
-                    c = c0 + n
-                    if c == 0:
-                        multiply(sums, d_codes, d_scales, g, w_codes, w_scales, n, True, False)
-                    else:
-                        multiply(sums, x_codes, x_scales, c - 1, w_codes, w_scales, n, False, c == BLK_PASSES - 1)
-            for rt in range(RT):
-                block = pre[:, rt, g * BH : (g + 1) * BH]
-                nc.scalar.copy(out=block, in_=sums[rt][:])
-                nc.vector.bn_stats(out=stats[:, rt, g, :], in_=block)
 
-        gain_bias = keep.tile([P, 2, DETER], BF16)
-        nc.sync.dma_start(out=gain_bias[:, 0, :], in_=ln_h_g.partition_broadcast(P))
-        nc.sync.dma_start(out=gain_bias[:, 1, :], in_=ln_h_b.partition_broadcast(P))
+        def close_block(sums, g):
+            def evacuate():
+                for rt in range(RT):
+                    nc.scalar.copy(out=pre[:, rt, g * BH : (g + 1) * BH], in_=sums[rt][:])
+
+            def statistics():
+                for rt in range(RT):
+                    nc.vector.bn_stats(out=stats[:, rt, g, :], in_=pre[:, rt, g * BH : (g + 1) * BH])
+
+            def statistics_in_psum():
+                for rt in range(RT):
+                    nc.vector.bn_stats(out=stats[:, rt, g, :], in_=sums[rt][:])
+
+            if g < G - KEPT:
+                open_chain([wait_a_step, wait_a_step, evacuate, statistics])
+            else:
+                open_chain([wait_a_step, wait_a_step, statistics_in_psum])
+
+        block_sums = []
+        for g in range(G):
+            sums = []
+            block_sums.append(sums)
+            weight_unit(sums, [(d_codes, d_scales, g, True, False), (x_codes, x_scales, 0, False, False)], False)
+            weight_unit(sums, [(x_codes, x_scales, 1, False, False), (x_codes, x_scales, 2, False, True)], False)
+            close_block(sums, g)
+        advance_chains()
+        advance_chains()
+        finish_waiting()
+        advance_chains()
+        advance_chains()
 
         mean_var = small.tile([P, RT, 2], F32)
         for rt in range(RT):
             nc.vector.bn_aggr(out=mean_var[:, rt, :], in_=stats[:, rt].rearrange("p g v -> p (g v)"))
         rstd = inverse_std(mean_var)
-        for rt in range(RT):
-            for c0 in range(0, DETER, TAIL_COLS):
-                piece = pre[:, rt, c0 : c0 + TAIL_COLS]
+        long_piece = (G - KEPT) * BH // 2
+        pieces = [(rt, c0, long_piece, None) for rt in range(RT) for c0 in range(0, (G - KEPT) * BH, long_piece)]
+        pieces.extend([(rt, g * BH, BH, block_sums[g][rt]) for g in range(G - KEPT, G) for rt in range(RT)])
+        for k in range(len(pieces) + 1):
+            if k < len(pieces):
+                rt, c0, width, bank = pieces[k]
                 nc.vector.scalar_tensor_tensor(
-                    out=piece, in0=piece, scalar=mean_var[:, rt, 0:1], in1=gain_bias[:, 0, c0 : c0 + TAIL_COLS],
-                    op0=ALU.subtract, op1=ALU.mult,
+                    out=pre[:, rt, c0 : c0 + width],
+                    in0=pre[:, rt, c0 : c0 + width] if bank is None else bank[:],
+                    scalar=mean_var[:, rt, 0:1],
+                    in1=gain_bias[:, 0, c0 : c0 + width],
+                    op0=ALU.subtract,
+                    op1=ALU.mult,
                 )
+            if k > 0:
+                rt, c0, width, bank = pieces[k - 1]
+                piece = pre[:, rt, c0 : c0 + width]
                 nc.vector.scalar_tensor_tensor(
-                    out=piece, in0=piece, scalar=rstd[:, rt, :], in1=gain_bias[:, 1, c0 : c0 + TAIL_COLS],
+                    out=piece, in0=piece, scalar=rstd[:, rt, :], in1=gain_bias[:, 1, c0 : c0 + width],
                     op0=ALU.mult, op1=ALU.add,
                 )
                 nc.scalar.activation(out=piece, in_=piece, func=ACT.Silu)
-                nc.sync.dma_start(out=out[rt * P : (rt + 1) * P, c0 : c0 + TAIL_COLS], in_=piece)
+                nc.sync.dma_start(out=out[rt * P : (rt + 1) * P, c0 : c0 + width], in_=piece)

@@ -24,8 +24,9 @@ BN_DIM = 6
 
 RUN = 4
 UNIT = 2
-KEPT = 3
 AHEAD = 4
+KEPT = 2
+TAIL_COLS = 1024
 
 FLOPS = 2 * ROWS * ((STOCH + ACTION + DETER) * HID + G * (BH + 3 * HID) * BH)
 
@@ -40,7 +41,7 @@ def tile_blockrecurrentmodel_pa_kernel(
         raw_pool = ctx.enter_context(tc.tile_pool(name="raw", bufs=AHEAD + 1))
         grouped_pool = ctx.enter_context(tc.tile_pool(name="grouped", bufs=3))
         quantised_pool = ctx.enter_context(tc.tile_pool(name="quantised", bufs=5))
-        norm_pool = ctx.enter_context(tc.tile_pool(name="norm", bufs=4))
+        norm_pool = ctx.enter_context(tc.tile_pool(name="norm", bufs=3))
         small = ctx.enter_context(tc.tile_pool(name="small", bufs=4))
         psum = ctx.enter_context(tc.psum_pool(name="psum", bufs=8))
 
@@ -62,7 +63,12 @@ def tile_blockrecurrentmodel_pa_kernel(
                 weight_rows.append(W_hid[g, k0 : k0 + UNIT * K_PASS, :])
         n_units = len(weight_rows)
 
-        gain_bias = keep.tile([P, 2, DETER], BF16)
+        first_kept = (G - KEPT) * BH
+        n_cols = 6 + 2 * KEPT
+        cols_bf = const.tile([P, n_cols, 16], BF16)
+        cols = const.tile([P, n_cols, PACK], F32)
+        gain_bias = keep.tile([P, 2, first_kept], BF16)
+
         raws = {}
         slices = {}
 
@@ -74,29 +80,21 @@ def tile_blockrecurrentmodel_pa_kernel(
                 raws[i] = raw_pool.tile([P, weight_rows[i].shape[0] // K_PASS, PACK, HID], BF16, name="raw", tag="raw")
                 nc.sync.dma_start(out=raws[i][:], in_=weight_rows[i].rearrange("(c p j) n -> p c j n", p=P, j=PACK))
             if i == n_units:
-                nc.sync.dma_start(out=gain_bias[:, 0, :], in_=ln_h_g.partition_broadcast(P))
-                nc.sync.dma_start(out=gain_bias[:, 1, :], in_=ln_h_b.partition_broadcast(P))
+                nc.sync.dma_start(out=gain_bias[:, 0, :], in_=ln_h_g[0:first_kept].partition_broadcast(P))
+                nc.sync.dma_start(out=gain_bias[:, 1, :], in_=ln_h_b[0:first_kept].partition_broadcast(P))
+                for v, vec in enumerate((ln_h_g, ln_h_b)):
+                    nc.sync.dma_start(
+                        out=cols_bf[:, 6 + v : n_cols : 2, 0:PACK],
+                        in_=vec[first_kept:DETER].rearrange("(g q t) -> q g t", q=P, t=PACK),
+                    )
+                nc.vector.tensor_copy(out=cols[:, 6:n_cols, :], in_=cols_bf[:, 6:n_cols, 0:PACK])
 
-        cols_bf = const.tile([P, 6, 16], BF16)
         load_unit(0)
         for i, vec in enumerate((ln_s_g, ln_s_b, ln_a_g, ln_a_b, ln_d_g, ln_d_b)):
             nc.sync.dma_start(out=cols_bf[:, i, 0:PACK], in_=vec.rearrange("(q t) -> q t", t=PACK))
+        nc.vector.tensor_copy(out=cols[:, 0:6, :], in_=cols_bf[:, 0:6, 0:PACK])
         for i in range(1, AHEAD):
             load_unit(i)
-
-        chains = []
-
-        def wait_a_step():
-            return None
-
-        def open_chain(steps):
-            chains.append({"steps": steps, "next": 0})
-
-        def advance_chains():
-            for chain in chains:
-                if chain["next"] < len(chain["steps"]):
-                    chain["steps"][chain["next"]]()
-                    chain["next"] = chain["next"] + 1
 
         def regrouped(dst, src):
             return dst.rearrange("p (c i) t -> p c t i", i=RUN), src.rearrange("p t (c i) -> p c t i", i=RUN)
@@ -157,7 +155,6 @@ def tile_blockrecurrentmodel_pa_kernel(
             load_unit(i + AHEAD)
             if from_rows:
                 banks = transpose_rows(slices[i])
-            advance_chains()
             grouped = grouped_pool.tile([P, len(uses) * HID, PACK], BF16, align_bytes=64)
             if len(uses) == UNIT:
                 first, second = (grouped[:, :HID], raws[i][:, 0]), (grouped[:, HID:], raws[i][:, 1])
@@ -175,16 +172,45 @@ def tile_blockrecurrentmodel_pa_kernel(
                 pairs = rows_grouped[:].bitcast(F32).rearrange("p (c r u) -> p c r u", c=len(uses), u=2)
                 for c in range(len(uses)):
                     nc.scalar.copy(out=pairs[:, c], in_=banks[c][:].rearrange("p u r -> p r u"))
-            advance_chains()
             finish_waiting()
             state["waiting"] = {"grouped": grouped, "rows_grouped": rows_grouped, "sums": sums, "uses": uses}
 
-        def inverse_std(mean_var):
+        def inverse_std_and_shift(mean_var):
             var_eps = small.tile([P, RT, 1], F32)
             nc.vector.tensor_scalar(out=var_eps[:], in0=mean_var[:, :, 1:2], scalar1=EPS, scalar2=None, op0=ALU.add)
             rstd = small.tile([P, RT, 1], F32)
             nc.gpsimd.tensor_tensor(out=rstd[:], in0=var_eps[:], in1=minus_half[:], op=ALU.pow)
-            return rstd
+            shift = small.tile([P, RT, 1], F32)
+            nc.vector.scalar_tensor_tensor(
+                out=shift[:], in0=mean_var[:, :, 0:1], scalar=-1.0, in1=rstd[:], op0=ALU.mult, op1=ALU.mult
+            )
+            return rstd, shift
+
+        def gated_transposed(sums, rstd, shift, vec, gated):
+            z = []
+            for rt in range(RT):
+                z.append(norm_pool.tile([P, PACK, P], F32, name="z%d" % rt, tag="z", bufs=4))
+                nc.scalar.activation(
+                    out=z[rt][:],
+                    in_=sums[rt][:].rearrange("r (q t) -> r t q", t=PACK),
+                    func=ACT.Identity,
+                    bias=shift[:, rt, :],
+                    scale=rstd[:, rt, :],
+                )
+            for half in range(2):
+                z_t = psum.tile([P, 2, ROWS], F32, name="z_t", tag="bank")
+                for i in range(2):
+                    for rt in range(RT):
+                        nc.tensor.transpose(z_t[:, i, rt * P : (rt + 1) * P], z[rt][:, 2 * half + i, :], ident[:])
+                for i in range(2):
+                    t = 2 * half + i
+                    nc.scalar.activation(
+                        out=gated[:, t, :],
+                        in_=z_t[:, i, :],
+                        func=ACT.Silu,
+                        bias=cols[:, vec + 1, t : t + 1],
+                        scale=cols[:, vec, t : t + 1],
+                    )
 
         def codes_and_scales(passes, name):
             codes = keep.tile([P, passes, ROWS], U32, align_bytes=64, name=name + "_codes")
@@ -194,134 +220,99 @@ def tile_blockrecurrentmodel_pa_kernel(
         x_codes, x_scales = codes_and_scales(3, "x")
 
         def embedding_norm(sums, vec, place):
-            tiles = {}
-
-            def statistics():
-                stats = small.tile([P, RT, BN_DIM], F32)
-                tiles["mean_var"] = small.tile([P, RT, 2], F32, name="mean_var")
-                for rt in range(RT):
-                    nc.vector.bn_stats(out=stats[:, rt, :], in_=sums[rt][:])
-                    nc.vector.bn_aggr(out=tiles["mean_var"][:, rt, :], in_=stats[:, rt, :])
-                tiles["rstd"] = inverse_std(tiles["mean_var"])
-
-            def normalise():
-                shift = small.tile([P, RT, 1], F32)
-                nc.vector.scalar_tensor_tensor(
-                    out=shift[:], in0=tiles["mean_var"][:, :, 0:1], scalar=-1.0, in1=tiles["rstd"][:],
-                    op0=ALU.mult, op1=ALU.mult,
-                )
-                tiles["cols"] = small.tile([P, 2, PACK], F32, name="cols")
-                nc.vector.tensor_copy(out=tiles["cols"][:], in_=cols_bf[:, 2 * vec : 2 * vec + 2, 0:PACK])
-                z = []
-                for rt in range(RT):
-                    z.append(norm_pool.tile([P, PACK, P], F32, name="z%d" % rt, tag="z"))
-                    nc.scalar.activation(
-                        out=z[rt][:],
-                        in_=sums[rt][:].rearrange("r (q t) -> r t q", t=PACK),
-                        func=ACT.Identity,
-                        bias=shift[:, rt, :],
-                        scale=tiles["rstd"][:, rt, :],
-                    )
-                tiles["z_t"] = []
-                for half in range(2):
-                    tiles["z_t"].append(psum.tile([P, 2, ROWS], F32, name="z_t%d" % half, tag="bank"))
-                    for i in range(2):
-                        for rt in range(RT):
-                            nc.tensor.transpose(
-                                tiles["z_t"][half][:, i, rt * P : (rt + 1) * P], z[rt][:, 2 * half + i, :], ident[:]
-                            )
-
-            def gate():
-                tiles["x_planes"] = norm_pool.tile([P, PACK, ROWS], BF16, name="x_planes")
-                for t in range(PACK):
-                    nc.scalar.activation(
-                        out=tiles["x_planes"][:, t, :],
-                        in_=tiles["z_t"][t // 2][:, t % 2, :],
-                        func=ACT.Silu,
-                        bias=tiles["cols"][:, 1, t : t + 1],
-                        scale=tiles["cols"][:, 0, t : t + 1],
-                    )
-
-            def quantise_x():
-                x_grouped = norm_pool.tile([P, ROWS, PACK], BF16, align_bytes=64)
-                dst, src = regrouped(x_grouped[:], tiles["x_planes"][:])
-                nc.vector.tensor_copy(out=dst, in_=src)
-                nc.vector.quantize_mx(
-                    out=x_codes[:, place, :].bitcast(FP8X4),
-                    scales=x_scales[:, place, :],
-                    in_=x_grouped[:].rearrange("p r t -> p (r t)"),
-                )
-
-            open_chain([wait_a_step, wait_a_step, statistics, normalise, gate, quantise_x])
+            stats = small.tile([P, RT, BN_DIM], F32)
+            mean_var = small.tile([P, RT, 2], F32)
+            for rt in range(RT):
+                nc.vector.bn_stats(out=stats[:, rt, :], in_=sums[rt][:])
+                nc.vector.bn_aggr(out=mean_var[:, rt, :], in_=stats[:, rt, :])
+            rstd, shift = inverse_std_and_shift(mean_var)
+            x_planes = norm_pool.tile([P, PACK, ROWS], BF16)
+            gated_transposed(sums, rstd, shift, vec, x_planes)
+            x_grouped = norm_pool.tile([P, ROWS, PACK], BF16, align_bytes=64)
+            dst, src = regrouped(x_grouped[:], x_planes[:])
+            nc.vector.tensor_copy(out=dst, in_=src)
+            nc.vector.quantize_mx(
+                out=x_codes[:, place, :].bitcast(FP8X4),
+                scales=x_scales[:, place, :],
+                in_=x_grouped[:].rearrange("p r t -> p (r t)"),
+            )
 
         d_codes, d_scales = codes_and_scales(DETER // K_PASS, "d")
-        for name, width, vec, place in (("a", ACTION, 1, 1), ("s", STOCH, 0, 0), ("d", DETER, 2, 2)):
+        open_norm = None
+        for name, width, vec, place in (("a", ACTION, 2, 1), ("s", STOCH, 0, 0), ("d", DETER, 4, 2)):
             passes = width // K_PASS
             codes, scales = (d_codes, d_scales) if name == "d" else codes_and_scales(passes, name)
             sums = []
             for c0 in range(0, passes, UNIT):
                 cs = range(c0, min(c0 + UNIT, passes))
                 weight_unit(sums, [(codes, scales, c, c == 0, c == passes - 1) for c in cs], True)
-            embedding_norm(sums, vec, place)
+                if c0 == 0 and open_norm is not None:
+                    embedding_norm(open_norm[0], open_norm[1], open_norm[2])
+            open_norm = (sums, vec, place)
 
-        pre = keep.tile([P, RT, DETER], F32)
+        result = keep.tile([P, RT, DETER], F32)
         stats = keep.tile([P, RT, G, BN_DIM], F32)
 
-        def close_block(sums, g):
-            def evacuate():
-                for rt in range(RT):
-                    nc.scalar.copy(out=pre[:, rt, g * BH : (g + 1) * BH], in_=sums[rt][:])
-
-            def statistics():
-                for rt in range(RT):
-                    nc.vector.bn_stats(out=stats[:, rt, g, :], in_=pre[:, rt, g * BH : (g + 1) * BH])
-
-            def statistics_in_psum():
-                for rt in range(RT):
-                    nc.vector.bn_stats(out=stats[:, rt, g, :], in_=sums[rt][:])
-
-            if g < G - KEPT:
-                open_chain([wait_a_step, wait_a_step, evacuate, statistics])
-            else:
-                open_chain([wait_a_step, wait_a_step, statistics_in_psum])
+        def close_block(g):
+            for rt in range(RT):
+                if g < G - KEPT:
+                    block = result[:, rt, g * BH : (g + 1) * BH]
+                    nc.scalar.copy(out=block, in_=block_sums[g][rt][:])
+                    nc.vector.bn_stats(out=stats[:, rt, g, :], in_=block)
+                else:
+                    nc.vector.bn_stats(out=stats[:, rt, g, :], in_=block_sums[g][rt][:])
 
         block_sums = []
         for g in range(G):
-            sums = []
-            block_sums.append(sums)
-            weight_unit(sums, [(d_codes, d_scales, g, True, False), (x_codes, x_scales, 0, False, False)], False)
-            weight_unit(sums, [(x_codes, x_scales, 1, False, False), (x_codes, x_scales, 2, False, True)], False)
-            close_block(sums, g)
-        advance_chains()
-        advance_chains()
+            block_sums.append([])
+            weight_unit(block_sums[g], [(d_codes, d_scales, g, True, False), (x_codes, x_scales, 0, False, False)], False)
+            if g == 0:
+                embedding_norm(open_norm[0], open_norm[1], open_norm[2])
+            else:
+                close_block(g - 1)
+            weight_unit(block_sums[g], [(x_codes, x_scales, 1, False, False), (x_codes, x_scales, 2, False, True)], False)
         finish_waiting()
-        advance_chains()
-        advance_chains()
+        close_block(G - 1)
 
         mean_var = small.tile([P, RT, 2], F32)
         for rt in range(RT):
             nc.vector.bn_aggr(out=mean_var[:, rt, :], in_=stats[:, rt].rearrange("p g v -> p (g v)"))
-        rstd = inverse_std(mean_var)
-        long_piece = (G - KEPT) * BH // 2
-        pieces = [(rt, c0, long_piece, None) for rt in range(RT) for c0 in range(0, (G - KEPT) * BH, long_piece)]
-        pieces.extend([(rt, g * BH, BH, block_sums[g][rt]) for g in range(G - KEPT, G) for rt in range(RT)])
+        rstd, shift = inverse_std_and_shift(mean_var)
+
+        def store(rt, c0, width):
+            nc.sync.dma_start(out=out[rt * P : (rt + 1) * P, c0 : c0 + width], in_=result[:, rt, c0 : c0 + width])
+
+        for g in range(G - KEPT, G):
+            gated = norm_pool.tile([P, PACK, ROWS], F32)
+            gated_transposed(block_sums[g], rstd, shift, 6 + 2 * (g - (G - KEPT)), gated)
+            for rt in range(RT):
+                back = psum.tile([P, PACK, P], F32, name="back", tag="bank")
+                for t in range(PACK):
+                    nc.tensor.transpose(back[:, t, :], gated[:, t, rt * P : (rt + 1) * P], ident[:])
+                nc.scalar.copy(
+                    out=result[:, rt, g * BH : (g + 1) * BH].rearrange("r (q t) -> r q t", t=PACK),
+                    in_=back[:].rearrange("r t q -> r q t"),
+                )
+                store(rt, g * BH, BH)
+
+        pieces = [(rt, c0) for rt in range(RT) for c0 in range(0, first_kept, TAIL_COLS)]
         for k in range(len(pieces) + 1):
             if k < len(pieces):
-                rt, c0, width, bank = pieces[k]
+                rt, c0 = pieces[k]
                 nc.vector.scalar_tensor_tensor(
-                    out=pre[:, rt, c0 : c0 + width],
-                    in0=pre[:, rt, c0 : c0 + width] if bank is None else bank[:],
+                    out=result[:, rt, c0 : c0 + TAIL_COLS],
+                    in0=result[:, rt, c0 : c0 + TAIL_COLS],
                     scalar=mean_var[:, rt, 0:1],
-                    in1=gain_bias[:, 0, c0 : c0 + width],
+                    in1=gain_bias[:, 0, c0 : c0 + TAIL_COLS],
                     op0=ALU.subtract,
                     op1=ALU.mult,
                 )
             if k > 0:
-                rt, c0, width, bank = pieces[k - 1]
-                piece = pre[:, rt, c0 : c0 + width]
+                rt, c0 = pieces[k - 1]
+                piece = result[:, rt, c0 : c0 + TAIL_COLS]
                 nc.vector.scalar_tensor_tensor(
-                    out=piece, in0=piece, scalar=rstd[:, rt, :], in1=gain_bias[:, 1, c0 : c0 + width],
+                    out=piece, in0=piece, scalar=rstd[:, rt, :], in1=gain_bias[:, 1, c0 : c0 + TAIL_COLS],
                     op0=ALU.mult, op1=ALU.add,
                 )
                 nc.scalar.activation(out=piece, in_=piece, func=ACT.Silu)
-                nc.sync.dma_start(out=out[rt * P : (rt + 1) * P, c0 : c0 + width], in_=piece)
+                store(rt, c0, TAIL_COLS)

@@ -1,4 +1,5 @@
 from contextlib import ExitStack
+from functools import partial
 
 import concourse.mybir as mybir
 from concourse.masks import make_identity
@@ -20,10 +21,14 @@ STOCH, ACTION, HID, DETER, G = 1024, 512, 512, 4096, 8
 BH = DETER // G
 BLK_PASSES = (BH + 3 * HID) // K_PASS
 EPS = 1e-3
-BN_DIM = 6
+TRIPLE = 3
+BN_DIM = 2 * TRIPLE
 
 RUN = 4
 UNIT = 2
+SCALAR_COLS_1 = 400
+SCALAR_COLS_2 = 336
+LAG = 2
 AHEAD = 4
 KEPT = 2
 TAIL_COLS = 1024
@@ -39,8 +44,8 @@ def tile_blockrecurrentmodel_pa_kernel(
         const = ctx.enter_context(tc.tile_pool(name="const", bufs=1))
         keep = ctx.enter_context(tc.tile_pool(name="keep", bufs=1))
         raw_pool = ctx.enter_context(tc.tile_pool(name="raw", bufs=AHEAD + 1))
-        grouped_pool = ctx.enter_context(tc.tile_pool(name="grouped", bufs=3))
-        quantised_pool = ctx.enter_context(tc.tile_pool(name="quantised", bufs=5))
+        grouped_pool = ctx.enter_context(tc.tile_pool(name="grouped", bufs=LAG + 3))
+        quantised_pool = ctx.enter_context(tc.tile_pool(name="quantised", bufs=6))
         norm_pool = ctx.enter_context(tc.tile_pool(name="norm", bufs=3))
         small = ctx.enter_context(tc.tile_pool(name="small", bufs=4))
         psum = ctx.enter_context(tc.psum_pool(name="psum", bufs=8))
@@ -111,12 +116,9 @@ def tile_blockrecurrentmodel_pa_kernel(
                 banks.append(planes)
             return banks
 
-        state = {"unit": 0, "waiting": None}
+        jobs = []
 
-        def finish_waiting():
-            job = state["waiting"]
-            if job is None:
-                return
+        def finish(job):
             uses = job["uses"]
             w_codes = quantised_pool.tile([P, len(uses), HID], U32, align_bytes=64)
             w_scales = quantised_pool.tile([P, len(uses), HID], U8, align_bytes=64)
@@ -147,33 +149,37 @@ def tile_blockrecurrentmodel_pa_kernel(
                         start=start,
                         stop=stop,
                     )
-            state["waiting"] = None
+            if job["after"] is not None:
+                job["after"]()
 
-        def weight_unit(sums, uses, from_rows):
-            i = state["unit"]
-            state["unit"] = i + 1
+        def weight_unit(sums, uses, from_rows, after=None):
+            i = len(jobs)
             load_unit(i + AHEAD)
             if from_rows:
                 banks = transpose_rows(slices[i])
             grouped = grouped_pool.tile([P, len(uses) * HID, PACK], BF16, align_bytes=64)
-            if len(uses) == UNIT:
-                first, second = (grouped[:, :HID], raws[i][:, 0]), (grouped[:, HID:], raws[i][:, 1])
-            else:
-                half = HID // 2
-                first = (grouped[:, :half], raws[i][:, 0, :, :half])
-                second = (grouped[:, half:], raws[i][:, 0, :, half:])
-            dst, src = regrouped(first[0], first[1])
-            nc.vector.tensor_copy(out=dst, in_=src)
-            dst, src = regrouped(second[0], second[1])
-            nc.scalar.copy(out=dst, in_=src)
+            scalar_cols = (SCALAR_COLS_1 if from_rows else SCALAR_COLS_2) * len(uses) // UNIT
+            for c in range(len(uses)):
+                vector_cols = HID - scalar_cols if c == len(uses) - 1 else HID
+                if vector_cols > 0:
+                    dst, src = regrouped(
+                        grouped[:, c * HID : c * HID + vector_cols], raws[i][:, c, :, :vector_cols]
+                    )
+                    nc.vector.tensor_copy(out=dst, in_=src)
+                if vector_cols < HID:
+                    dst, src = regrouped(
+                        grouped[:, c * HID + vector_cols : (c + 1) * HID], raws[i][:, c, :, vector_cols:]
+                    )
+                    nc.scalar.copy(out=dst, in_=src)
             rows_grouped = None
             if from_rows:
-                rows_grouped = grouped_pool.tile([P, len(uses) * ROWS * PACK], BF16, align_bytes=64)
+                rows_grouped = grouped_pool.tile([P, len(uses) * ROWS * PACK], BF16, align_bytes=64, bufs=LAG + 1)
                 pairs = rows_grouped[:].bitcast(F32).rearrange("p (c r u) -> p c r u", c=len(uses), u=2)
                 for c in range(len(uses)):
                     nc.scalar.copy(out=pairs[:, c], in_=banks[c][:].rearrange("p u r -> p r u"))
-            finish_waiting()
-            state["waiting"] = {"grouped": grouped, "rows_grouped": rows_grouped, "sums": sums, "uses": uses}
+            jobs.append({"grouped": grouped, "rows_grouped": rows_grouped, "sums": sums, "uses": uses, "after": after})
+            if i >= LAG:
+                finish(jobs[i - LAG])
 
         def inverse_std_and_shift(mean_var):
             var_eps = small.tile([P, RT, 1], F32)
@@ -226,9 +232,9 @@ def tile_blockrecurrentmodel_pa_kernel(
                 nc.vector.bn_stats(out=stats[:, rt, :], in_=sums[rt][:])
                 nc.vector.bn_aggr(out=mean_var[:, rt, :], in_=stats[:, rt, :])
             rstd, shift = inverse_std_and_shift(mean_var)
-            x_planes = norm_pool.tile([P, PACK, ROWS], BF16)
+            x_planes = norm_pool.tile([P, PACK, ROWS], BF16, bufs=2)
             gated_transposed(sums, rstd, shift, vec, x_planes)
-            x_grouped = norm_pool.tile([P, ROWS, PACK], BF16, align_bytes=64)
+            x_grouped = norm_pool.tile([P, ROWS, PACK], BF16, align_bytes=64, bufs=2)
             dst, src = regrouped(x_grouped[:], x_planes[:])
             nc.vector.tensor_copy(out=dst, in_=src)
             nc.vector.quantize_mx(
@@ -238,52 +244,71 @@ def tile_blockrecurrentmodel_pa_kernel(
             )
 
         d_codes, d_scales = codes_and_scales(DETER // K_PASS, "d")
-        open_norm = None
         for name, width, vec, place in (("a", ACTION, 2, 1), ("s", STOCH, 0, 0), ("d", DETER, 4, 2)):
             passes = width // K_PASS
             codes, scales = (d_codes, d_scales) if name == "d" else codes_and_scales(passes, name)
             sums = []
             for c0 in range(0, passes, UNIT):
                 cs = range(c0, min(c0 + UNIT, passes))
-                weight_unit(sums, [(codes, scales, c, c == 0, c == passes - 1) for c in cs], True)
-                if c0 == 0 and open_norm is not None:
-                    embedding_norm(open_norm[0], open_norm[1], open_norm[2])
-            open_norm = (sums, vec, place)
+                after = partial(embedding_norm, sums, vec, place) if cs[-1] == passes - 1 else None
+                weight_unit(sums, [(codes, scales, c, c == 0, c == passes - 1) for c in cs], True, after)
 
         result = keep.tile([P, RT, DETER], F32)
-        stats = keep.tile([P, RT, G, BN_DIM], F32)
+        n_early = G - KEPT
+        stats = keep.tile([P, RT, n_early + 2 * KEPT, TRIPLE], F32)
+        nc.vector.memset(stats[:, :, 0:n_early, 0:1], float(BH))
 
         def close_block(g):
-            for rt in range(RT):
-                if g < G - KEPT:
-                    block = result[:, rt, g * BH : (g + 1) * BH]
-                    nc.scalar.copy(out=block, in_=block_sums[g][rt][:])
-                    nc.vector.bn_stats(out=stats[:, rt, g, :], in_=block)
-                else:
-                    nc.vector.bn_stats(out=stats[:, rt, g, :], in_=block_sums[g][rt][:])
+            if g < n_early:
+                total = small.tile([P, RT, 1], F32)
+                for rt in range(RT):
+                    nc.scalar.activation(
+                        out=result[:, rt, g * BH : (g + 1) * BH],
+                        in_=block_sums[g][rt][:],
+                        func=ACT.Identity,
+                        accum_out=total[:, rt, :],
+                    )
+                nc.scalar.activation(out=stats[:, :, g, 1:2], in_=total[:], func=ACT.Copy, scale=1.0 / BH)
+                for rt in range(RT):
+                    squares = norm_pool.tile([P, BH], BF16, name="squares", tag="squares", bufs=2)
+                    nc.scalar.activation(
+                        out=squares[:],
+                        in_=result[:, rt, g * BH : (g + 1) * BH],
+                        func=ACT.Square,
+                        scale=-1.0,
+                        bias=stats[:, rt, g, 1:2],
+                        accum_out=stats[:, rt, g, 2:3],
+                    )
+            else:
+                first = n_early + 2 * (g - n_early)
+                for rt in range(RT):
+                    nc.vector.bn_stats(
+                        out=stats[:, rt, first : first + 2, :].rearrange("p n v -> p (n v)"), in_=block_sums[g][rt][:]
+                    )
 
         block_sums = []
         for g in range(G):
             block_sums.append([])
             weight_unit(block_sums[g], [(d_codes, d_scales, g, True, False), (x_codes, x_scales, 0, False, False)], False)
-            if g == 0:
-                embedding_norm(open_norm[0], open_norm[1], open_norm[2])
-            else:
-                close_block(g - 1)
-            weight_unit(block_sums[g], [(x_codes, x_scales, 1, False, False), (x_codes, x_scales, 2, False, True)], False)
-        finish_waiting()
-        close_block(G - 1)
+            weight_unit(
+                block_sums[g],
+                [(x_codes, x_scales, 1, False, False), (x_codes, x_scales, 2, False, True)],
+                False,
+                partial(close_block, g),
+            )
+        for job in jobs[n_units - LAG :]:
+            finish(job)
 
         mean_var = small.tile([P, RT, 2], F32)
         for rt in range(RT):
-            nc.vector.bn_aggr(out=mean_var[:, rt, :], in_=stats[:, rt].rearrange("p g v -> p (g v)"))
+            nc.vector.bn_aggr(out=mean_var[:, rt, :], in_=stats[:, rt].rearrange("p n v -> p (n v)"))
         rstd, shift = inverse_std_and_shift(mean_var)
 
         def store(rt, c0, width):
             nc.sync.dma_start(out=out[rt * P : (rt + 1) * P, c0 : c0 + width], in_=result[:, rt, c0 : c0 + width])
 
         for g in range(G - KEPT, G):
-            gated = norm_pool.tile([P, PACK, ROWS], F32)
+            gated = norm_pool.tile([P, PACK, ROWS], F32, bufs=2)
             gated_transposed(block_sums[g], rstd, shift, 6 + 2 * (g - (G - KEPT)), gated)
             for rt in range(RT):
                 back = psum.tile([P, PACK, P], F32, name="back", tag="bank")

@@ -24,7 +24,7 @@ EPS = 1e-3
 TRIPLE = 3
 BN_DIM = 2 * TRIPLE
 
-RUN = 4
+RUN = 2
 UNIT = 2
 SCALAR_COLS_1 = 400
 SCALAR_COLS_2 = 336

@@ -26,12 +26,12 @@ BN_DIM = 2 * TRIPLE
 
 RUN = 2
 UNIT = 2
-SCALAR_COLS_1 = 400
-SCALAR_COLS_2 = 336
+SCALAR_COLS_1 = 416
+SCALAR_COLS_2 = (512, 480, 272, 272, 272, 272, 512, 512)
 LAG = 2
-AHEAD = 4
-KEPT = 2
-TAIL_COLS = 1024
+AHEAD = 3
+KEPT = 4
+SCALED = 4
 
 FLOPS = 2 * ROWS * ((STOCH + ACTION + DETER) * HID + G * (BH + 3 * HID) * BH)
 
@@ -52,6 +52,8 @@ def tile_blockrecurrentmodel_pa_kernel(
 
         ident = const.tile([P, P], F32)
         make_identity(nc, ident[:])
+        ident_bf = const.tile([P, P], BF16)
+        make_identity(nc, ident_bf[:])
         minus_half = const.tile([P, RT, 1], F32)
         nc.vector.memset(minus_half[:], -0.5)
 
@@ -68,11 +70,15 @@ def tile_blockrecurrentmodel_pa_kernel(
                 weight_rows.append(W_hid[g, k0 : k0 + UNIT * K_PASS, :])
         n_units = len(weight_rows)
 
-        first_kept = (G - KEPT) * BH
-        n_cols = 6 + 2 * KEPT
+        first_plain = SCALED * BH
+        n_cols = 6 + SCALED
         cols_bf = const.tile([P, n_cols, 16], BF16)
         cols = const.tile([P, n_cols, PACK], F32)
-        gain_bias = keep.tile([P, 2, first_kept], BF16)
+        gain_bias = keep.tile([P, 2, DETER - first_plain], BF16)
+        term_rows = keep.tile([P, first_plain], BF16)
+        nc.gpsimd.memset(term_rows[:], 0.0)
+        terms = keep.tile([P, RT, P], BF16)
+        nc.gpsimd.memset(terms[:], 0.0)
 
         raws = {}
         slices = {}
@@ -84,15 +90,17 @@ def tile_blockrecurrentmodel_pa_kernel(
             if i < n_units:
                 raws[i] = raw_pool.tile([P, weight_rows[i].shape[0] // K_PASS, PACK, HID], BF16, name="raw", tag="raw")
                 nc.sync.dma_start(out=raws[i][:], in_=weight_rows[i].rearrange("(c p j) n -> p c j n", p=P, j=PACK))
-            if i == n_units:
-                nc.sync.dma_start(out=gain_bias[:, 0, :], in_=ln_h_g[0:first_kept].partition_broadcast(P))
-                nc.sync.dma_start(out=gain_bias[:, 1, :], in_=ln_h_b[0:first_kept].partition_broadcast(P))
-                for v, vec in enumerate((ln_h_g, ln_h_b)):
-                    nc.sync.dma_start(
-                        out=cols_bf[:, 6 + v : n_cols : 2, 0:PACK],
-                        in_=vec[first_kept:DETER].rearrange("(g q t) -> q g t", q=P, t=PACK),
-                    )
+            if i == len(row_slices):
+                nc.sync.dma_start(
+                    out=cols_bf[:, 6:n_cols, 0:PACK],
+                    in_=ln_h_g[0:first_plain].rearrange("(g q t) -> q g t", q=P, t=PACK),
+                )
                 nc.vector.tensor_copy(out=cols[:, 6:n_cols, :], in_=cols_bf[:, 6:n_cols, 0:PACK])
+            if i == n_units:
+                for v, vec in enumerate((ln_h_g, ln_h_b)):
+                    nc.sync.dma_start(out=gain_bias[:, v, :], in_=vec[first_plain:DETER].partition_broadcast(P))
+                for row, vec in enumerate((ln_h_b, ln_h_g, ln_h_b, ln_h_g)):
+                    nc.sync.dma_start(out=term_rows[row : row + 1, :], in_=vec[0:first_plain].unsqueeze(0))
 
         load_unit(0)
         for i, vec in enumerate((ln_s_g, ln_s_b, ln_a_g, ln_a_b, ln_d_g, ln_d_b)):
@@ -152,13 +160,13 @@ def tile_blockrecurrentmodel_pa_kernel(
             if job["after"] is not None:
                 job["after"]()
 
-        def weight_unit(sums, uses, from_rows, after=None):
+        def weight_unit(sums, uses, scalar_cols, from_rows, after=None):
             i = len(jobs)
             load_unit(i + AHEAD)
             if from_rows:
                 banks = transpose_rows(slices[i])
             grouped = grouped_pool.tile([P, len(uses) * HID, PACK], BF16, align_bytes=64)
-            scalar_cols = (SCALAR_COLS_1 if from_rows else SCALAR_COLS_2) * len(uses) // UNIT
+            scalar_cols = scalar_cols * len(uses) // UNIT
             for c in range(len(uses)):
                 vector_cols = HID - scalar_cols if c == len(uses) - 1 else HID
                 if vector_cols > 0:
@@ -181,40 +189,26 @@ def tile_blockrecurrentmodel_pa_kernel(
             if i >= LAG:
                 finish(jobs[i - LAG])
 
-        def inverse_std_and_shift(mean_var):
+        def inverse_std(mean_var):
             var_eps = small.tile([P, RT, 1], F32)
             nc.vector.tensor_scalar(out=var_eps[:], in0=mean_var[:, :, 1:2], scalar1=EPS, scalar2=None, op0=ALU.add)
             rstd = small.tile([P, RT, 1], F32)
             nc.gpsimd.tensor_tensor(out=rstd[:], in0=var_eps[:], in1=minus_half[:], op=ALU.pow)
-            shift = small.tile([P, RT, 1], F32)
-            nc.vector.scalar_tensor_tensor(
-                out=shift[:], in0=mean_var[:, :, 0:1], scalar=-1.0, in1=rstd[:], op0=ALU.mult, op1=ALU.mult
-            )
-            return rstd, shift
+            return var_eps, rstd
 
-        def gated_transposed(sums, rstd, shift, vec, gated):
-            z = []
-            for rt in range(RT):
-                z.append(norm_pool.tile([P, PACK, P], F32, name="z%d" % rt, tag="z", bufs=4))
-                nc.scalar.activation(
-                    out=z[rt][:],
-                    in_=sums[rt][:].rearrange("r (q t) -> r t q", t=PACK),
-                    func=ACT.Identity,
-                    bias=shift[:, rt, :],
-                    scale=rstd[:, rt, :],
-                )
+        def transposed(planes, out, func, vec):
             for half in range(2):
                 z_t = psum.tile([P, 2, ROWS], F32, name="z_t", tag="bank")
                 for i in range(2):
                     for rt in range(RT):
-                        nc.tensor.transpose(z_t[:, i, rt * P : (rt + 1) * P], z[rt][:, 2 * half + i, :], ident[:])
+                        nc.tensor.transpose(z_t[:, i, rt * P : (rt + 1) * P], planes[rt][:, 2 * half + i, :], ident[:])
                 for i in range(2):
                     t = 2 * half + i
                     nc.scalar.activation(
-                        out=gated[:, t, :],
+                        out=out[:, t, :],
                         in_=z_t[:, i, :],
-                        func=ACT.Silu,
-                        bias=cols[:, vec + 1, t : t + 1],
+                        func=func,
+                        bias=cols[:, vec + 1, t : t + 1] if func == ACT.Silu else 0.0,
                         scale=cols[:, vec, t : t + 1],
                     )
 
@@ -231,9 +225,23 @@ def tile_blockrecurrentmodel_pa_kernel(
             for rt in range(RT):
                 nc.vector.bn_stats(out=stats[:, rt, :], in_=sums[rt][:])
                 nc.vector.bn_aggr(out=mean_var[:, rt, :], in_=stats[:, rt, :])
-            rstd, shift = inverse_std_and_shift(mean_var)
+            rstd = inverse_std(mean_var)[1]
+            shift = small.tile([P, RT, 1], F32)
+            nc.vector.scalar_tensor_tensor(
+                out=shift[:], in0=mean_var[:, :, 0:1], scalar=-1.0, in1=rstd[:], op0=ALU.mult, op1=ALU.mult
+            )
+            z = []
+            for rt in range(RT):
+                z.append(norm_pool.tile([P, PACK, P], F32, name="z%d" % rt, tag="z", bufs=4))
+                nc.scalar.activation(
+                    out=z[rt][:],
+                    in_=sums[rt][:].rearrange("r (q t) -> r t q", t=PACK),
+                    func=ACT.Identity,
+                    bias=shift[:, rt, :],
+                    scale=rstd[:, rt, :],
+                )
             x_planes = norm_pool.tile([P, PACK, ROWS], BF16, bufs=2)
-            gated_transposed(sums, rstd, shift, vec, x_planes)
+            transposed(z, x_planes, ACT.Silu, vec)
             x_grouped = norm_pool.tile([P, ROWS, PACK], BF16, align_bytes=64, bufs=2)
             dst, src = regrouped(x_grouped[:], x_planes[:])
             nc.vector.tensor_copy(out=dst, in_=src)
@@ -251,9 +259,10 @@ def tile_blockrecurrentmodel_pa_kernel(
             for c0 in range(0, passes, UNIT):
                 cs = range(c0, min(c0 + UNIT, passes))
                 after = partial(embedding_norm, sums, vec, place) if cs[-1] == passes - 1 else None
-                weight_unit(sums, [(codes, scales, c, c == 0, c == passes - 1) for c in cs], True, after)
+                weight_unit(sums, [(codes, scales, c, c == 0, c == passes - 1) for c in cs], SCALAR_COLS_1, True, after)
 
         result = keep.tile([P, RT, DETER], F32)
+        scaled = keep.tile([P, SCALED, PACK, ROWS], F32)
         n_early = G - KEPT
         stats = keep.tile([P, RT, n_early + 2 * KEPT, TRIPLE], F32)
         nc.vector.memset(stats[:, :, 0:n_early, 0:1], float(BH))
@@ -261,10 +270,16 @@ def tile_blockrecurrentmodel_pa_kernel(
         def close_block(g):
             if g < n_early:
                 total = small.tile([P, RT, 1], F32)
+                planes = []
                 for rt in range(RT):
+                    block, block_sum = result[:, rt, g * BH : (g + 1) * BH], block_sums[g][rt][:]
+                    if g < SCALED:
+                        block = block.rearrange("r (t q) -> r t q", t=PACK)
+                        block_sum = block_sum.rearrange("r (q t) -> r t q", t=PACK)
+                    planes.append(block)
                     nc.scalar.activation(
-                        out=result[:, rt, g * BH : (g + 1) * BH],
-                        in_=block_sums[g][rt][:],
+                        out=block,
+                        in_=block_sum,
                         func=ACT.Identity,
                         accum_out=total[:, rt, :],
                     )
@@ -279,6 +294,8 @@ def tile_blockrecurrentmodel_pa_kernel(
                         bias=stats[:, rt, g, 1:2],
                         accum_out=stats[:, rt, g, 2:3],
                     )
+                if g < SCALED:
+                    transposed(planes, scaled[:, g], ACT.Copy, 6 + g)
             else:
                 first = n_early + 2 * (g - n_early)
                 for rt in range(RT):
@@ -289,10 +306,16 @@ def tile_blockrecurrentmodel_pa_kernel(
         block_sums = []
         for g in range(G):
             block_sums.append([])
-            weight_unit(block_sums[g], [(d_codes, d_scales, g, True, False), (x_codes, x_scales, 0, False, False)], False)
+            weight_unit(
+                block_sums[g],
+                [(d_codes, d_scales, g, True, False), (x_codes, x_scales, 0, False, False)],
+                SCALAR_COLS_2[g],
+                False,
+            )
             weight_unit(
                 block_sums[g],
                 [(x_codes, x_scales, 1, False, False), (x_codes, x_scales, 2, False, True)],
+                SCALAR_COLS_2[g],
                 False,
                 partial(close_block, g),
             )
@@ -302,42 +325,76 @@ def tile_blockrecurrentmodel_pa_kernel(
         mean_var = small.tile([P, RT, 2], F32)
         for rt in range(RT):
             nc.vector.bn_aggr(out=mean_var[:, rt, :], in_=stats[:, rt].rearrange("p n v -> p (n v)"))
-        rstd, shift = inverse_std_and_shift(mean_var)
+        var_eps, rstd = inverse_std(mean_var)
 
         def store(rt, c0, width):
             nc.sync.dma_start(out=out[rt * P : (rt + 1) * P, c0 : c0 + width], in_=result[:, rt, c0 : c0 + width])
 
-        for g in range(G - KEPT, G):
-            gated = norm_pool.tile([P, PACK, ROWS], F32, bufs=2)
-            gated_transposed(block_sums[g], rstd, shift, 6 + 2 * (g - (G - KEPT)), gated)
+        std_mean = small.tile([P, RT, 2], F32)
+        nc.vector.tensor_scalar(
+            out=std_mean[:, :, 1:2], in0=mean_var[:, :, 0:1], scalar1=-1.0, scalar2=None, op0=ALU.mult
+        )
+        nc.vector.tensor_tensor(out=std_mean[:, :, 0:1], in0=var_eps[:], in1=rstd[:], op=ALU.mult)
+        nc.vector.tensor_copy(out=terms[:, :, 0:2], in_=std_mean[:])
+        nc.vector.tensor_tensor(out=terms[:, :, 2:4], in0=std_mean[:], in1=terms[:, :, 0:2], op=ALU.subtract)
+        terms_t = psum.tile([P, RT, P], BF16, name="terms_t", tag="bank")
+        for rt in range(RT):
+            nc.tensor.transpose(terms_t[:, rt, :], terms[:, rt, :], ident_bf[:])
+        row_terms = keep.tile([P, RT, P], BF16)
+        nc.vector.tensor_copy(out=row_terms[:], in_=terms_t[:])
+
+        def finish_scaled(g):
             for rt in range(RT):
-                back = psum.tile([P, PACK, P], F32, name="back", tag="bank")
+                total = psum.tile([P, PACK, P], F32, name="total", tag="bank")
+                nc.tensor.matmul(
+                    out=total[:],
+                    lhsT=row_terms[:, rt, :],
+                    rhs=term_rows[:, g * BH : (g + 1) * BH].rearrange("k (q t) -> k t q", t=PACK),
+                    start=True,
+                    stop=False,
+                )
                 for t in range(PACK):
-                    nc.tensor.transpose(back[:, t, :], gated[:, t, rt * P : (rt + 1) * P], ident[:])
-                nc.scalar.copy(
+                    nc.tensor.matmul(
+                        out=total[:, t, :],
+                        lhsT=scaled[:, g, t, rt * P : (rt + 1) * P],
+                        rhs=ident[:],
+                        is_transpose=True,
+                        start=False,
+                        stop=t == PACK - 1,
+                    )
+                nc.scalar.activation(
                     out=result[:, rt, g * BH : (g + 1) * BH].rearrange("r (q t) -> r q t", t=PACK),
-                    in_=back[:].rearrange("r t q -> r q t"),
+                    in_=total[:].rearrange("r t q -> r q t"),
+                    func=ACT.Silu,
+                    scale=rstd[:, rt, :],
                 )
                 store(rt, g * BH, BH)
 
-        pieces = [(rt, c0) for rt in range(RT) for c0 in range(0, first_kept, TAIL_COLS)]
+        pieces = [(rt, g) for g in range(SCALED, G) for rt in range(RT)]
         for k in range(len(pieces) + 1):
             if k < len(pieces):
-                rt, c0 = pieces[k]
+                rt, g = pieces[k]
+                block = result[:, rt, g * BH : (g + 1) * BH]
                 nc.vector.scalar_tensor_tensor(
-                    out=result[:, rt, c0 : c0 + TAIL_COLS],
-                    in0=result[:, rt, c0 : c0 + TAIL_COLS],
+                    out=block,
+                    in0=block if g < n_early else block_sums[g][rt][:],
                     scalar=mean_var[:, rt, 0:1],
-                    in1=gain_bias[:, 0, c0 : c0 + TAIL_COLS],
+                    in1=gain_bias[:, 0, (g - SCALED) * BH : (g - SCALED + 1) * BH],
                     op0=ALU.subtract,
                     op1=ALU.mult,
                 )
             if k > 0:
-                rt, c0 = pieces[k - 1]
-                piece = result[:, rt, c0 : c0 + TAIL_COLS]
+                rt, g = pieces[k - 1]
+                block = result[:, rt, g * BH : (g + 1) * BH]
                 nc.vector.scalar_tensor_tensor(
-                    out=piece, in0=piece, scalar=rstd[:, rt, :], in1=gain_bias[:, 1, c0 : c0 + TAIL_COLS],
-                    op0=ALU.mult, op1=ALU.add,
+                    out=block,
+                    in0=block,
+                    scalar=rstd[:, rt, :],
+                    in1=gain_bias[:, 1, (g - SCALED) * BH : (g - SCALED + 1) * BH],
+                    op0=ALU.mult,
+                    op1=ALU.add,
                 )
-                nc.scalar.activation(out=piece, in_=piece, func=ACT.Silu)
-                store(rt, c0, TAIL_COLS)
+                nc.scalar.activation(out=block, in_=block, func=ACT.Silu)
+                store(rt, g * BH, BH)
+            if k % 2 == 0 and k // 2 < SCALED:
+                finish_scaled(k // 2)

@@ -26,11 +26,18 @@ BN_DIM = 2 * TRIPLE
 
 RUN = 2
 UNIT = 2
-SCALAR_COLS_1 = 416
-SCALAR_COLS_2 = (512, 480, 272, 272, 272, 272, 512, 512)
+UNITS_A, UNITS_S, UNITS_D = (1,), (1, 1), (1, 1, 2, 2, 2)
+SCALAR_COLS_1 = 448
+SCALAR_COLS_2 = 560
+SCALAR_COLS_CLOSING = 160
+SCALAR_COLS_LATE = 640
 LAG = 2
+CLOSING_FROM, CLOSING_TO = 6, 13
+CATCH_UP = 2 * (G - 4)
+X_SLOTS = 6
 AHEAD = 3
 KEPT = 4
+SCALAR_STATS = (6,)
 SCALED = 4
 
 FLOPS = 2 * ROWS * ((STOCH + ACTION + DETER) * HID + G * (BH + 3 * HID) * BH)
@@ -49,6 +56,7 @@ def tile_blockrecurrentmodel_pa_kernel(
         norm_pool = ctx.enter_context(tc.tile_pool(name="norm", bufs=3))
         small = ctx.enter_context(tc.tile_pool(name="small", bufs=4))
         psum = ctx.enter_context(tc.psum_pool(name="psum", bufs=8))
+        ctx.enter_context(tc.manual_schedule())
 
         ident = const.tile([P, P], F32)
         make_identity(nc, ident[:])
@@ -59,15 +67,20 @@ def tile_blockrecurrentmodel_pa_kernel(
 
         weight_rows = []
         row_slices = []
-        for x, w, width in ((a, W_a, ACTION), (s, W_s, STOCH), (d, W_d, DETER)):
+        for x, w, passes in ((a, W_a, UNITS_A), (s, W_s, UNITS_S), (d, W_d, UNITS_D)):
             x_rows = x.flatten_outer_dims().rearrange("(rt p) k -> p rt k", p=P)
-            step = min(width, UNIT * K_PASS)
-            for k0 in range(0, width, step):
-                weight_rows.append(w[k0 : k0 + step, :])
-                row_slices.append(x_rows[:, :, k0 : k0 + step])
+            k0 = 0
+            for n in passes:
+                k1 = k0 + n * K_PASS
+                weight_rows.append(w[k0:k1, :])
+                row_slices.append(x_rows[:, :, k0:k1])
+                k0 = k1
+        block_units = [(UNIT, UNIT)] * (G - 1) + [(UNIT, 1, 1)]
         for g in range(G):
-            for k0 in range(0, BLK_PASSES * K_PASS, UNIT * K_PASS):
-                weight_rows.append(W_hid[g, k0 : k0 + UNIT * K_PASS, :])
+            k0 = 0
+            for n in block_units[g]:
+                weight_rows.append(W_hid[g, k0 : k0 + n * K_PASS, :])
+                k0 += n * K_PASS
         n_units = len(weight_rows)
 
         first_plain = SCALED * BH
@@ -84,30 +97,30 @@ def tile_blockrecurrentmodel_pa_kernel(
         slices = {}
 
         def load_unit(i):
-            if i < len(row_slices):
-                slices[i] = raw_pool.tile([P, RT, row_slices[i].shape[2]], BF16, name="rows", tag="rows")
-                nc.sync.dma_start(out=slices[i][:], in_=row_slices[i])
             if i < n_units:
                 raws[i] = raw_pool.tile([P, weight_rows[i].shape[0] // K_PASS, PACK, HID], BF16, name="raw", tag="raw")
                 nc.sync.dma_start(out=raws[i][:], in_=weight_rows[i].rearrange("(c p j) n -> p c j n", p=P, j=PACK))
+            if i < len(row_slices):
+                slices[i] = raw_pool.tile([P, RT, row_slices[i].shape[2]], BF16, name="rows", tag="rows")
+                nc.sync.dma_start(out=slices[i][:], in_=row_slices[i])
             if i == len(row_slices):
                 nc.sync.dma_start(
                     out=cols_bf[:, 6:n_cols, 0:PACK],
                     in_=ln_h_g[0:first_plain].rearrange("(g q t) -> q g t", q=P, t=PACK),
                 )
-                nc.vector.tensor_copy(out=cols[:, 6:n_cols, :], in_=cols_bf[:, 6:n_cols, 0:PACK])
             if i == n_units:
                 for v, vec in enumerate((ln_h_g, ln_h_b)):
                     nc.sync.dma_start(out=gain_bias[:, v, :], in_=vec[first_plain:DETER].partition_broadcast(P))
                 for row, vec in enumerate((ln_h_b, ln_h_g, ln_h_b, ln_h_g)):
                     nc.sync.dma_start(out=term_rows[row : row + 1, :], in_=vec[0:first_plain].unsqueeze(0))
 
-        load_unit(0)
+        for i in range(AHEAD):
+            load_unit(i)
         for i, vec in enumerate((ln_s_g, ln_s_b, ln_a_g, ln_a_b, ln_d_g, ln_d_b)):
             nc.sync.dma_start(out=cols_bf[:, i, 0:PACK], in_=vec.rearrange("(q t) -> q t", t=PACK))
-        nc.vector.tensor_copy(out=cols[:, 0:6, :], in_=cols_bf[:, 0:6, 0:PACK])
-        for i in range(1, AHEAD):
-            load_unit(i)
+
+        def widen(first, last):
+            nc.vector.tensor_copy(out=cols[:, first:last, :], in_=cols_bf[:, first:last, 0:PACK])
 
         def regrouped(dst, src):
             return dst.rearrange("p (c i) t -> p c t i", i=RUN), src.rearrange("p t (c i) -> p c t i", i=RUN)
@@ -124,25 +137,63 @@ def tile_blockrecurrentmodel_pa_kernel(
                 banks.append(planes)
             return banks
 
+        agenda = {}
+
+        def plan(slot, point, step):
+            agenda.setdefault((slot, point), []).append(step)
+
+        def work_off(slot, point):
+            for step in agenda.get((slot, point), []):
+                step()
+
         jobs = []
 
-        def finish(job):
+        def regroup(i):
+            job = jobs[i]
+            n = len(job["uses"])
+            grouped = grouped_pool.tile([P, n * HID, PACK], BF16, align_bytes=64, name="grouped", tag="grouped")
+            job["grouped"] = grouped
+            scalar_cols = job["scalar_cols"]
+            for c in range(n):
+                vector_cols = max(0, min(HID, n * HID - scalar_cols - c * HID))
+                if vector_cols > 0:
+                    dst, src = regrouped(grouped[:, c * HID : c * HID + vector_cols], raws[i][:, c, :, :vector_cols])
+                    nc.vector.tensor_copy(out=dst, in_=src)
+                if vector_cols < HID:
+                    dst, src = regrouped(grouped[:, c * HID + vector_cols : (c + 1) * HID], raws[i][:, c, :, vector_cols:])
+                    nc.scalar.copy(out=dst, in_=src)
+            if i in slices:
+                rows_grouped = grouped_pool.tile(
+                    [P, n * ROWS * PACK], BF16, align_bytes=64, bufs=LAG + 1, name="rows_grouped", tag="rows_grouped"
+                )
+                job["rows_grouped"] = rows_grouped
+                pairs = rows_grouped[:].bitcast(F32).rearrange("p (c r u) -> p c r u", c=n, u=2)
+                for c in range(n):
+                    nc.scalar.copy(out=pairs[:, c], in_=job["banks"][c][:].rearrange("p u r -> p r u"))
+
+        def quantise(i):
+            job = jobs[i]
             uses = job["uses"]
-            w_codes = quantised_pool.tile([P, len(uses), HID], U32, align_bytes=64)
-            w_scales = quantised_pool.tile([P, len(uses), HID], U8, align_bytes=64)
+            w_codes = quantised_pool.tile([P, len(uses), HID], U32, align_bytes=64, name="w_codes", tag="w_codes")
+            w_scales = quantised_pool.tile([P, len(uses), HID], U8, align_bytes=64, name="w_scales", tag="w_scales")
+            job["w"] = (w_codes, w_scales)
             nc.vector.quantize_mx(
                 out=w_codes[:].rearrange("p c w -> p (c w)").bitcast(FP8X4),
                 scales=w_scales[:].rearrange("p c w -> p (c w)"),
                 in_=job["grouped"][:].rearrange("p w t -> p (w t)"),
             )
-            if job["rows_grouped"] is not None:
+            if i in slices:
                 codes, scales, c0 = uses[0][0], uses[0][1], uses[0][2]
                 nc.vector.quantize_mx(
                     out=codes[:, c0 : c0 + len(uses), :].rearrange("p c r -> p (c r)").bitcast(FP8X4),
                     scales=scales[:, c0 : c0 + len(uses), :].rearrange("p c r -> p (c r)"),
                     in_=job["rows_grouped"][:],
                 )
-            for n, (codes, scales, c, start, stop) in enumerate(uses):
+
+        def multiply(i, slot):
+            job = jobs[i]
+            w_codes, w_scales = job["w"]
+            for n, (codes, scales, c, start, stop) in enumerate(job["uses"]):
                 if start:
                     for rt in range(RT):
                         job["sums"].append(psum.tile([P, HID], F32, name="sums%d" % rt, tag="bank"))
@@ -158,59 +209,34 @@ def tile_blockrecurrentmodel_pa_kernel(
                         stop=stop,
                     )
             if job["after"] is not None:
-                job["after"]()
-
-        def weight_unit(sums, uses, scalar_cols, from_rows, after=None):
-            i = len(jobs)
-            load_unit(i + AHEAD)
-            if from_rows:
-                banks = transpose_rows(slices[i])
-            grouped = grouped_pool.tile([P, len(uses) * HID, PACK], BF16, align_bytes=64)
-            scalar_cols = scalar_cols * len(uses) // UNIT
-            for c in range(len(uses)):
-                vector_cols = HID - scalar_cols if c == len(uses) - 1 else HID
-                if vector_cols > 0:
-                    dst, src = regrouped(
-                        grouped[:, c * HID : c * HID + vector_cols], raws[i][:, c, :, :vector_cols]
-                    )
-                    nc.vector.tensor_copy(out=dst, in_=src)
-                if vector_cols < HID:
-                    dst, src = regrouped(
-                        grouped[:, c * HID + vector_cols : (c + 1) * HID], raws[i][:, c, :, vector_cols:]
-                    )
-                    nc.scalar.copy(out=dst, in_=src)
-            rows_grouped = None
-            if from_rows:
-                rows_grouped = grouped_pool.tile([P, len(uses) * ROWS * PACK], BF16, align_bytes=64, bufs=LAG + 1)
-                pairs = rows_grouped[:].bitcast(F32).rearrange("p (c r u) -> p c r u", c=len(uses), u=2)
-                for c in range(len(uses)):
-                    nc.scalar.copy(out=pairs[:, c], in_=banks[c][:].rearrange("p u r -> p r u"))
-            jobs.append({"grouped": grouped, "rows_grouped": rows_grouped, "sums": sums, "uses": uses, "after": after})
-            if i >= LAG:
-                finish(jobs[i - LAG])
+                job["after"](slot)
 
         def inverse_std(mean_var):
-            var_eps = small.tile([P, RT, 1], F32)
+            var_eps = small.tile([P, RT, 1], F32, name="var_eps", tag="var_eps")
             nc.vector.tensor_scalar(out=var_eps[:], in0=mean_var[:, :, 1:2], scalar1=EPS, scalar2=None, op0=ALU.add)
-            rstd = small.tile([P, RT, 1], F32)
+            rstd = small.tile([P, RT, 1], F32, name="rstd", tag="rstd")
             nc.gpsimd.tensor_tensor(out=rstd[:], in0=var_eps[:], in1=minus_half[:], op=ALU.pow)
             return var_eps, rstd
 
-        def transposed(planes, out, func, vec):
+        def turn(planes):
+            banks = []
             for half in range(2):
                 z_t = psum.tile([P, 2, ROWS], F32, name="z_t", tag="bank")
                 for i in range(2):
                     for rt in range(RT):
                         nc.tensor.transpose(z_t[:, i, rt * P : (rt + 1) * P], planes[rt][:, 2 * half + i, :], ident[:])
-                for i in range(2):
-                    t = 2 * half + i
-                    nc.scalar.activation(
-                        out=out[:, t, :],
-                        in_=z_t[:, i, :],
-                        func=func,
-                        bias=cols[:, vec + 1, t : t + 1] if func == ACT.Silu else 0.0,
-                        scale=cols[:, vec, t : t + 1],
-                    )
+                banks.append(z_t)
+            return banks
+
+        def turned_out(banks, out, func, vec):
+            for t in range(PACK):
+                nc.scalar.activation(
+                    out=out[:, t, :],
+                    in_=banks[t // 2][:, t % 2, :],
+                    func=func,
+                    bias=cols[:, vec + 1, t : t + 1] if func == ACT.Silu else 0.0,
+                    scale=cols[:, vec, t : t + 1],
+                )
 
         def codes_and_scales(passes, name):
             codes = keep.tile([P, passes, ROWS], U32, align_bytes=64, name=name + "_codes")
@@ -219,182 +245,273 @@ def tile_blockrecurrentmodel_pa_kernel(
 
         x_codes, x_scales = codes_and_scales(3, "x")
 
-        def embedding_norm(sums, vec, place):
-            stats = small.tile([P, RT, BN_DIM], F32)
-            mean_var = small.tile([P, RT, 2], F32)
-            for rt in range(RT):
-                nc.vector.bn_stats(out=stats[:, rt, :], in_=sums[rt][:])
-                nc.vector.bn_aggr(out=mean_var[:, rt, :], in_=stats[:, rt, :])
-            rstd = inverse_std(mean_var)[1]
-            shift = small.tile([P, RT, 1], F32)
-            nc.vector.scalar_tensor_tensor(
-                out=shift[:], in0=mean_var[:, :, 0:1], scalar=-1.0, in1=rstd[:], op0=ALU.mult, op1=ALU.mult
-            )
-            z = []
-            for rt in range(RT):
-                z.append(norm_pool.tile([P, PACK, P], F32, name="z%d" % rt, tag="z", bufs=4))
-                nc.scalar.activation(
-                    out=z[rt][:],
-                    in_=sums[rt][:].rearrange("r (q t) -> r t q", t=PACK),
-                    func=ACT.Identity,
-                    bias=shift[:, rt, :],
-                    scale=rstd[:, rt, :],
+        def embedding_norm(sums, vec, place, slot):
+            held = {}
+
+            def statistics():
+                stats = small.tile([P, RT, BN_DIM], F32, name="emb_stats", tag="emb_stats")
+                mean_var = small.tile([P, RT, 2], F32, name="emb_mean_var", tag="emb_mean_var")
+                for rt in range(RT):
+                    nc.vector.bn_stats(out=stats[:, rt, :], in_=sums[rt][:])
+                for rt in range(RT):
+                    nc.vector.bn_aggr(out=mean_var[:, rt, :], in_=stats[:, rt, :])
+                held["mean_var"] = mean_var
+                held["rstd"] = inverse_std(mean_var)[1]
+
+            def normalise():
+                shift = small.tile([P, RT, 1], F32, name="shift", tag="shift")
+                nc.vector.scalar_tensor_tensor(
+                    out=shift[:], in0=held["mean_var"][:, :, 0:1], scalar=-1.0, in1=held["rstd"][:], op0=ALU.mult, op1=ALU.mult
                 )
-            x_planes = norm_pool.tile([P, PACK, ROWS], BF16, bufs=2)
-            transposed(z, x_planes, ACT.Silu, vec)
-            x_grouped = norm_pool.tile([P, ROWS, PACK], BF16, align_bytes=64, bufs=2)
-            dst, src = regrouped(x_grouped[:], x_planes[:])
-            nc.vector.tensor_copy(out=dst, in_=src)
-            nc.vector.quantize_mx(
-                out=x_codes[:, place, :].bitcast(FP8X4),
-                scales=x_scales[:, place, :],
-                in_=x_grouped[:].rearrange("p r t -> p (r t)"),
-            )
+                z = []
+                for rt in range(RT):
+                    z.append(norm_pool.tile([P, PACK, P], F32, name="z%d" % rt, tag="z", bufs=4))
+                    nc.scalar.activation(
+                        out=z[rt][:],
+                        in_=sums[rt][:].rearrange("r (q t) -> r t q", t=PACK),
+                        func=ACT.Identity,
+                        bias=shift[:, rt, :],
+                        scale=held["rstd"][:, rt, :],
+                    )
+                held["banks"] = turn(z)
+
+            def gate():
+                held["x_planes"] = norm_pool.tile([P, PACK, ROWS], BF16, bufs=2, name="x_planes", tag="x_planes")
+                turned_out(held["banks"], held["x_planes"], ACT.Silu, vec)
+
+            def regroup_x():
+                held["x_grouped"] = norm_pool.tile([P, ROWS, PACK], BF16, align_bytes=64, bufs=2, name="x_grouped", tag="x_grouped")
+                dst, src = regrouped(held["x_grouped"][:], held["x_planes"][:])
+                nc.vector.tensor_copy(out=dst, in_=src)
+
+            def quantise_x():
+                nc.vector.quantize_mx(
+                    out=x_codes[:, place, :].bitcast(FP8X4),
+                    scales=x_scales[:, place, :],
+                    in_=held["x_grouped"][:].rearrange("p r t -> p (r t)"),
+                )
+
+            plan(slot + 1, "A", statistics)
+            plan(slot + 2, "A", normalise)
+            plan(slot + 3, "A", gate)
+            plan(slot + 5, "A", regroup_x)
+            plan(slot + 5, "B", quantise_x)
+
+        def add_unit(sums, uses, scalar_cols, after):
+            jobs.append({"sums": sums, "uses": uses, "scalar_cols": scalar_cols, "after": after})
 
         d_codes, d_scales = codes_and_scales(DETER // K_PASS, "d")
-        for name, width, vec, place in (("a", ACTION, 2, 1), ("s", STOCH, 0, 0), ("d", DETER, 4, 2)):
-            passes = width // K_PASS
+        for name, units, vec, place in (("a", UNITS_A, 2, 1), ("s", UNITS_S, 0, 0), ("d", UNITS_D, 4, 2)):
+            passes = sum(units)
+            c0 = 0
             codes, scales = (d_codes, d_scales) if name == "d" else codes_and_scales(passes, name)
             sums = []
-            for c0 in range(0, passes, UNIT):
-                cs = range(c0, min(c0 + UNIT, passes))
+            for n in units:
+                cs = range(c0, c0 + n)
+                c0 += n
                 after = partial(embedding_norm, sums, vec, place) if cs[-1] == passes - 1 else None
-                weight_unit(sums, [(codes, scales, c, c == 0, c == passes - 1) for c in cs], SCALAR_COLS_1, True, after)
+                add_unit(
+                    sums,
+                    [(codes, scales, c, c == 0, c == passes - 1) for c in cs],
+                    SCALAR_COLS_1 * len(cs) // UNIT,
+                    after,
+                )
 
         result = keep.tile([P, RT, DETER], F32)
         scaled = keep.tile([P, SCALED, PACK, ROWS], F32)
         n_early = G - KEPT
-        stats = keep.tile([P, RT, n_early + 2 * KEPT, TRIPLE], F32)
-        nc.vector.memset(stats[:, :, 0:n_early, 0:1], float(BH))
+        by_scalar_too = [g for g in range(G) if g < n_early or g in SCALAR_STATS]
+        n_single = len(by_scalar_too)
+        triples = {}
+        for g in range(G):
+            triples[g] = by_scalar_too.index(g) if g in by_scalar_too else n_single + 2 * (g - sum(b < g for b in by_scalar_too))
+        stats = keep.tile([P, RT, n_single + 2 * (G - n_single), TRIPLE], F32)
+        nc.vector.memset(stats[:, :, 0:n_single, 0:1], float(BH))
 
-        def close_block(g):
-            if g < n_early:
-                total = small.tile([P, RT, 1], F32)
+        def close_block(g, slot):
+            held = {}
+
+            def squared(block, rt):
+                squares = norm_pool.tile([P, BH], BF16, name="squares", tag="squares", bufs=2)
+                nc.scalar.activation(
+                    out=squares[:],
+                    in_=block,
+                    func=ACT.Square,
+                    scale=-1.0,
+                    bias=stats[:, rt, triples[g], 1:2],
+                    accum_out=stats[:, rt, triples[g], 2:3],
+                )
+
+            def early():
+                total = small.tile([P, RT, 1], F32, name="total", tag="total")
                 planes = []
                 for rt in range(RT):
-                    block, block_sum = result[:, rt, g * BH : (g + 1) * BH], block_sums[g][rt][:]
-                    if g < SCALED:
-                        block = block.rearrange("r (t q) -> r t q", t=PACK)
-                        block_sum = block_sum.rearrange("r (q t) -> r t q", t=PACK)
+                    block = result[:, rt, g * BH : (g + 1) * BH].rearrange("r (t q) -> r t q", t=PACK)
                     planes.append(block)
                     nc.scalar.activation(
                         out=block,
-                        in_=block_sum,
+                        in_=block_sums[g][rt][:].rearrange("r (q t) -> r t q", t=PACK),
                         func=ACT.Identity,
                         accum_out=total[:, rt, :],
                     )
-                nc.scalar.activation(out=stats[:, :, g, 1:2], in_=total[:], func=ACT.Copy, scale=1.0 / BH)
+                nc.scalar.activation(out=stats[:, :, triples[g], 1:2], in_=total[:], func=ACT.Copy, scale=1.0 / BH)
+                held["banks"] = turn(planes)
+
+            def variance():
                 for rt in range(RT):
-                    squares = norm_pool.tile([P, BH], BF16, name="squares", tag="squares", bufs=2)
-                    nc.scalar.activation(
-                        out=squares[:],
-                        in_=result[:, rt, g * BH : (g + 1) * BH],
-                        func=ACT.Square,
-                        scale=-1.0,
-                        bias=stats[:, rt, g, 1:2],
-                        accum_out=stats[:, rt, g, 2:3],
-                    )
-                if g < SCALED:
-                    transposed(planes, scaled[:, g], ACT.Copy, 6 + g)
-            else:
-                first = n_early + 2 * (g - n_early)
+                    squared(result[:, rt, g * BH : (g + 1) * BH], rt)
+                turned_out(held["banks"], scaled[:, g], ACT.Copy, 6 + g)
+
+            def late():
                 for rt in range(RT):
                     nc.vector.bn_stats(
-                        out=stats[:, rt, first : first + 2, :].rearrange("p n v -> p (n v)"), in_=block_sums[g][rt][:]
+                        out=stats[:, rt, triples[g] : triples[g] + 2, :].rearrange("p n v -> p (n v)"),
+                        in_=block_sums[g][rt][:],
                     )
 
+            def by_scalar():
+                total = small.tile([P, RT, 1], F32, name="total", tag="total")
+                for rt in range(RT):
+                    copy = norm_pool.tile([P, BH], BF16, name="squares", tag="squares", bufs=2)
+                    nc.scalar.activation(
+                        out=copy[:], in_=block_sums[g][rt][:], func=ACT.Identity, accum_out=total[:, rt, :]
+                    )
+                nc.scalar.activation(out=stats[:, :, triples[g], 1:2], in_=total[:], func=ACT.Copy, scale=1.0 / BH)
+                for rt in range(RT):
+                    squared(block_sums[g][rt][:], rt)
+
+            if g < n_early:
+                plan(slot + 1, "A", early)
+                plan(slot + 2, "A", variance)
+            elif g in SCALAR_STATS:
+                plan(slot + 1, "B", by_scalar)
+            else:
+                plan(slot + 1, "B", late)
+
         block_sums = []
+        j = 0
         for g in range(G):
             block_sums.append([])
-            weight_unit(
-                block_sums[g],
-                [(d_codes, d_scales, g, True, False), (x_codes, x_scales, 0, False, False)],
-                SCALAR_COLS_2[g],
-                False,
-            )
-            weight_unit(
-                block_sums[g],
-                [(x_codes, x_scales, 1, False, False), (x_codes, x_scales, 2, False, True)],
-                SCALAR_COLS_2[g],
-                False,
-                partial(close_block, g),
-            )
-        for job in jobs[n_units - LAG :]:
-            finish(job)
+            uses = [(d_codes, d_scales, g, True, False)]
+            uses += [(x_codes, x_scales, c, False, c == 2) for c in range(3)]
+            for u, n in enumerate(block_units[g]):
+                if j < CLOSING_FROM:
+                    cols2 = SCALAR_COLS_2
+                elif j < CLOSING_TO:
+                    cols2 = SCALAR_COLS_CLOSING
+                else:
+                    cols2 = SCALAR_COLS_LATE
+                last = u == len(block_units[g]) - 1
+                add_unit(block_sums[g], uses[:n], cols2 * n // UNIT, partial(close_block, g) if last else None)
+                uses = uses[n:]
+                j += 1
 
-        mean_var = small.tile([P, RT, 2], F32)
+        n_stage_1 = len(row_slices)
+        plan(LAG + 1, "A", partial(widen, 0, 6))
+        plan(n_stage_1 + LAG, "A", partial(widen, 6, n_cols))
+        done = n_stage_1
+        for slot in range(n_units + LAG + 2):
+            if slot < n_units + 1:
+                load_unit(slot + AHEAD)
+            if slot == 0:
+                jobs[0]["banks"] = transpose_rows(slices[0])
+            if slot < n_units:
+                regroup(slot)
+            if slot + 1 < n_stage_1:
+                jobs[slot + 1]["banks"] = transpose_rows(slices[slot + 1])
+            work_off(slot, "A")
+            if 0 <= slot - LAG < n_units:
+                quantise(slot - LAG)
+            work_off(slot, "B")
+            if 0 <= slot - LAG < n_stage_1:
+                multiply(slot - LAG, slot)
+            for i in (done, done + 1):
+                if i > done and i < n_stage_1 + CATCH_UP:
+                    continue
+                if n_stage_1 <= i <= min(slot - LAG, n_units - 1) and (i == n_stage_1 or slot >= n_stage_1 + X_SLOTS):
+                    multiply(i, slot)
+                    done = i + 1
+
+        mean_var = small.tile([P, RT, 2], F32, name="mean_var", tag="mean_var")
         for rt in range(RT):
             nc.vector.bn_aggr(out=mean_var[:, rt, :], in_=stats[:, rt].rearrange("p n v -> p (n v)"))
         var_eps, rstd = inverse_std(mean_var)
 
-        def store(rt, c0, width):
-            nc.sync.dma_start(out=out[rt * P : (rt + 1) * P, c0 : c0 + width], in_=result[:, rt, c0 : c0 + width])
+        def store(g, rt):
+            nc.sync.dma_start(
+                out=out[rt * P : (rt + 1) * P, g * BH : (g + 1) * BH], in_=result[:, rt, g * BH : (g + 1) * BH]
+            )
 
-        std_mean = small.tile([P, RT, 2], F32)
+        def centre(g, rt):
+            nc.vector.scalar_tensor_tensor(
+                out=result[:, rt, g * BH : (g + 1) * BH],
+                in0=block_sums[g][rt][:],
+                scalar=mean_var[:, rt, 0:1],
+                in1=gain_bias[:, 0, (g - SCALED) * BH : (g - SCALED + 1) * BH],
+                op0=ALU.subtract,
+                op1=ALU.mult,
+            )
+
+        def finish_centred(g, rt):
+            block = result[:, rt, g * BH : (g + 1) * BH]
+            nc.vector.scalar_tensor_tensor(
+                out=block,
+                in0=block,
+                scalar=rstd[:, rt, :],
+                in1=gain_bias[:, 1, (g - SCALED) * BH : (g - SCALED + 1) * BH],
+                op0=ALU.mult,
+                op1=ALU.add,
+            )
+            nc.scalar.activation(out=block, in_=block, func=ACT.Silu)
+            store(g, rt)
+
+        def finish_scaled(g, rt):
+            total = psum.tile([P, PACK, P], F32, name="total", tag="bank")
+            nc.tensor.matmul(
+                out=total[:],
+                lhsT=row_terms[:, rt, :],
+                rhs=term_rows[:, g * BH : (g + 1) * BH].rearrange("k (q t) -> k t q", t=PACK),
+                start=True,
+                stop=False,
+            )
+            for t in range(PACK):
+                nc.tensor.matmul(
+                    out=total[:, t, :],
+                    lhsT=scaled[:, g, t, rt * P : (rt + 1) * P],
+                    rhs=ident[:],
+                    is_transpose=True,
+                    start=False,
+                    stop=t == PACK - 1,
+                )
+            nc.scalar.activation(
+                out=result[:, rt, g * BH : (g + 1) * BH].rearrange("r (q t) -> r q t", t=PACK),
+                in_=total[:].rearrange("r t q -> r q t"),
+                func=ACT.Silu,
+                scale=rstd[:, rt, :],
+            )
+            store(g, rt)
+
+        centred = [(g, rt) for g in range(n_early, G) for rt in range(RT)]
+        centre(centred[0][0], centred[0][1])
+        std_mean = small.tile([P, RT, 2], F32, name="std_mean", tag="std_mean")
         nc.vector.tensor_scalar(
             out=std_mean[:, :, 1:2], in0=mean_var[:, :, 0:1], scalar1=-1.0, scalar2=None, op0=ALU.mult
         )
+        centre(centred[1][0], centred[1][1])
+        finish_centred(centred[0][0], centred[0][1])
         nc.vector.tensor_tensor(out=std_mean[:, :, 0:1], in0=var_eps[:], in1=rstd[:], op=ALU.mult)
         nc.vector.tensor_copy(out=terms[:, :, 0:2], in_=std_mean[:])
         nc.vector.tensor_tensor(out=terms[:, :, 2:4], in0=std_mean[:], in1=terms[:, :, 0:2], op=ALU.subtract)
         terms_t = psum.tile([P, RT, P], BF16, name="terms_t", tag="bank")
         for rt in range(RT):
             nc.tensor.transpose(terms_t[:, rt, :], terms[:, rt, :], ident_bf[:])
-        row_terms = keep.tile([P, RT, P], BF16)
+        finish_centred(centred[1][0], centred[1][1])
+        row_terms = keep.tile([P, RT, P], BF16, name="row_terms", tag="row_terms")
         nc.vector.tensor_copy(out=row_terms[:], in_=terms_t[:])
-
-        def finish_scaled(g):
-            for rt in range(RT):
-                total = psum.tile([P, PACK, P], F32, name="total", tag="bank")
-                nc.tensor.matmul(
-                    out=total[:],
-                    lhsT=row_terms[:, rt, :],
-                    rhs=term_rows[:, g * BH : (g + 1) * BH].rearrange("k (q t) -> k t q", t=PACK),
-                    start=True,
-                    stop=False,
-                )
-                for t in range(PACK):
-                    nc.tensor.matmul(
-                        out=total[:, t, :],
-                        lhsT=scaled[:, g, t, rt * P : (rt + 1) * P],
-                        rhs=ident[:],
-                        is_transpose=True,
-                        start=False,
-                        stop=t == PACK - 1,
-                    )
-                nc.scalar.activation(
-                    out=result[:, rt, g * BH : (g + 1) * BH].rearrange("r (q t) -> r q t", t=PACK),
-                    in_=total[:].rearrange("r t q -> r q t"),
-                    func=ACT.Silu,
-                    scale=rstd[:, rt, :],
-                )
-                store(rt, g * BH, BH)
-
-        pieces = [(rt, g) for g in range(SCALED, G) for rt in range(RT)]
-        for k in range(len(pieces) + 1):
-            if k < len(pieces):
-                rt, g = pieces[k]
-                block = result[:, rt, g * BH : (g + 1) * BH]
-                nc.vector.scalar_tensor_tensor(
-                    out=block,
-                    in0=block if g < n_early else block_sums[g][rt][:],
-                    scalar=mean_var[:, rt, 0:1],
-                    in1=gain_bias[:, 0, (g - SCALED) * BH : (g - SCALED + 1) * BH],
-                    op0=ALU.subtract,
-                    op1=ALU.mult,
-                )
-            if k > 0:
-                rt, g = pieces[k - 1]
-                block = result[:, rt, g * BH : (g + 1) * BH]
-                nc.vector.scalar_tensor_tensor(
-                    out=block,
-                    in0=block,
-                    scalar=rstd[:, rt, :],
-                    in1=gain_bias[:, 1, (g - SCALED) * BH : (g - SCALED + 1) * BH],
-                    op0=ALU.mult,
-                    op1=ALU.add,
-                )
-                nc.scalar.activation(out=block, in_=block, func=ACT.Silu)
-                store(rt, g * BH, BH)
-            if k % 2 == 0 and k // 2 < SCALED:
-                finish_scaled(k // 2)
+        centre(centred[2][0], centred[2][1])
+        for k in range(len(centred)):
+            finish_scaled(k // RT, k % RT)
+            if k + 3 < len(centred):
+                centre(centred[k + 3][0], centred[k + 3][1])
+            if k + 2 < len(centred):
+                finish_centred(centred[k + 2][0], centred[k + 2][1])

@@ -27,10 +27,9 @@ BN_DIM = 2 * TRIPLE
 RUN = 2
 UNIT = 2
 UNITS_A, UNITS_S, UNITS_D = (1,), (1, 1), (1, 1, 2, 2, 2)
-SCALAR_COLS_1 = 448
-SCALAR_COLS_2 = 560
-SCALAR_COLS_CLOSING = 160
-SCALAR_COLS_LATE = 640
+HALF = 256
+COLS_1 = 416
+CLOSING_EVERY = 3
 LAG = 2
 CLOSING_FROM, CLOSING_TO = 6, 13
 CATCH_UP = 2 * (G - 4)
@@ -100,9 +99,9 @@ def tile_blockrecurrentmodel_pa_kernel(
             if i < n_units:
                 raws[i] = raw_pool.tile([P, weight_rows[i].shape[0] // K_PASS, PACK, HID], BF16, name="raw", tag="raw")
                 nc.sync.dma_start(out=raws[i][:], in_=weight_rows[i].rearrange("(c p j) n -> p c j n", p=P, j=PACK))
-            if i < len(row_slices):
-                slices[i] = raw_pool.tile([P, RT, row_slices[i].shape[2]], BF16, name="rows", tag="rows")
-                nc.sync.dma_start(out=slices[i][:], in_=row_slices[i])
+            if 0 < i <= len(row_slices):
+                slices[i - 1] = raw_pool.tile([P, RT, row_slices[i - 1].shape[2]], BF16, name="rows", tag="rows")
+                nc.sync.dma_start(out=slices[i - 1][:], in_=row_slices[i - 1])
             if i == len(row_slices):
                 nc.sync.dma_start(
                     out=cols_bf[:, 6:n_cols, 0:PACK],
@@ -154,22 +153,27 @@ def tile_blockrecurrentmodel_pa_kernel(
             grouped = grouped_pool.tile([P, n * HID, PACK], BF16, align_bytes=64, name="grouped", tag="grouped")
             job["grouped"] = grouped
             scalar_cols = job["scalar_cols"]
+            if scalar_cols == 0:
+                dst = grouped[:].rearrange("p (c w i) t -> p c w t i", c=n, i=RUN)
+                nc.vector.tensor_copy(out=dst, in_=raws[i][:].rearrange("p c t (w i) -> p c w t i", i=RUN))
             for c in range(n):
                 vector_cols = max(0, min(HID, n * HID - scalar_cols - c * HID))
-                if vector_cols > 0:
+                if scalar_cols > 0 and vector_cols > 0:
                     dst, src = regrouped(grouped[:, c * HID : c * HID + vector_cols], raws[i][:, c, :, :vector_cols])
                     nc.vector.tensor_copy(out=dst, in_=src)
                 if vector_cols < HID:
                     dst, src = regrouped(grouped[:, c * HID + vector_cols : (c + 1) * HID], raws[i][:, c, :, vector_cols:])
                     nc.scalar.copy(out=dst, in_=src)
-            if i in slices:
-                rows_grouped = grouped_pool.tile(
-                    [P, n * ROWS * PACK], BF16, align_bytes=64, bufs=LAG + 1, name="rows_grouped", tag="rows_grouped"
-                )
-                job["rows_grouped"] = rows_grouped
-                pairs = rows_grouped[:].bitcast(F32).rearrange("p (c r u) -> p c r u", c=n, u=2)
-                for c in range(n):
-                    nc.scalar.copy(out=pairs[:, c], in_=job["banks"][c][:].rearrange("p u r -> p r u"))
+
+        def copy_words(i):
+            job = jobs[i]
+            n = len(job["uses"])
+            job["rows_grouped"] = grouped_pool.tile(
+                [P, n * ROWS * PACK], BF16, align_bytes=64, bufs=LAG + 1, name="rows_grouped", tag="rows_grouped"
+            )
+            pairs = job["rows_grouped"][:].bitcast(F32).rearrange("p (c r u) -> p c r u", c=n, u=2)
+            for c in range(n):
+                nc.scalar.copy(out=pairs[:, c], in_=job["banks"][c][:].rearrange("p u r -> p r u"))
 
         def quantise(i):
             job = jobs[i]
@@ -182,7 +186,7 @@ def tile_blockrecurrentmodel_pa_kernel(
                 scales=w_scales[:].rearrange("p c w -> p (c w)"),
                 in_=job["grouped"][:].rearrange("p w t -> p (w t)"),
             )
-            if i in slices:
+            if job["rows_grouped"] is not None:
                 codes, scales, c0 = uses[0][0], uses[0][1], uses[0][2]
                 nc.vector.quantize_mx(
                     out=codes[:, c0 : c0 + len(uses), :].rearrange("p c r -> p (c r)").bitcast(FP8X4),
@@ -291,14 +295,15 @@ def tile_blockrecurrentmodel_pa_kernel(
                     in_=held["x_grouped"][:].rearrange("p r t -> p (r t)"),
                 )
 
-            plan(slot + 1, "A", statistics)
-            plan(slot + 2, "A", normalise)
-            plan(slot + 3, "A", gate)
-            plan(slot + 5, "A", regroup_x)
-            plan(slot + 5, "B", quantise_x)
+            start = slot + 1 if place == 2 else slot + 2
+            plan(start, "A", statistics)
+            plan(start + 1, "A", normalise)
+            plan(start + 2, "A", gate)
+            plan(start + 4, "A", regroup_x)
+            plan(start + 4, "B", quantise_x)
 
         def add_unit(sums, uses, scalar_cols, after):
-            jobs.append({"sums": sums, "uses": uses, "scalar_cols": scalar_cols, "after": after})
+            jobs.append({"rows_grouped": None, "sums": sums, "uses": uses, "scalar_cols": scalar_cols, "after": after})
 
         d_codes, d_scales = codes_and_scales(DETER // K_PASS, "d")
         for name, units, vec, place in (("a", UNITS_A, 2, 1), ("s", UNITS_S, 0, 0), ("d", UNITS_D, 4, 2)):
@@ -313,7 +318,7 @@ def tile_blockrecurrentmodel_pa_kernel(
                 add_unit(
                     sums,
                     [(codes, scales, c, c == 0, c == passes - 1) for c in cs],
-                    SCALAR_COLS_1 * len(cs) // UNIT,
+                    COLS_1 if n == UNIT else HALF,
                     after,
                 )
 
@@ -384,9 +389,9 @@ def tile_blockrecurrentmodel_pa_kernel(
                 plan(slot + 1, "A", early)
                 plan(slot + 2, "A", variance)
             elif g in SCALAR_STATS:
-                plan(slot + 1, "B", by_scalar)
+                plan(slot + 2, "A", by_scalar)
             else:
-                plan(slot + 1, "B", late)
+                plan(slot + 2 if g < G - 1 else slot + 1, "A", late)
 
         block_sums = []
         j = 0
@@ -395,30 +400,30 @@ def tile_blockrecurrentmodel_pa_kernel(
             uses = [(d_codes, d_scales, g, True, False)]
             uses += [(x_codes, x_scales, c, False, c == 2) for c in range(3)]
             for u, n in enumerate(block_units[g]):
-                if j < CLOSING_FROM:
-                    cols2 = SCALAR_COLS_2
-                elif j < CLOSING_TO:
-                    cols2 = SCALAR_COLS_CLOSING
+                if n == 1:
+                    cols2 = HALF
+                elif CLOSING_FROM <= j < CLOSING_TO and j % CLOSING_EVERY != 0:
+                    cols2 = 0
                 else:
-                    cols2 = SCALAR_COLS_LATE
+                    cols2 = HID
                 last = u == len(block_units[g]) - 1
-                add_unit(block_sums[g], uses[:n], cols2 * n // UNIT, partial(close_block, g) if last else None)
+                add_unit(block_sums[g], uses[:n], cols2, partial(close_block, g) if last else None)
                 uses = uses[n:]
                 j += 1
 
         n_stage_1 = len(row_slices)
-        plan(LAG + 1, "A", partial(widen, 0, 6))
+        plan(LAG + 2, "A", partial(widen, 0, 6))
         plan(n_stage_1 + LAG, "A", partial(widen, 6, n_cols))
         done = n_stage_1
-        for slot in range(n_units + LAG + 2):
+        for slot in range(n_units + LAG + 3):
             if slot < n_units + 1:
                 load_unit(slot + AHEAD)
-            if slot == 0:
-                jobs[0]["banks"] = transpose_rows(slices[0])
             if slot < n_units:
                 regroup(slot)
-            if slot + 1 < n_stage_1:
-                jobs[slot + 1]["banks"] = transpose_rows(slices[slot + 1])
+            if 0 < slot <= n_stage_1:
+                copy_words(slot - 1)
+            if slot < n_stage_1:
+                jobs[slot]["banks"] = transpose_rows(slices[slot])
             work_off(slot, "A")
             if 0 <= slot - LAG < n_units:
                 quantise(slot - LAG)
@@ -437,10 +442,9 @@ def tile_blockrecurrentmodel_pa_kernel(
             nc.vector.bn_aggr(out=mean_var[:, rt, :], in_=stats[:, rt].rearrange("p n v -> p (n v)"))
         var_eps, rstd = inverse_std(mean_var)
 
-        def store(g, rt):
-            nc.sync.dma_start(
-                out=out[rt * P : (rt + 1) * P, g * BH : (g + 1) * BH], in_=result[:, rt, g * BH : (g + 1) * BH]
-            )
+        def store(g, rt, blocks=1):
+            cols_out = slice(g * BH, (g + blocks) * BH)
+            nc.sync.dma_start(out=out[rt * P : (rt + 1) * P, cols_out], in_=result[:, rt, cols_out])
 
         def centre(g, rt):
             nc.vector.scalar_tensor_tensor(
@@ -452,18 +456,18 @@ def tile_blockrecurrentmodel_pa_kernel(
                 op1=ALU.mult,
             )
 
-        def finish_centred(g, rt):
-            block = result[:, rt, g * BH : (g + 1) * BH]
+        def finish_centred(g, rt, blocks):
+            piece = result[:, rt, g * BH : (g + blocks) * BH]
             nc.vector.scalar_tensor_tensor(
-                out=block,
-                in0=block,
+                out=piece,
+                in0=piece,
                 scalar=rstd[:, rt, :],
-                in1=gain_bias[:, 1, (g - SCALED) * BH : (g - SCALED + 1) * BH],
+                in1=gain_bias[:, 1, (g - SCALED) * BH : (g - SCALED + blocks) * BH],
                 op0=ALU.mult,
                 op1=ALU.add,
             )
-            nc.scalar.activation(out=block, in_=block, func=ACT.Silu)
-            store(g, rt)
+            nc.scalar.activation(out=piece, in_=piece, func=ACT.Silu)
+            store(g, rt, blocks)
 
         def finish_scaled(g, rt):
             total = psum.tile([P, PACK, P], F32, name="total", tag="bank")
@@ -491,27 +495,31 @@ def tile_blockrecurrentmodel_pa_kernel(
             )
             store(g, rt)
 
-        centred = [(g, rt) for g in range(n_early, G) for rt in range(RT)]
-        centre(centred[0][0], centred[0][1])
+        centre(4, 0)
         std_mean = small.tile([P, RT, 2], F32, name="std_mean", tag="std_mean")
         nc.vector.tensor_scalar(
             out=std_mean[:, :, 1:2], in0=mean_var[:, :, 0:1], scalar1=-1.0, scalar2=None, op0=ALU.mult
         )
-        centre(centred[1][0], centred[1][1])
-        finish_centred(centred[0][0], centred[0][1])
+        centre(5, 0)
+        finish_centred(4, 0, 1)
         nc.vector.tensor_tensor(out=std_mean[:, :, 0:1], in0=var_eps[:], in1=rstd[:], op=ALU.mult)
         nc.vector.tensor_copy(out=terms[:, :, 0:2], in_=std_mean[:])
         nc.vector.tensor_tensor(out=terms[:, :, 2:4], in0=std_mean[:], in1=terms[:, :, 0:2], op=ALU.subtract)
         terms_t = psum.tile([P, RT, P], BF16, name="terms_t", tag="bank")
         for rt in range(RT):
             nc.tensor.transpose(terms_t[:, rt, :], terms[:, rt, :], ident_bf[:])
-        finish_centred(centred[1][0], centred[1][1])
+        finish_centred(5, 0, 1)
         row_terms = keep.tile([P, RT, P], BF16, name="row_terms", tag="row_terms")
         nc.vector.tensor_copy(out=row_terms[:], in_=terms_t[:])
-        centre(centred[2][0], centred[2][1])
-        for k in range(len(centred)):
-            finish_scaled(k // RT, k % RT)
-            if k + 3 < len(centred):
-                centre(centred[k + 3][0], centred[k + 3][1])
-            if k + 2 < len(centred):
-                finish_centred(centred[k + 2][0], centred[k + 2][1])
+        finish_scaled(0, 0)
+        finish_scaled(0, 1)
+        for k, (g, rt) in enumerate(((6, 0), (4, 1), (6, 1))):
+            centre(g, rt)
+            centre(g + 1, rt)
+            if k < 2:
+                finish_centred(g, rt, 2)
+            else:
+                finish_centred(g, rt, 1)
+                finish_centred(g + 1, rt, 1)
+            finish_scaled(1 + k, 0)
+            finish_scaled(1 + k, 1)

@@ -30,9 +30,9 @@ UNITS_A, UNITS_S, UNITS_D = (1,), (1, 1), (1, 1, 2, 2, 2)
 HALF = 256
 COLS_1 = 416
 CLOSING_EVERY = 3
+SHORT_LAG = 4
 LAG = 2
-CLOSING_FROM, CLOSING_TO = 6, 13
-CATCH_UP = 2 * (G - 4)
+CLOSING_FROM, CLOSING_TO = 7, 14
 X_SLOTS = 6
 AHEAD = 3
 KEPT = 4
@@ -303,7 +303,7 @@ def tile_blockrecurrentmodel_pa_kernel(
             plan(start + 4, "B", quantise_x)
 
         def add_unit(sums, uses, scalar_cols, after):
-            jobs.append({"rows_grouped": None, "sums": sums, "uses": uses, "scalar_cols": scalar_cols, "after": after})
+            jobs.append({"meets_d": any(use[0] is x_codes and use[2] == 2 for use in uses), "rows_grouped": None, "sums": sums, "uses": uses, "scalar_cols": scalar_cols, "after": after})
 
         d_codes, d_scales = codes_and_scales(DETER // K_PASS, "d")
         for name, units, vec, place in (("a", UNITS_A, 2, 1), ("s", UNITS_S, 0, 0), ("d", UNITS_D, 4, 2)):
@@ -386,8 +386,9 @@ def tile_blockrecurrentmodel_pa_kernel(
                     squared(block_sums[g][rt][:], rt)
 
             if g < n_early:
-                plan(slot + 1, "A", early)
-                plan(slot + 2, "A", variance)
+                start = max(slot + 1, len(row_slices) + X_SLOTS + 1 + 2 * g)
+                plan(start, "A", early)
+                plan(start + 1, "A", variance)
             elif g in SCALAR_STATS:
                 plan(slot + 2, "A", by_scalar)
             else:
@@ -414,7 +415,8 @@ def tile_blockrecurrentmodel_pa_kernel(
         n_stage_1 = len(row_slices)
         plan(LAG + 2, "A", partial(widen, 0, 6))
         plan(n_stage_1 + LAG, "A", partial(widen, 6, n_cols))
-        done = n_stage_1
+        unquantised = list(range(n_units))
+        unmultiplied = list(range(n_stage_1, n_units))
         for slot in range(n_units + LAG + 3):
             if slot < n_units + 1:
                 load_unit(slot + AHEAD)
@@ -425,17 +427,16 @@ def tile_blockrecurrentmodel_pa_kernel(
             if slot < n_stage_1:
                 jobs[slot]["banks"] = transpose_rows(slices[slot])
             work_off(slot, "A")
-            if 0 <= slot - LAG < n_units:
-                quantise(slot - LAG)
+            for i in [i for i in unquantised if i + (LAG if i < n_units - SHORT_LAG else 1) <= slot]:
+                quantise(i)
+                unquantised.remove(i)
             work_off(slot, "B")
             if 0 <= slot - LAG < n_stage_1:
                 multiply(slot - LAG, slot)
-            for i in (done, done + 1):
-                if i > done and i < n_stage_1 + CATCH_UP:
-                    continue
-                if n_stage_1 <= i <= min(slot - LAG, n_units - 1) and (i == n_stage_1 or slot >= n_stage_1 + X_SLOTS):
-                    multiply(i, slot)
-                    done = i + 1
+            ready = [i for i in unmultiplied if i not in unquantised and (slot >= n_stage_1 + X_SLOTS or not jobs[i]["meets_d"])]
+            for i in ready[:2]:
+                multiply(i, slot)
+                unmultiplied.remove(i)
 
         mean_var = small.tile([P, RT, 2], F32, name="mean_var", tag="mean_var")
         for rt in range(RT):
@@ -469,24 +470,30 @@ def tile_blockrecurrentmodel_pa_kernel(
             nc.scalar.activation(out=piece, in_=piece, func=ACT.Silu)
             store(g, rt, blocks)
 
-        def finish_scaled(g, rt):
+        totals = {}
+
+        def turn_back(g, rt):
             total = psum.tile([P, PACK, P], F32, name="total", tag="bank")
-            nc.tensor.matmul(
-                out=total[:],
-                lhsT=row_terms[:, rt, :],
-                rhs=term_rows[:, g * BH : (g + 1) * BH].rearrange("k (q t) -> k t q", t=PACK),
-                start=True,
-                stop=False,
-            )
+            totals[(g, rt)] = total
             for t in range(PACK):
                 nc.tensor.matmul(
                     out=total[:, t, :],
                     lhsT=scaled[:, g, t, rt * P : (rt + 1) * P],
                     rhs=ident[:],
                     is_transpose=True,
-                    start=False,
-                    stop=t == PACK - 1,
+                    start=t == 0,
+                    stop=False,
                 )
+
+        def finish_scaled(g, rt):
+            total = totals[(g, rt)]
+            nc.tensor.matmul(
+                out=total[:],
+                lhsT=row_terms[:, rt, :],
+                rhs=term_rows[:, g * BH : (g + 1) * BH].rearrange("k (q t) -> k t q", t=PACK),
+                start=False,
+                stop=True,
+            )
             nc.scalar.activation(
                 out=result[:, rt, g * BH : (g + 1) * BH].rearrange("r (q t) -> r q t", t=PACK),
                 in_=total[:].rearrange("r t q -> r q t"),
@@ -501,6 +508,7 @@ def tile_blockrecurrentmodel_pa_kernel(
             out=std_mean[:, :, 1:2], in0=mean_var[:, :, 0:1], scalar1=-1.0, scalar2=None, op0=ALU.mult
         )
         centre(5, 0)
+        turn_back(0, 0)
         finish_centred(4, 0, 1)
         nc.vector.tensor_tensor(out=std_mean[:, :, 0:1], in0=var_eps[:], in1=rstd[:], op=ALU.mult)
         nc.vector.tensor_copy(out=terms[:, :, 0:2], in_=std_mean[:])
@@ -508,18 +516,28 @@ def tile_blockrecurrentmodel_pa_kernel(
         terms_t = psum.tile([P, RT, P], BF16, name="terms_t", tag="bank")
         for rt in range(RT):
             nc.tensor.transpose(terms_t[:, rt, :], terms[:, rt, :], ident_bf[:])
+        centre(6, 0)
+        turn_back(0, 1)
         finish_centred(5, 0, 1)
         row_terms = keep.tile([P, RT, P], BF16, name="row_terms", tag="row_terms")
         nc.vector.tensor_copy(out=row_terms[:], in_=terms_t[:])
         finish_scaled(0, 0)
+        centre(7, 0)
+        turn_back(1, 0)
         finish_scaled(0, 1)
-        for k, (g, rt) in enumerate(((6, 0), (4, 1), (6, 1))):
+        finish_centred(6, 0, 2)
+        for k, (g, rt) in enumerate(((4, 1), (6, 1))):
             centre(g, rt)
+            turn_back(1 + k, 1)
+            finish_scaled(1 + k, 0)
             centre(g + 1, rt)
-            if k < 2:
+            turn_back(2 + k, 0)
+            finish_scaled(1 + k, 1)
+            if k == 0:
                 finish_centred(g, rt, 2)
             else:
+                turn_back(3, 1)
                 finish_centred(g, rt, 1)
+                finish_scaled(3, 0)
                 finish_centred(g + 1, rt, 1)
-            finish_scaled(1 + k, 0)
-            finish_scaled(1 + k, 1)
+                finish_scaled(3, 1)

@@ -30,13 +30,13 @@ UNITS_A, UNITS_S, UNITS_D = (1,), (1, 1), (1, 1, 2, 2, 2)
 HALF = 256
 COLS_1 = 416
 CLOSING_EVERY = 3
-SHORT_LAG = 4
+SHORT_LAG = 6
 LAG = 2
 CLOSING_FROM, CLOSING_TO = 7, 14
 X_SLOTS = 6
 AHEAD = 3
 KEPT = 4
-SCALAR_STATS = (6,)
+SCALAR_STATS = (5, 6)
 SCALED = 4
 
 FLOPS = 2 * ROWS * ((STOCH + ACTION + DETER) * HID + G * (BH + 3 * HID) * BH)
@@ -119,7 +119,7 @@ def tile_blockrecurrentmodel_pa_kernel(
             nc.sync.dma_start(out=cols_bf[:, i, 0:PACK], in_=vec.rearrange("(q t) -> q t", t=PACK))
 
         def widen(first, last):
-            nc.vector.tensor_copy(out=cols[:, first:last, :], in_=cols_bf[:, first:last, 0:PACK])
+            nc.gpsimd.tensor_copy(out=cols[:, first:last, :], in_=cols_bf[:, first:last, 0:PACK])
 
         def regrouped(dst, src):
             return dst.rearrange("p (c i) t -> p c t i", i=RUN), src.rearrange("p t (c i) -> p c t i", i=RUN)
@@ -215,9 +215,9 @@ def tile_blockrecurrentmodel_pa_kernel(
             if job["after"] is not None:
                 job["after"](slot)
 
-        def inverse_std(mean_var):
+        def inverse_std(mean_var, engine):
             var_eps = small.tile([P, RT, 1], F32, name="var_eps", tag="var_eps")
-            nc.vector.tensor_scalar(out=var_eps[:], in0=mean_var[:, :, 1:2], scalar1=EPS, scalar2=None, op0=ALU.add)
+            engine.tensor_scalar(out=var_eps[:], in0=mean_var[:, :, 1:2], scalar1=EPS, scalar2=None, op0=ALU.add)
             rstd = small.tile([P, RT, 1], F32, name="rstd", tag="rstd")
             nc.gpsimd.tensor_tensor(out=rstd[:], in0=var_eps[:], in1=minus_half[:], op=ALU.pow)
             return var_eps, rstd
@@ -260,7 +260,7 @@ def tile_blockrecurrentmodel_pa_kernel(
                 for rt in range(RT):
                     nc.vector.bn_aggr(out=mean_var[:, rt, :], in_=stats[:, rt, :])
                 held["mean_var"] = mean_var
-                held["rstd"] = inverse_std(mean_var)[1]
+                held["rstd"] = inverse_std(mean_var, nc.gpsimd)[1]
 
             def normalise():
                 shift = small.tile([P, RT, 1], F32, name="shift", tag="shift")
@@ -441,7 +441,7 @@ def tile_blockrecurrentmodel_pa_kernel(
         mean_var = small.tile([P, RT, 2], F32, name="mean_var", tag="mean_var")
         for rt in range(RT):
             nc.vector.bn_aggr(out=mean_var[:, rt, :], in_=stats[:, rt].rearrange("p n v -> p (n v)"))
-        var_eps, rstd = inverse_std(mean_var)
+        var_eps, rstd = inverse_std(mean_var, nc.vector)
 
         def store(g, rt, blocks=1):
             cols_out = slice(g * BH, (g + blocks) * BH)

from contextlib import ExitStack
from functools import partial

import concourse.mybir as mybir
from concourse.masks import make_identity

F32 = mybir.dt.float32
BF16 = mybir.dt.bfloat16
U32 = mybir.dt.uint32
U8 = mybir.dt.uint8
FP8X4 = mybir.dt.float8_e4m3fn_x4
ALU = mybir.AluOpType
ACT = mybir.ActivationFunctionType

P = 128
PACK = 4
K_PASS = P * PACK
ROWS = 256
RT = ROWS // P
STOCH, ACTION, HID, DETER, G = 1024, 512, 512, 4096, 8
BH = DETER // G
BLK_PASSES = (BH + 3 * HID) // K_PASS
EPS = 1e-3
TRIPLE = 3
BN_DIM = 2 * TRIPLE

RUN = 2
UNIT = 2
UNITS_A, UNITS_S, UNITS_D = (1,), (1, 1), (1, 1, 2, 2, 2)
HALF = 256
COLS_1 = 416
CLOSING_EVERY = 3
SHORT_LAG = 6
LAG = 2
CLOSING_FROM, CLOSING_TO = 7, 14
X_SLOTS = 6
AHEAD = 3
KEPT = 4
SCALAR_STATS = (5, 6)
SCALED = 4

FLOPS = 2 * ROWS * ((STOCH + ACTION + DETER) * HID + G * (BH + 3 * HID) * BH)


def tile_blockrecurrentmodel_pa_kernel(
    tc, s, a, d, W_s, W_a, W_d, ln_s_g, ln_s_b, ln_a_g, ln_a_b, ln_d_g, ln_d_b, W_hid, ln_h_g, ln_h_b, out
):
    nc = tc.nc
    with ExitStack() as ctx:
        const = ctx.enter_context(tc.tile_pool(name="const", bufs=1))
        keep = ctx.enter_context(tc.tile_pool(name="keep", bufs=1))
        raw_pool = ctx.enter_context(tc.tile_pool(name="raw", bufs=AHEAD + 1))
        grouped_pool = ctx.enter_context(tc.tile_pool(name="grouped", bufs=LAG + 3))
        quantised_pool = ctx.enter_context(tc.tile_pool(name="quantised", bufs=6))
        norm_pool = ctx.enter_context(tc.tile_pool(name="norm", bufs=3))
        small = ctx.enter_context(tc.tile_pool(name="small", bufs=4))
        psum = ctx.enter_context(tc.psum_pool(name="psum", bufs=8))
        ctx.enter_context(tc.manual_schedule())

        ident = const.tile([P, P], F32)
        make_identity(nc, ident[:])
        ident_bf = const.tile([P, P], BF16)
        make_identity(nc, ident_bf[:])
        minus_half = const.tile([P, RT, 1], F32)
        nc.vector.memset(minus_half[:], -0.5)

        weight_rows = []
        row_slices = []
        for x, w, passes in ((a, W_a, UNITS_A), (s, W_s, UNITS_S), (d, W_d, UNITS_D)):
            x_rows = x.flatten_outer_dims().rearrange("(rt p) k -> p rt k", p=P)
            k0 = 0
            for n in passes:
                k1 = k0 + n * K_PASS
                weight_rows.append(w[k0:k1, :])
                row_slices.append(x_rows[:, :, k0:k1])
                k0 = k1
        block_units = [(UNIT, UNIT)] * (G - 1) + [(UNIT, 1, 1)]
        for g in range(G):
            k0 = 0
            for n in block_units[g]:
                weight_rows.append(W_hid[g, k0 : k0 + n * K_PASS, :])
                k0 += n * K_PASS
        n_units = len(weight_rows)

        first_plain = SCALED * BH
        n_cols = 6 + SCALED
        cols_bf = const.tile([P, n_cols, 16], BF16)
        cols = const.tile([P, n_cols, PACK], F32)
        gain_bias = keep.tile([P, 2, DETER - first_plain], BF16)
        term_rows = keep.tile([P, first_plain], BF16)
        nc.gpsimd.memset(term_rows[:], 0.0)
        terms = keep.tile([P, RT, P], BF16)
        nc.gpsimd.memset(terms[:], 0.0)

        raws = {}
        slices = {}

        def load_unit(i):
            if i < n_units:
                raws[i] = raw_pool.tile([P, weight_rows[i].shape[0] // K_PASS, PACK, HID], BF16, name="raw", tag="raw")
                nc.sync.dma_start(out=raws[i][:], in_=weight_rows[i].rearrange("(c p j) n -> p c j n", p=P, j=PACK))
            if 0 < i <= len(row_slices):
                slices[i - 1] = raw_pool.tile([P, RT, row_slices[i - 1].shape[2]], BF16, name="rows", tag="rows")
                nc.sync.dma_start(out=slices[i - 1][:], in_=row_slices[i - 1])
            if i == len(row_slices):
                nc.sync.dma_start(
                    out=cols_bf[:, 6:n_cols, 0:PACK],
                    in_=ln_h_g[0:first_plain].rearrange("(g q t) -> q g t", q=P, t=PACK),
                )
            if i == n_units:
                for v, vec in enumerate((ln_h_g, ln_h_b)):
                    nc.sync.dma_start(out=gain_bias[:, v, :], in_=vec[first_plain:DETER].partition_broadcast(P))
                for row, vec in enumerate((ln_h_b, ln_h_g, ln_h_b, ln_h_g)):
                    nc.sync.dma_start(out=term_rows[row : row + 1, :], in_=vec[0:first_plain].unsqueeze(0))

        for i in range(AHEAD):
            load_unit(i)
        for i, vec in enumerate((ln_s_g, ln_s_b, ln_a_g, ln_a_b, ln_d_g, ln_d_b)):
            nc.sync.dma_start(out=cols_bf[:, i, 0:PACK], in_=vec.rearrange("(q t) -> q t", t=PACK))

        def widen(first, last):
            nc.gpsimd.tensor_copy(out=cols[:, first:last, :], in_=cols_bf[:, first:last, 0:PACK])

        def regrouped(dst, src):
            return dst.rearrange("p (c i) t -> p c t i", i=RUN), src.rearrange("p t (c i) -> p c t i", i=RUN)

        def transpose_rows(rows):
            banks = []
            for c in range(rows.shape[2] // K_PASS):
                planes = psum.tile([P, 2, ROWS], F32, name="planes", tag="bank")
                for rt in range(RT):
                    words = rows[:, rt, c * K_PASS : (c + 1) * K_PASS].bitcast(F32)
                    words = words.rearrange("p (q u) -> p u q", u=2)
                    for u in range(2):
                        nc.tensor.transpose(planes[:, u, rt * P : (rt + 1) * P], words[:, u, :], ident[:])
                banks.append(planes)
            return banks

        agenda = {}

        def plan(slot, point, step):
            agenda.setdefault((slot, point), []).append(step)

        def work_off(slot, point):
            for step in agenda.get((slot, point), []):
                step()

        jobs = []

        def regroup(i):
            job = jobs[i]
            n = len(job["uses"])
            grouped = grouped_pool.tile([P, n * HID, PACK], BF16, align_bytes=64, name="grouped", tag="grouped")
            job["grouped"] = grouped
            scalar_cols = job["scalar_cols"]
            if scalar_cols == 0:
                dst = grouped[:].rearrange("p (c w i) t -> p c w t i", c=n, i=RUN)
                nc.vector.tensor_copy(out=dst, in_=raws[i][:].rearrange("p c t (w i) -> p c w t i", i=RUN))
            for c in range(n):
                vector_cols = max(0, min(HID, n * HID - scalar_cols - c * HID))
                if scalar_cols > 0 and vector_cols > 0:
                    dst, src = regrouped(grouped[:, c * HID : c * HID + vector_cols], raws[i][:, c, :, :vector_cols])
                    nc.vector.tensor_copy(out=dst, in_=src)
                if vector_cols < HID:
                    dst, src = regrouped(grouped[:, c * HID + vector_cols : (c + 1) * HID], raws[i][:, c, :, vector_cols:])
                    nc.scalar.copy(out=dst, in_=src)

        def copy_words(i):
            job = jobs[i]
            n = len(job["uses"])
            job["rows_grouped"] = grouped_pool.tile(
                [P, n * ROWS * PACK], BF16, align_bytes=64, bufs=LAG + 1, name="rows_grouped", tag="rows_grouped"
            )
            pairs = job["rows_grouped"][:].bitcast(F32).rearrange("p (c r u) -> p c r u", c=n, u=2)
            for c in range(n):
                nc.scalar.copy(out=pairs[:, c], in_=job["banks"][c][:].rearrange("p u r -> p r u"))

        def quantise(i):
            job = jobs[i]
            uses = job["uses"]
            w_codes = quantised_pool.tile([P, len(uses), HID], U32, align_bytes=64, name="w_codes", tag="w_codes")
            w_scales = quantised_pool.tile([P, len(uses), HID], U8, align_bytes=64, name="w_scales", tag="w_scales")
            job["w"] = (w_codes, w_scales)
            nc.vector.quantize_mx(
                out=w_codes[:].rearrange("p c w -> p (c w)").bitcast(FP8X4),
                scales=w_scales[:].rearrange("p c w -> p (c w)"),
                in_=job["grouped"][:].rearrange("p w t -> p (w t)"),
            )
            if job["rows_grouped"] is not None:
                codes, scales, c0 = uses[0][0], uses[0][1], uses[0][2]
                nc.vector.quantize_mx(
                    out=codes[:, c0 : c0 + len(uses), :].rearrange("p c r -> p (c r)").bitcast(FP8X4),
                    scales=scales[:, c0 : c0 + len(uses), :].rearrange("p c r -> p (c r)"),
                    in_=job["rows_grouped"][:],
                )

        def multiply(i, slot):
            job = jobs[i]
            w_codes, w_scales = job["w"]
            for n, (codes, scales, c, start, stop) in enumerate(job["uses"]):
                if start:
                    for rt in range(RT):
                        job["sums"].append(psum.tile([P, HID], F32, name="sums%d" % rt, tag="bank"))
                for rt in range(RT):
                    r = slice(rt * P, (rt + 1) * P)
                    nc.tensor.matmul_mx(
                        out=job["sums"][rt][:],
                        lhsT=codes[:, c, r].bitcast(FP8X4),
                        lhsT_scale=scales[:, c, r],
                        rhs=w_codes[:, n, :].bitcast(FP8X4),
                        rhs_scale=w_scales[:, n, :],
                        start=start,
                        stop=stop,
                    )
            if job["after"] is not None:
                job["after"](slot)

        def inverse_std(mean_var, engine):
            var_eps = small.tile([P, RT, 1], F32, name="var_eps", tag="var_eps")
            engine.tensor_scalar(out=var_eps[:], in0=mean_var[:, :, 1:2], scalar1=EPS, scalar2=None, op0=ALU.add)
            rstd = small.tile([P, RT, 1], F32, name="rstd", tag="rstd")
            nc.gpsimd.tensor_tensor(out=rstd[:], in0=var_eps[:], in1=minus_half[:], op=ALU.pow)
            return var_eps, rstd

        def turn(planes):
            banks = []
            for half in range(2):
                z_t = psum.tile([P, 2, ROWS], F32, name="z_t", tag="bank")
                for i in range(2):
                    for rt in range(RT):
                        nc.tensor.transpose(z_t[:, i, rt * P : (rt + 1) * P], planes[rt][:, 2 * half + i, :], ident[:])
                banks.append(z_t)
            return banks

        def turned_out(banks, out, func, vec):
            for t in range(PACK):
                nc.scalar.activation(
                    out=out[:, t, :],
                    in_=banks[t // 2][:, t % 2, :],
                    func=func,
                    bias=cols[:, vec + 1, t : t + 1] if func == ACT.Silu else 0.0,
                    scale=cols[:, vec, t : t + 1],
                )

        def codes_and_scales(passes, name):
            codes = keep.tile([P, passes, ROWS], U32, align_bytes=64, name=name + "_codes")
            scales = keep.tile([P, passes, ROWS], U8, align_bytes=64, name=name + "_scales")
            return codes, scales

        x_codes, x_scales = codes_and_scales(3, "x")

        def embedding_norm(sums, vec, place, slot):
            held = {}

            def statistics():
                stats = small.tile([P, RT, BN_DIM], F32, name="emb_stats", tag="emb_stats")
                mean_var = small.tile([P, RT, 2], F32, name="emb_mean_var", tag="emb_mean_var")
                for rt in range(RT):
                    nc.vector.bn_stats(out=stats[:, rt, :], in_=sums[rt][:])
                for rt in range(RT):
                    nc.vector.bn_aggr(out=mean_var[:, rt, :], in_=stats[:, rt, :])
                held["mean_var"] = mean_var
                held["rstd"] = inverse_std(mean_var, nc.gpsimd)[1]

            def normalise():
                shift = small.tile([P, RT, 1], F32, name="shift", tag="shift")
                nc.vector.scalar_tensor_tensor(
                    out=shift[:], in0=held["mean_var"][:, :, 0:1], scalar=-1.0, in1=held["rstd"][:], op0=ALU.mult, op1=ALU.mult
                )
                z = []
                for rt in range(RT):
                    z.append(norm_pool.tile([P, PACK, P], F32, name="z%d" % rt, tag="z", bufs=4))
                    nc.scalar.activation(
                        out=z[rt][:],
                        in_=sums[rt][:].rearrange("r (q t) -> r t q", t=PACK),
                        func=ACT.Identity,
                        bias=shift[:, rt, :],
                        scale=held["rstd"][:, rt, :],
                    )
                held["banks"] = turn(z)

            def gate():
                held["x_planes"] = norm_pool.tile([P, PACK, ROWS], BF16, bufs=2, name="x_planes", tag="x_planes")
                turned_out(held["banks"], held["x_planes"], ACT.Silu, vec)

            def regroup_x():
                held["x_grouped"] = norm_pool.tile([P, ROWS, PACK], BF16, align_bytes=64, bufs=2, name="x_grouped", tag="x_grouped")
                dst, src = regrouped(held["x_grouped"][:], held["x_planes"][:])
                nc.vector.tensor_copy(out=dst, in_=src)

            def quantise_x():
                nc.vector.quantize_mx(
                    out=x_codes[:, place, :].bitcast(FP8X4),
                    scales=x_scales[:, place, :],
                    in_=held["x_grouped"][:].rearrange("p r t -> p (r t)"),
                )

            start = slot + 1 if place == 2 else slot + 2
            plan(start, "A", statistics)
            plan(start + 1, "A", normalise)
            plan(start + 2, "A", gate)
            plan(start + 4, "A", regroup_x)
            plan(start + 4, "B", quantise_x)

        def add_unit(sums, uses, scalar_cols, after):
            jobs.append({"meets_d": any(use[0] is x_codes and use[2] == 2 for use in uses), "rows_grouped": None, "sums": sums, "uses": uses, "scalar_cols": scalar_cols, "after": after})

        d_codes, d_scales = codes_and_scales(DETER // K_PASS, "d")
        for name, units, vec, place in (("a", UNITS_A, 2, 1), ("s", UNITS_S, 0, 0), ("d", UNITS_D, 4, 2)):
            passes = sum(units)
            c0 = 0
            codes, scales = (d_codes, d_scales) if name == "d" else codes_and_scales(passes, name)
            sums = []
            for n in units:
                cs = range(c0, c0 + n)
                c0 += n
                after = partial(embedding_norm, sums, vec, place) if cs[-1] == passes - 1 else None
                add_unit(
                    sums,
                    [(codes, scales, c, c == 0, c == passes - 1) for c in cs],
                    COLS_1 if n == UNIT else HALF,
                    after,
                )

        result = keep.tile([P, RT, DETER], F32)
        scaled = keep.tile([P, SCALED, PACK, ROWS], F32)
        n_early = G - KEPT
        by_scalar_too = [g for g in range(G) if g < n_early or g in SCALAR_STATS]
        n_single = len(by_scalar_too)
        triples = {}
        for g in range(G):
            triples[g] = by_scalar_too.index(g) if g in by_scalar_too else n_single + 2 * (g - sum(b < g for b in by_scalar_too))
        stats = keep.tile([P, RT, n_single + 2 * (G - n_single), TRIPLE], F32)
        nc.vector.memset(stats[:, :, 0:n_single, 0:1], float(BH))

        def close_block(g, slot):
            held = {}

            def squared(block, rt):
                squares = norm_pool.tile([P, BH], BF16, name="squares", tag="squares", bufs=2)
                nc.scalar.activation(
                    out=squares[:],
                    in_=block,
                    func=ACT.Square,
                    scale=-1.0,
                    bias=stats[:, rt, triples[g], 1:2],
                    accum_out=stats[:, rt, triples[g], 2:3],
                )

            def early():
                total = small.tile([P, RT, 1], F32, name="total", tag="total")
                planes = []
                for rt in range(RT):
                    block = result[:, rt, g * BH : (g + 1) * BH].rearrange("r (t q) -> r t q", t=PACK)
                    planes.append(block)
                    nc.scalar.activation(
                        out=block,
                        in_=block_sums[g][rt][:].rearrange("r (q t) -> r t q", t=PACK),
                        func=ACT.Identity,
                        accum_out=total[:, rt, :],
                    )
                nc.scalar.activation(out=stats[:, :, triples[g], 1:2], in_=total[:], func=ACT.Copy, scale=1.0 / BH)
                held["banks"] = turn(planes)

            def variance():
                for rt in range(RT):
                    squared(result[:, rt, g * BH : (g + 1) * BH], rt)
                turned_out(held["banks"], scaled[:, g], ACT.Copy, 6 + g)

            def late():
                for rt in range(RT):
                    nc.vector.bn_stats(
                        out=stats[:, rt, triples[g] : triples[g] + 2, :].rearrange("p n v -> p (n v)"),
                        in_=block_sums[g][rt][:],
                    )

            def by_scalar():
                total = small.tile([P, RT, 1], F32, name="total", tag="total")
                for rt in range(RT):
                    copy = norm_pool.tile([P, BH], BF16, name="squares", tag="squares", bufs=2)
                    nc.scalar.activation(
                        out=copy[:], in_=block_sums[g][rt][:], func=ACT.Identity, accum_out=total[:, rt, :]
                    )
                nc.scalar.activation(out=stats[:, :, triples[g], 1:2], in_=total[:], func=ACT.Copy, scale=1.0 / BH)
                for rt in range(RT):
                    squared(block_sums[g][rt][:], rt)

            if g < n_early:
                start = max(slot + 1, len(row_slices) + X_SLOTS + 1 + 2 * g)
                plan(start, "A", early)
                plan(start + 1, "A", variance)
            elif g in SCALAR_STATS:
                plan(slot + 2, "A", by_scalar)
            else:
                plan(slot + 2 if g < G - 1 else slot + 1, "A", late)

        block_sums = []
        j = 0
        for g in range(G):
            block_sums.append([])
            uses = [(d_codes, d_scales, g, True, False)]
            uses += [(x_codes, x_scales, c, False, c == 2) for c in range(3)]
            for u, n in enumerate(block_units[g]):
                if n == 1:
                    cols2 = HALF
                elif CLOSING_FROM <= j < CLOSING_TO and j % CLOSING_EVERY != 0:
                    cols2 = 0
                else:
                    cols2 = HID
                last = u == len(block_units[g]) - 1
                add_unit(block_sums[g], uses[:n], cols2, partial(close_block, g) if last else None)
                uses = uses[n:]
                j += 1

        n_stage_1 = len(row_slices)
        plan(LAG + 2, "A", partial(widen, 0, 6))
        plan(n_stage_1 + LAG, "A", partial(widen, 6, n_cols))
        unquantised = list(range(n_units))
        unmultiplied = list(range(n_stage_1, n_units))
        for slot in range(n_units + LAG + 3):
            if slot < n_units + 1:
                load_unit(slot + AHEAD)
            if slot < n_units:
                regroup(slot)
            if 0 < slot <= n_stage_1:
                copy_words(slot - 1)
            if slot < n_stage_1:
                jobs[slot]["banks"] = transpose_rows(slices[slot])
            work_off(slot, "A")
            for i in [i for i in unquantised if i + (LAG if i < n_units - SHORT_LAG else 1) <= slot]:
                quantise(i)
                unquantised.remove(i)
            work_off(slot, "B")
            if 0 <= slot - LAG < n_stage_1:
                multiply(slot - LAG, slot)
            ready = [i for i in unmultiplied if i not in unquantised and (slot >= n_stage_1 + X_SLOTS or not jobs[i]["meets_d"])]
            for i in ready[:2]:
                multiply(i, slot)
                unmultiplied.remove(i)

        mean_var = small.tile([P, RT, 2], F32, name="mean_var", tag="mean_var")
        for rt in range(RT):
            nc.vector.bn_aggr(out=mean_var[:, rt, :], in_=stats[:, rt].rearrange("p n v -> p (n v)"))
        var_eps, rstd = inverse_std(mean_var, nc.vector)

        def store(g, rt, blocks=1):
            cols_out = slice(g * BH, (g + blocks) * BH)
            nc.sync.dma_start(out=out[rt * P : (rt + 1) * P, cols_out], in_=result[:, rt, cols_out])

        def centre(g, rt):
            nc.vector.scalar_tensor_tensor(
                out=result[:, rt, g * BH : (g + 1) * BH],
                in0=block_sums[g][rt][:],
                scalar=mean_var[:, rt, 0:1],
                in1=gain_bias[:, 0, (g - SCALED) * BH : (g - SCALED + 1) * BH],
                op0=ALU.subtract,
                op1=ALU.mult,
            )

        def finish_centred(g, rt, blocks):
            piece = result[:, rt, g * BH : (g + blocks) * BH]
            nc.vector.scalar_tensor_tensor(
                out=piece,
                in0=piece,
                scalar=rstd[:, rt, :],
                in1=gain_bias[:, 1, (g - SCALED) * BH : (g - SCALED + blocks) * BH],
                op0=ALU.mult,
                op1=ALU.add,
            )
            nc.scalar.activation(out=piece, in_=piece, func=ACT.Silu)
            store(g, rt, blocks)

        totals = {}

        def turn_back(g, rt):
            total = psum.tile([P, PACK, P], F32, name="total", tag="bank")
            totals[(g, rt)] = total
            for t in range(PACK):
                nc.tensor.matmul(
                    out=total[:, t, :],
                    lhsT=scaled[:, g, t, rt * P : (rt + 1) * P],
                    rhs=ident[:],
                    is_transpose=True,
                    start=t == 0,
                    stop=False,
                )

        def finish_scaled(g, rt):
            total = totals[(g, rt)]
            nc.tensor.matmul(
                out=total[:],
                lhsT=row_terms[:, rt, :],
                rhs=term_rows[:, g * BH : (g + 1) * BH].rearrange("k (q t) -> k t q", t=PACK),
                start=False,
                stop=True,
            )
            nc.scalar.activation(
                out=result[:, rt, g * BH : (g + 1) * BH].rearrange("r (q t) -> r q t", t=PACK),
                in_=total[:].rearrange("r t q -> r q t"),
                func=ACT.Silu,
                scale=rstd[:, rt, :],
            )
            store(g, rt)

        centre(4, 0)
        std_mean = small.tile([P, RT, 2], F32, name="std_mean", tag="std_mean")
        nc.vector.tensor_scalar(
            out=std_mean[:, :, 1:2], in0=mean_var[:, :, 0:1], scalar1=-1.0, scalar2=None, op0=ALU.mult
        )
        centre(5, 0)
        turn_back(0, 0)
        finish_centred(4, 0, 1)
        nc.vector.tensor_tensor(out=std_mean[:, :, 0:1], in0=var_eps[:], in1=rstd[:], op=ALU.mult)
        nc.vector.tensor_copy(out=terms[:, :, 0:2], in_=std_mean[:])
        nc.vector.tensor_tensor(out=terms[:, :, 2:4], in0=std_mean[:], in1=terms[:, :, 0:2], op=ALU.subtract)
        terms_t = psum.tile([P, RT, P], BF16, name="terms_t", tag="bank")
        for rt in range(RT):
            nc.tensor.transpose(terms_t[:, rt, :], terms[:, rt, :], ident_bf[:])
        centre(6, 0)
        turn_back(0, 1)
        finish_centred(5, 0, 1)
        row_terms = keep.tile([P, RT, P], BF16, name="row_terms", tag="row_terms")
        nc.vector.tensor_copy(out=row_terms[:], in_=terms_t[:])
        finish_scaled(0, 0)
        centre(7, 0)
        turn_back(1, 0)
        finish_scaled(0, 1)
        finish_centred(6, 0, 2)
        for k, (g, rt) in enumerate(((4, 1), (6, 1))):
            centre(g, rt)
            turn_back(1 + k, 1)
            finish_scaled(1 + k, 0)
            centre(g + 1, rt)
            turn_back(2 + k, 0)
            finish_scaled(1 + k, 1)
            if k == 0:
                finish_centred(g, rt, 2)
            else:
                turn_back(3, 1)
                finish_centred(g, rt, 1)
                finish_scaled(3, 0)
                finish_centred(g + 1, rt, 1)
                finish_scaled(3, 1)
